import numpy as np
import ml_dtypes


def mxq(x, axis, fmt="e4m3"):
    dtype, down = {"e4m3": (ml_dtypes.float8_e4m3fn, 7), "e5m2": (ml_dtypes.float8_e5m2, 14)}[fmt]
    v = np.moveaxis(np.asarray(x, np.float32).astype(ml_dtypes.bfloat16).astype(np.float64), axis, -1)
    blocks = v.reshape(v.shape[:-1] + (-1, 32))
    amax = np.abs(blocks).max(-1, keepdims=True)
    byte = np.maximum(np.where(amax > 0, np.frexp(amax)[1] - 1 + 127, 0) - down, 1)
    scale = np.exp2(byte - 127.0)
    codes = (blocks / scale).astype(np.float32).astype(dtype).astype(np.float64)
    return np.moveaxis((codes * scale).reshape(v.shape), -1, axis)


WIDE = False


def mx_kscale(k):
    if not WIDE:
        return np.ones(k)
    levels = np.array([10, -10, 5, -5, 0])
    a = np.random.permutation(np.resize(levels, k // 512 * 4)).reshape(k // 512, 4)
    idx = np.arange(k)
    return np.exp2(a[idx // 512, idx % 128 // 32])


BF16 = ml_dtypes.bfloat16


def bf(x):
    return np.asarray(x, np.float32).astype(BF16)


def f64(x):
    return np.asarray(x).astype(np.float64)


B, S, E, NH = 4, 512, 1024, 8
DH = E // NH
EPS = 1e-08
NEG = -2.0**32 + 1.0


def setup_inputs():
    s = mx_kscale(E)
    keep = np.random.random((B, S)) >= 0.25
    return {
        "q_relu": bf(np.maximum(np.random.standard_normal((B, S, E)) * 2.2, 0.0)),
        "k_relu": bf(np.maximum(np.random.standard_normal((B, S, E)) * 2.2, 0.0)),
        "keys": bf(np.random.standard_normal((B, S, E)) * keep[:, :, None]),
        "values": bf(np.random.standard_normal((B, S, E)) * s),
        "Wv": bf(np.random.standard_normal((E, E)) * 2.0 / np.sqrt(E) / s[None, :]),
        "bv": bf(np.random.standard_normal(E) * 0.3),
        "queries": bf(np.random.standard_normal((B, S, E))),
        "gamma": bf(1.0 + 0.1 * np.random.standard_normal(E)),
        "betta": bf(0.1 * np.random.standard_normal(E)),
    }


def reference(q_relu, k_relu, keys, values, Wv, bv, queries, gamma, betta):
    q = f64(q_relu).reshape(B, S, NH, DH).transpose(0, 2, 1, 3)
    kt = f64(k_relu).reshape(B, S, NH, DH).transpose(0, 2, 3, 1)
    scores = (q @ kt) / (DH ** 0.5)
    key_mask = np.sign(np.abs(f64(keys).sum(-1)))
    cond = np.where(key_mask == 0.0, 1.0, 0.0)[:, None, None, :]
    scores = NEG * cond + scores * (1.0 - cond)
    e = np.exp(scores - scores.max(-1, keepdims=True))
    v = np.maximum((mxq(f64(values), 2, "e4m3") @ mxq(f64(Wv), 1, "e4m3").T) + f64(bv), 0.0)
    v = v.reshape(B, S, NH, DH).transpose(0, 2, 1, 3)
    att = (mxq(e, 3, "e4m3") @ mxq(v, 2, "e4m3")) / e.sum(-1, keepdims=True)
    out = att.transpose(0, 2, 1, 3).reshape(B, S, E) + f64(queries)
    mean = out.mean(-1, keepdims=True)
    var = np.sum((out - mean) ** 2, axis=-1, keepdims=True) / (E - 1)
    std = np.sqrt(var)
    return f64(gamma) * (out - mean) / (std + EPS) + f64(betta)

@@ -1,0 +1,325 @@
+from contextlib import ExitStack
+
+import concourse.mybir as mybir
+from concourse.masks import make_identity
+
+F32 = mybir.dt.float32
+BF16 = mybir.dt.bfloat16
+U32 = mybir.dt.uint32
+U8 = mybir.dt.uint8
+FP8X4 = mybir.dt.float8_e4m3fn_x4
+ALU = mybir.AluOpType
+ACT = mybir.ActivationFunctionType
+AXIS = mybir.AxisListType
+
+B, S, E, NH = 4, 512, 1024, 8
+DH = E // NH
+P = 128
+PACK = 4
+K_PASS = P * PACK
+S_BLOCKS = S // P
+E_BLOCKS = E // P
+PASSES = E // K_PASS
+PAIR = 2 * P
+HALF_HEADS = NH // 2
+SCALE = 1.0 / DH**0.5
+NEG = -(2.0**32) + 1.0
+EPS = 1e-08
+
+FLOPS = 2 * B * S * E * E + 2 * (2 * B * NH * S * S * DH)
+
+
+def flip_words(nc, identity, bank, row_blocks, first_word):
+    for u in range(2):
+        for a, words in enumerate(row_blocks):
+            nc.tensor.transpose(
+                bank[:, u, a * P : (a + 1) * P],
+                words[:, first_word + u * P : first_word + (u + 1) * P],
+                identity,
+            )
+
+
+def tile_multihead_attention_pa_kernel(
+    tc, q_relu, k_relu, keys, values, Wv, bv, queries, gamma, betta, out
+):
+    nc = tc.nc
+    with ExitStack() as ctx:
+        const = ctx.enter_context(tc.tile_pool(name="const", bufs=1))
+        raw = ctx.enter_context(tc.tile_pool(name="raw", bufs=1))
+        stage = ctx.enter_context(tc.tile_pool(name="stage", bufs=1))
+        batch = ctx.enter_context(tc.tile_pool(name="batch", bufs=2))
+        work = ctx.enter_context(tc.tile_pool(name="work", bufs=4))
+        halves = ctx.enter_context(tc.tile_pool(name="halves", bufs=2))
+        rows = ctx.enter_context(tc.tile_pool(name="rows", bufs=3))
+        small = ctx.enter_context(tc.tile_pool(name="small", bufs=4))
+        prep_ps = ctx.enter_context(tc.psum_pool(name="prep_ps", bufs=2))
+        score_ps = ctx.enter_context(tc.psum_pool(name="score_ps", bufs=3))
+        flip_ps = ctx.enter_context(tc.psum_pool(name="flip_ps", bufs=2))
+        att_ps = ctx.enter_context(tc.psum_pool(name="att_ps", bufs=1))
+
+        ident_bf = const.tile([P, P], BF16)
+        make_identity(nc, ident_bf[:])
+        ident_f32 = const.tile([P, P], F32)
+        make_identity(nc, ident_f32[:])
+
+        def load_batch(b):
+            keys_raw = raw.tile([P, S_BLOCKS, E], BF16)
+            nc.sync.dma_start(out=keys_raw[:], in_=keys[b].rearrange("(j p) e -> p j e", p=P))
+            q_raw = raw.tile([P, S_BLOCKS, E], BF16)
+            nc.sync.dma_start(out=q_raw[:], in_=q_relu[b].rearrange("(j p) e -> p j e", p=P))
+            k_raw = raw.tile([P, S_BLOCKS, E], BF16)
+            nc.sync.dma_start(out=k_raw[:], in_=k_relu[b].rearrange("(j p) e -> p j e", p=P))
+            x_raw = raw.tile([P, S_BLOCKS, E], BF16)
+            nc.sync.dma_start(out=x_raw[:], in_=values[b].rearrange("(j p) e -> p j e", p=P))
+            return keys_raw, k_raw, q_raw, x_raw
+
+        first_loads = load_batch(0)
+
+        w_codes = const.tile([P, PASSES, E], U32, align_bytes=64)
+        w_scales = const.tile([P, PASSES, E], U8, align_bytes=64)
+        for pair in range(E_BLOCKS // 2):
+            cols = slice(pair * PAIR, (pair + 1) * PAIR)
+            w_raw = raw.tile([P, 2, E], BF16, bufs=2)
+            nc.sync.dma_start(out=w_raw[:], in_=Wv[cols, :].rearrange("(a p) k -> p a k", p=P))
+            w_words = w_raw[:].bitcast(F32)
+            w_grouped = stage.tile([P, PASSES, PAIR, PACK], BF16, bufs=2, align_bytes=64)
+            for g in range(PASSES):
+                w_bank = prep_ps.tile([P, 2, PAIR], F32, tag="prep")
+                flip_words(nc, ident_f32[:], w_bank, [w_words[:, a, :] for a in range(2)], g * PAIR)
+                nc.scalar.copy(
+                    out=w_grouped[:, g, :, :].bitcast(F32),
+                    in_=w_bank[:].rearrange("p u c -> p c u"),
+                )
+            for g in range(PASSES):
+                nc.vector.quantize_mx(
+                    out=w_codes[:, g, cols].bitcast(FP8X4),
+                    scales=w_scales[:, g, cols],
+                    in_=w_grouped[:, g, :, :].rearrange("p c j -> p (c j)"),
+                )
+
+        bv_rows = const.tile([P, P], BF16)
+        nc.vector.memset(bv_rows[:], 0.0)
+        nc.sync.dma_start(out=bv_rows[0:E_BLOCKS, :], in_=bv.rearrange("(r c) -> r c", c=P))
+        bv_bank = prep_ps.tile([P, P], BF16, tag="prep")
+        nc.tensor.transpose(bv_bank[:], bv_rows[:], ident_bf[:])
+        bv_col = const.tile([P, E_BLOCKS], F32)
+        nc.vector.tensor_copy(out=bv_col[:], in_=bv_bank[:, 0:E_BLOCKS])
+        gamma_all = const.tile([P, E], BF16)
+        nc.sync.dma_start(out=gamma_all[:], in_=gamma.partition_broadcast(P))
+        betta_all = const.tile([P, E], BF16)
+        nc.sync.dma_start(out=betta_all[:], in_=betta.partition_broadcast(P))
+        one_half = const.tile([P, 1], F32)
+        nc.vector.memset(one_half[:], 0.5)
+        minus_one = const.tile([P, 1], F32)
+        nc.vector.memset(minus_one[:], -1.0)
+
+        def prepare_batch(loads):
+            keys_raw, k_raw, q_raw, x_raw = loads
+
+            fold_a = stage.tile([P, S_BLOCKS, E // 2], F32)
+            nc.gpsimd.tensor_tensor(
+                out=fold_a[:], in0=keys_raw[:, :, 0 : E // 2], in1=keys_raw[:, :, E // 2 : E], op=ALU.add
+            )
+            fold_b = stage.tile([P, S_BLOCKS, E // 4], F32)
+            nc.gpsimd.tensor_tensor(
+                out=fold_b[:], in0=fold_a[:, :, 0 : E // 4], in1=fold_a[:, :, E // 4 : E // 2], op=ALU.add
+            )
+            fold_c = stage.tile([P, S_BLOCKS, E // 8], F32)
+            nc.gpsimd.tensor_tensor(
+                out=fold_c[:], in0=fold_b[:, :, 0 : E // 8], in1=fold_b[:, :, E // 8 : E // 4], op=ALU.add
+            )
+            key_sum = small.tile([P, S_BLOCKS], F32)
+            nc.vector.tensor_reduce(out=key_sum[:], in_=fold_c[:], axis=AXIS.X, op=ALU.add)
+            keep = small.tile([P, S_BLOCKS], F32)
+            nc.vector.tensor_single_scalar(out=keep[:], in_=key_sum[:], scalar=0.0, op=ALU.not_equal)
+            neg_c = batch.tile([P, S_BLOCKS], F32)
+            nc.vector.tensor_scalar(
+                out=neg_c[:], in0=key_sum[:], scalar1=0.0, scalar2=NEG, op0=ALU.is_equal, op1=ALU.mult
+            )
+            keep_diag = batch.tile([P, S_BLOCKS, P], BF16)
+            for j in range(S_BLOCKS):
+                nc.vector.tensor_scalar(
+                    out=keep_diag[:, j, :], in0=ident_bf[:], scalar1=keep[:, j : j + 1], scalar2=None,
+                    op0=ALU.mult,
+                )
+
+            kT = batch.tile([P, NH, S], BF16)
+            qT = batch.tile([P, NH, S], BF16)
+            for first_head in range(0, NH, 2):
+                k_bank = prep_ps.tile([P, 2, S], BF16, tag="prep")
+                q_bank = prep_ps.tile([P, 2, S], BF16, tag="prep")
+                for a in range(2):
+                    feats = slice((first_head + a) * DH, (first_head + a + 1) * DH)
+                    for j in range(S_BLOCKS):
+                        nc.tensor.transpose(
+                            k_bank[:, a, j * P : (j + 1) * P], k_raw[:, j, feats], keep_diag[:, j, :]
+                        )
+                    for j in range(S_BLOCKS):
+                        nc.tensor.transpose(q_bank[:, a, j * P : (j + 1) * P], q_raw[:, j, feats], ident_bf[:])
+                nc.vector.tensor_copy(out=kT[:, first_head : first_head + 2, :], in_=k_bank[:])
+                nc.scalar.copy(out=qT[:, first_head : first_head + 2, :], in_=q_bank[:])
+
+            x_words = x_raw[:].bitcast(F32)
+            x_grouped = stage.tile([P, PASSES, S, PACK], BF16, align_bytes=64)
+            x_codes = stage.tile([P, PASSES, S], U32, align_bytes=64)
+            x_scales = stage.tile([P, PASSES, S], U8, align_bytes=64)
+            for g in range(PASSES):
+                for pair in range(S_BLOCKS // 2):
+                    x_bank = prep_ps.tile([P, 2, PAIR], F32, tag="prep")
+                    flip_words(
+                        nc, ident_f32[:], x_bank, [x_words[:, 2 * pair + a, :] for a in range(2)], g * PAIR
+                    )
+                    nc.scalar.copy(
+                        out=x_grouped[:, g, pair * PAIR : (pair + 1) * PAIR, :].bitcast(F32),
+                        in_=x_bank[:].rearrange("p u c -> p c u"),
+                    )
+            for g in range(PASSES):
+                nc.vector.quantize_mx(
+                    out=x_codes[:, g, :].bitcast(FP8X4),
+                    scales=x_scales[:, g, :],
+                    in_=x_grouped[:, g, :, :].rearrange("p c j -> p (c j)"),
+                )
+
+            vT = stage.tile([P, E_BLOCKS, S], BF16)
+            for m in range(E_BLOCKS):
+                v_bank = prep_ps.tile([P, S], F32, tag="prep")
+                for g in range(PASSES):
+                    nc.tensor.matmul_mx(
+                        out=v_bank[:],
+                        lhsT=w_codes[:, g, m * P : (m + 1) * P].bitcast(FP8X4),
+                        lhsT_scale=w_scales[:, g, m * P : (m + 1) * P],
+                        rhs=x_codes[:, g, :].bitcast(FP8X4),
+                        rhs_scale=x_scales[:, g, :],
+                        start=(g == 0),
+                        stop=(g == PASSES - 1),
+                    )
+                nc.scalar.activation(
+                    out=vT[:, m, :], in_=v_bank[:], func=ACT.Relu, bias=bv_col[:, m : m + 1], scale=1.0
+                )
+
+            vT_words = vT[:].bitcast(F32)
+            v_grouped = stage.tile([P, E, PACK], BF16, align_bytes=64)
+            for pair in range(E_BLOCKS // 2):
+                vk_bank = prep_ps.tile([P, 2, PAIR], F32, tag="prep")
+                flip_words(nc, ident_f32[:], vk_bank, [vT_words[:, 2 * pair + a, :] for a in range(2)], 0)
+                nc.scalar.copy(
+                    out=v_grouped[:, pair * PAIR : (pair + 1) * PAIR, :].bitcast(F32),
+                    in_=vk_bank[:].rearrange("p u c -> p c u"),
+                )
+            v_codes = batch.tile([P, E], U32, align_bytes=64)
+            v_scales = batch.tile([P, E], U8, align_bytes=64)
+            nc.vector.quantize_mx(
+                out=v_codes[:].bitcast(FP8X4),
+                scales=v_scales[:],
+                in_=v_grouped[:].rearrange("p c j -> p (c j)"),
+            )
+            return qT, kT, neg_c, v_codes, v_scales
+
+        def attend(b, i, operands):
+            qT, kT, neg_c, v_codes, v_scales = operands
+            q_rows = slice(i * P, (i + 1) * P)
+            resid = rows.tile([P, E], BF16)
+            nc.sync.dma_start(out=resid[:], in_=queries[b, q_rows, :])
+            y = rows.tile([P, E], F32)
+            neg_max = small.tile([P, NH], F32)
+            shift = small.tile([P, NH], F32)
+            row_sum = small.tile([P, NH], F32)
+            for first_head in range(0, NH, HALF_HEADS):
+                e_grouped = halves.tile([P, HALF_HEADS * P, PACK], BF16, align_bytes=64)
+                for pair in range(HALF_HEADS // 2):
+                    e_words = []
+                    for a in range(2):
+                        h = first_head + 2 * pair + a
+                        score = score_ps.tile([P, S], F32)
+                        nc.tensor.matmul(
+                            out=score[:], lhsT=qT[:, h, q_rows], rhs=kT[:, h, :], start=True, stop=False
+                        )
+                        for j in range(S_BLOCKS):
+                            nc.tensor.matmul(
+                                out=score[:, j * P : (j + 1) * P],
+                                lhsT=neg_c[:, j : j + 1].to_broadcast([P, P]),
+                                rhs=ident_f32[:],
+                                is_transpose=True,
+                                start=False,
+                                stop=(j == S_BLOCKS - 1),
+                            )
+                        nc.vector.tensor_reduce(
+                            out=neg_max[:, h : h + 1], in_=score[:], axis=AXIS.X, op=ALU.max, negate=True
+                        )
+                        nc.vector.tensor_scalar(
+                            out=shift[:, h : h + 1], in0=neg_max[:, h : h + 1], scalar1=SCALE, scalar2=None,
+                            op0=ALU.mult,
+                        )
+                        e = work.tile([P, S], BF16)
+                        nc.scalar.activation(
+                            out=e[:], in_=score[:], func=ACT.Exp, bias=shift[:, h : h + 1], scale=SCALE,
+                            accum_out=row_sum[:, h : h + 1],
+                        )
+                        e_words.append(e[:].bitcast(F32))
+                    e_bank = flip_ps.tile([P, 2, PAIR], F32)
+                    flip_words(nc, ident_f32[:], e_bank, e_words, 0)
+                    nc.scalar.copy(
+                        out=e_grouped[:, pair * PAIR : (pair + 1) * PAIR, :].bitcast(F32),
+                        in_=e_bank[:].rearrange("p u c -> p c u"),
+                    )
+                e_codes = halves.tile([P, HALF_HEADS * P], U32, align_bytes=64)
+                e_scales = halves.tile([P, HALF_HEADS * P], U8, align_bytes=64)
+                nc.vector.quantize_mx(
+                    out=e_codes[:].bitcast(FP8X4),
+                    scales=e_scales[:],
+                    in_=e_grouped[:].rearrange("p c j -> p (c j)"),
+                )
+                att = att_ps.tile([P, HALF_HEADS, DH], F32)
+                for a in range(HALF_HEADS):
+                    h = first_head + a
+                    nc.tensor.matmul_mx(
+                        out=att[:, a, :],
+                        lhsT=e_codes[:, a * P : (a + 1) * P].bitcast(FP8X4),
+                        lhsT_scale=e_scales[:, a * P : (a + 1) * P],
+                        rhs=v_codes[:, h * DH : (h + 1) * DH].bitcast(FP8X4),
+                        rhs_scale=v_scales[:, h * DH : (h + 1) * DH],
+                        start=True,
+                        stop=True,
+                    )
+                inv_sum = small.tile([P, HALF_HEADS], F32)
+                nc.vector.reciprocal(out=inv_sum[:], in_=row_sum[:, first_head : first_head + HALF_HEADS])
+                for a in range(HALF_HEADS):
+                    feats = slice((first_head + a) * DH, (first_head + a + 1) * DH)
+                    nc.vector.scalar_tensor_tensor(
+                        out=y[:, feats], in0=att[:, a, :], scalar=inv_sum[:, a : a + 1], in1=resid[:, feats],
+                        op0=ALU.mult, op1=ALU.add,
+                    )
+
+            stats = small.tile([P, 2, 6], F32)
+            for c in range(2):
+                nc.vector.bn_stats(out=stats[:, c, :], in_=y[:, c * (E // 2) : (c + 1) * (E // 2)])
+            mean_var = small.tile([P, 2], F32)
+            nc.vector.bn_aggr(out=mean_var[:], in_=stats[:].rearrange("p c s -> p (c s)"))
+            nc.vector.scalar_tensor_tensor(
+                out=y[:], in0=y[:], scalar=mean_var[:, 0:1], in1=gamma_all[:], op0=ALU.subtract, op1=ALU.mult
+            )
+            var = small.tile([P, 1], F32)
+            nc.gpsimd.tensor_scalar(
+                out=var[:], in0=mean_var[:, 1:2], scalar1=E / (E - 1.0), scalar2=0.0, op0=ALU.mult, op1=ALU.add
+            )
+            sd = small.tile([P, 1], F32)
+            nc.gpsimd.tensor_tensor(out=sd[:], in0=var[:], in1=one_half[:], op=ALU.pow)
+            sd_eps = small.tile([P, 1], F32)
+            nc.gpsimd.tensor_scalar(
+                out=sd_eps[:], in0=sd[:], scalar1=EPS, scalar2=1.0, op0=ALU.add, op1=ALU.mult
+            )
+            inv_sd = small.tile([P, 1], F32)
+            nc.gpsimd.tensor_tensor(out=inv_sd[:], in0=sd_eps[:], in1=minus_one[:], op=ALU.pow)
+            nc.gpsimd.tensor_scalar(
+                out=y[:], in0=y[:], scalar1=inv_sd[:, 0:1], scalar2=0.0, op0=ALU.mult, op1=ALU.add
+            )
+            nc.gpsimd.tensor_tensor(out=y[:], in0=y[:], in1=betta_all[:], op=ALU.add)
+            nc.gpsimd.dma_start(out=out[b, q_rows, :], in_=y[:])
+
+        loads = first_loads
+        for b in range(B):
+            operands = prepare_batch(loads)
+            if b + 1 < B:
+                loads = load_batch(b + 1)
+            for i in range(S_BLOCKS):
+                attend(b, i, operands)

@@ -53,9 +53,9 @@ def tile_multihead_attention_pa_kernel(
         rows = ctx.enter_context(tc.tile_pool(name="rows", bufs=3))
         small = ctx.enter_context(tc.tile_pool(name="small", bufs=4))
         prep_ps = ctx.enter_context(tc.psum_pool(name="prep_ps", bufs=2))
-        score_ps = ctx.enter_context(tc.psum_pool(name="score_ps", bufs=3))
+        score_ps = ctx.enter_context(tc.psum_pool(name="score_ps", bufs=2))
         flip_ps = ctx.enter_context(tc.psum_pool(name="flip_ps", bufs=2))
-        att_ps = ctx.enter_context(tc.psum_pool(name="att_ps", bufs=1))
+        att_ps = ctx.enter_context(tc.psum_pool(name="att_ps", bufs=2))
 
         ident_bf = const.tile([P, P], BF16)
         make_identity(nc, ident_bf[:])
@@ -132,7 +132,7 @@ def tile_multihead_attention_pa_kernel(
             nc.vector.tensor_reduce(out=key_sum[:], in_=fold_c[:], axis=AXIS.X, op=ALU.add)
             keep = small.tile([P, S_BLOCKS], F32)
             nc.vector.tensor_single_scalar(out=keep[:], in_=key_sum[:], scalar=0.0, op=ALU.not_equal)
-            neg_c = batch.tile([P, S_BLOCKS], F32)
+            neg_c = small.tile([P, S_BLOCKS], BF16)
             nc.vector.tensor_scalar(
                 out=neg_c[:], in0=key_sum[:], scalar1=0.0, scalar2=NEG, op0=ALU.is_equal, op1=ALU.mult
             )
@@ -142,6 +142,18 @@ def tile_multihead_attention_pa_kernel(
                     out=keep_diag[:, j, :], in0=ident_bf[:], scalar1=keep[:, j : j + 1], scalar2=None,
                     op0=ALU.mult,
                 )
+
+            mask_bank = prep_ps.tile([P, S], F32, tag="prep")
+            for j in range(S_BLOCKS):
+                nc.tensor.matmul(
+                    out=mask_bank[:, j * P : (j + 1) * P],
+                    lhsT=neg_c[:, j : j + 1].to_broadcast([P, P]),
+                    rhs=ident_bf[:],
+                    start=True,
+                    stop=True,
+                )
+            neg_mask = batch.tile([P, S], BF16)
+            nc.vector.tensor_copy(out=neg_mask[:], in_=mask_bank[:])
 
             kT = batch.tile([P, NH, S], BF16)
             qT = batch.tile([P, NH, S], BF16)
@@ -156,7 +168,7 @@ def tile_multihead_attention_pa_kernel(
                         )
                     for j in range(S_BLOCKS):
                         nc.tensor.transpose(q_bank[:, a, j * P : (j + 1) * P], q_raw[:, j, feats], ident_bf[:])
-                nc.vector.tensor_copy(out=kT[:, first_head : first_head + 2, :], in_=k_bank[:])
+                nc.scalar.copy(out=kT[:, first_head : first_head + 2, :], in_=k_bank[:])
                 nc.scalar.copy(out=qT[:, first_head : first_head + 2, :], in_=q_bank[:])
 
             x_words = x_raw[:].bitcast(F32)
@@ -213,17 +225,17 @@ def tile_multihead_attention_pa_kernel(
                 scales=v_scales[:],
                 in_=v_grouped[:].rearrange("p c j -> p (c j)"),
             )
-            return qT, kT, neg_c, v_codes, v_scales
+            return qT, kT, neg_mask, v_codes, v_scales
 
         def attend(b, i, operands):
-            qT, kT, neg_c, v_codes, v_scales = operands
+            qT, kT, neg_mask, v_codes, v_scales = operands
             q_rows = slice(i * P, (i + 1) * P)
             resid = rows.tile([P, E], BF16)
             nc.sync.dma_start(out=resid[:], in_=queries[b, q_rows, :])
             y = rows.tile([P, E], F32)
             neg_max = small.tile([P, NH], F32)
-            shift = small.tile([P, NH], F32)
             row_sum = small.tile([P, NH], F32)
+            y_sums = small.tile([P, NH], F32)
             for first_head in range(0, NH, HALF_HEADS):
                 e_grouped = halves.tile([P, HALF_HEADS * P, PACK], BF16, align_bytes=64)
                 for pair in range(HALF_HEADS // 2):
@@ -232,27 +244,19 @@ def tile_multihead_attention_pa_kernel(
                         h = first_head + 2 * pair + a
                         score = score_ps.tile([P, S], F32)
                         nc.tensor.matmul(
-                            out=score[:], lhsT=qT[:, h, q_rows], rhs=kT[:, h, :], start=True, stop=False
+                            out=score[:], lhsT=qT[:, h, q_rows], rhs=kT[:, h, :], start=True, stop=True
                         )
-                        for j in range(S_BLOCKS):
-                            nc.tensor.matmul(
-                                out=score[:, j * P : (j + 1) * P],
-                                lhsT=neg_c[:, j : j + 1].to_broadcast([P, P]),
-                                rhs=ident_f32[:],
-                                is_transpose=True,
-                                start=False,
-                                stop=(j == S_BLOCKS - 1),
-                            )
+                        masked = work.tile([P, S], F32)
+                        nc.vector.scalar_tensor_tensor(
+                            out=masked[:], in0=score[:], scalar=SCALE, in1=neg_mask[:],
+                            op0=ALU.mult, op1=ALU.add,
+                        )
                         nc.vector.tensor_reduce(
-                            out=neg_max[:, h : h + 1], in_=score[:], axis=AXIS.X, op=ALU.max, negate=True
-                        )
-                        nc.vector.tensor_scalar(
-                            out=shift[:, h : h + 1], in0=neg_max[:, h : h + 1], scalar1=SCALE, scalar2=None,
-                            op0=ALU.mult,
+                            out=neg_max[:, h : h + 1], in_=masked[:], axis=AXIS.X, op=ALU.max, negate=True
                         )
                         e = work.tile([P, S], BF16)
                         nc.scalar.activation(
-                            out=e[:], in_=score[:], func=ACT.Exp, bias=shift[:, h : h + 1], scale=SCALE,
+                            out=e[:], in_=masked[:], func=ACT.Exp, bias=neg_max[:, h : h + 1], scale=1.0,
                             accum_out=row_sum[:, h : h + 1],
                         )
                         e_words.append(e[:].bitcast(F32))
@@ -284,23 +288,27 @@ def tile_multihead_attention_pa_kernel(
                 inv_sum = small.tile([P, HALF_HEADS], F32)
                 nc.vector.reciprocal(out=inv_sum[:], in_=row_sum[:, first_head : first_head + HALF_HEADS])
                 for a in range(HALF_HEADS):
-                    feats = slice((first_head + a) * DH, (first_head + a + 1) * DH)
+                    h = first_head + a
+                    feats = slice(h * DH, (h + 1) * DH)
                     nc.vector.scalar_tensor_tensor(
                         out=y[:, feats], in0=att[:, a, :], scalar=inv_sum[:, a : a + 1], in1=resid[:, feats],
-                        op0=ALU.mult, op1=ALU.add,
+                        op0=ALU.mult, op1=ALU.add, accum_out=y_sums[:, h : h + 1],
                     )
 
-            stats = small.tile([P, 2, 6], F32)
-            for c in range(2):
-                nc.vector.bn_stats(out=stats[:, c, :], in_=y[:, c * (E // 2) : (c + 1) * (E // 2)])
-            mean_var = small.tile([P, 2], F32)
-            nc.vector.bn_aggr(out=mean_var[:], in_=stats[:].rearrange("p c s -> p (c s)"))
-            nc.vector.scalar_tensor_tensor(
-                out=y[:], in0=y[:], scalar=mean_var[:, 0:1], in1=gamma_all[:], op0=ALU.subtract, op1=ALU.mult
+            neg_total = small.tile([P, 1], F32)
+            nc.vector.tensor_reduce(out=neg_total[:], in_=y_sums[:], axis=AXIS.X, op=ALU.add, negate=True)
+            neg_mean = small.tile([P, 1], F32)
+            nc.vector.tensor_scalar(
+                out=neg_mean[:], in0=neg_total[:], scalar1=1.0 / E, scalar2=None, op0=ALU.mult
+            )
+            squares = rows.tile([P, E], BF16)
+            sum_sq = small.tile([P, 1], F32)
+            nc.scalar.activation(
+                out=squares[:], in_=y[:], func=ACT.Square, bias=neg_mean[:, 0:1], scale=1.0, accum_out=sum_sq[:]
             )
             var = small.tile([P, 1], F32)
             nc.gpsimd.tensor_scalar(
-                out=var[:], in0=mean_var[:, 1:2], scalar1=E / (E - 1.0), scalar2=0.0, op0=ALU.mult, op1=ALU.add
+                out=var[:], in0=sum_sq[:], scalar1=1.0 / (E - 1.0), scalar2=0.0, op0=ALU.mult, op1=ALU.add
             )
             sd = small.tile([P, 1], F32)
             nc.gpsimd.tensor_tensor(out=sd[:], in0=var[:], in1=one_half[:], op=ALU.pow)
@@ -311,8 +319,9 @@ def tile_multihead_attention_pa_kernel(
             inv_sd = small.tile([P, 1], F32)
             nc.gpsimd.tensor_tensor(out=inv_sd[:], in0=sd_eps[:], in1=minus_one[:], op=ALU.pow)
             nc.gpsimd.tensor_scalar(
-                out=y[:], in0=y[:], scalar1=inv_sd[:, 0:1], scalar2=0.0, op0=ALU.mult, op1=ALU.add
+                out=y[:], in0=y[:], scalar1=neg_mean[:, 0:1], scalar2=inv_sd[:, 0:1], op0=ALU.add, op1=ALU.mult
             )
+            nc.gpsimd.tensor_tensor(out=y[:], in0=y[:], in1=gamma_all[:], op=ALU.mult)
             nc.gpsimd.tensor_tensor(out=y[:], in0=y[:], in1=betta_all[:], op=ALU.add)
             nc.gpsimd.dma_start(out=out[b, q_rows, :], in_=y[:])
 

@@ -48,14 +48,14 @@ def tile_multihead_attention_pa_kernel(
         raw = ctx.enter_context(tc.tile_pool(name="raw", bufs=1))
         stage = ctx.enter_context(tc.tile_pool(name="stage", bufs=1))
         batch = ctx.enter_context(tc.tile_pool(name="batch", bufs=2))
-        work = ctx.enter_context(tc.tile_pool(name="work", bufs=4))
+        work = ctx.enter_context(tc.tile_pool(name="work", bufs=3))
         halves = ctx.enter_context(tc.tile_pool(name="halves", bufs=2))
         rows = ctx.enter_context(tc.tile_pool(name="rows", bufs=3))
         small = ctx.enter_context(tc.tile_pool(name="small", bufs=4))
         prep_ps = ctx.enter_context(tc.psum_pool(name="prep_ps", bufs=2))
-        score_ps = ctx.enter_context(tc.psum_pool(name="score_ps", bufs=2))
+        score_ps = ctx.enter_context(tc.psum_pool(name="score_ps", bufs=3))
         flip_ps = ctx.enter_context(tc.psum_pool(name="flip_ps", bufs=2))
-        att_ps = ctx.enter_context(tc.psum_pool(name="att_ps", bufs=2))
+        att_ps = ctx.enter_context(tc.psum_pool(name="att_ps", bufs=1))
 
         ident_bf = const.tile([P, P], BF16)
         make_identity(nc, ident_bf[:])
@@ -75,160 +75,139 @@ def tile_multihead_attention_pa_kernel(
 
         first_loads = load_batch(0)
 
-        w_codes = const.tile([P, PASSES, E], U32, align_bytes=64)
-        w_scales = const.tile([P, PASSES, E], U8, align_bytes=64)
-        for pair in range(E_BLOCKS // 2):
-            cols = slice(pair * PAIR, (pair + 1) * PAIR)
-            w_raw = raw.tile([P, 2, E], BF16, bufs=2)
-            nc.sync.dma_start(out=w_raw[:], in_=Wv[cols, :].rearrange("(a p) k -> p a k", p=P))
-            w_words = w_raw[:].bitcast(F32)
-            w_grouped = stage.tile([P, PASSES, PAIR, PACK], BF16, bufs=2, align_bytes=64)
-            for g in range(PASSES):
-                w_bank = prep_ps.tile([P, 2, PAIR], F32, tag="prep")
-                flip_words(nc, ident_f32[:], w_bank, [w_words[:, a, :] for a in range(2)], g * PAIR)
-                nc.scalar.copy(
-                    out=w_grouped[:, g, :, :].bitcast(F32),
-                    in_=w_bank[:].rearrange("p u c -> p c u"),
-                )
-            for g in range(PASSES):
-                nc.vector.quantize_mx(
-                    out=w_codes[:, g, cols].bitcast(FP8X4),
-                    scales=w_scales[:, g, cols],
-                    in_=w_grouped[:, g, :, :].rearrange("p c j -> p (c j)"),
-                )
-
-        bv_rows = const.tile([P, P], BF16)
-        nc.vector.memset(bv_rows[:], 0.0)
-        nc.sync.dma_start(out=bv_rows[0:E_BLOCKS, :], in_=bv.rearrange("(r c) -> r c", c=P))
-        bv_bank = prep_ps.tile([P, P], BF16, tag="prep")
-        nc.tensor.transpose(bv_bank[:], bv_rows[:], ident_bf[:])
-        bv_col = const.tile([P, E_BLOCKS], F32)
-        nc.vector.tensor_copy(out=bv_col[:], in_=bv_bank[:, 0:E_BLOCKS])
-        gamma_all = const.tile([P, E], BF16)
-        nc.sync.dma_start(out=gamma_all[:], in_=gamma.partition_broadcast(P))
-        betta_all = const.tile([P, E], BF16)
-        nc.sync.dma_start(out=betta_all[:], in_=betta.partition_broadcast(P))
-        one_half = const.tile([P, 1], F32)
-        nc.vector.memset(one_half[:], 0.5)
-        minus_one = const.tile([P, 1], F32)
-        nc.vector.memset(minus_one[:], -1.0)
-
-        def prepare_batch(loads):
+        def preparation(loads):
             keys_raw, k_raw, q_raw, x_raw = loads
+            made = {}
 
-            fold_a = stage.tile([P, S_BLOCKS, E // 2], F32)
-            nc.gpsimd.tensor_tensor(
-                out=fold_a[:], in0=keys_raw[:, :, 0 : E // 2], in1=keys_raw[:, :, E // 2 : E], op=ALU.add
-            )
-            fold_b = stage.tile([P, S_BLOCKS, E // 4], F32)
-            nc.gpsimd.tensor_tensor(
-                out=fold_b[:], in0=fold_a[:, :, 0 : E // 4], in1=fold_a[:, :, E // 4 : E // 2], op=ALU.add
-            )
-            fold_c = stage.tile([P, S_BLOCKS, E // 8], F32)
-            nc.gpsimd.tensor_tensor(
-                out=fold_c[:], in0=fold_b[:, :, 0 : E // 8], in1=fold_b[:, :, E // 8 : E // 4], op=ALU.add
-            )
-            key_sum = small.tile([P, S_BLOCKS], F32)
-            nc.vector.tensor_reduce(out=key_sum[:], in_=fold_c[:], axis=AXIS.X, op=ALU.add)
-            keep = small.tile([P, S_BLOCKS], F32)
-            nc.vector.tensor_single_scalar(out=keep[:], in_=key_sum[:], scalar=0.0, op=ALU.not_equal)
-            neg_c = small.tile([P, S_BLOCKS], BF16)
-            nc.vector.tensor_scalar(
-                out=neg_c[:], in0=key_sum[:], scalar1=0.0, scalar2=NEG, op0=ALU.is_equal, op1=ALU.mult
-            )
-            keep_diag = batch.tile([P, S_BLOCKS, P], BF16)
-            for j in range(S_BLOCKS):
+            def mask_and_heads():
+                qT = batch.tile([P, NH, S], BF16)
+                for first_head in range(0, NH, 2):
+                    q_bank = prep_ps.tile([P, 2, S], BF16, tag="prep")
+                    for a in range(2):
+                        feats = slice((first_head + a) * DH, (first_head + a + 1) * DH)
+                        for j in range(S_BLOCKS):
+                            nc.tensor.transpose(q_bank[:, a, j * P : (j + 1) * P], q_raw[:, j, feats], ident_bf[:])
+                    nc.scalar.copy(out=qT[:, first_head : first_head + 2, :], in_=q_bank[:])
+
+                fold_a = stage.tile([P, S_BLOCKS, E // 2], F32)
+                nc.gpsimd.tensor_tensor(
+                    out=fold_a[:], in0=keys_raw[:, :, 0 : E // 2], in1=keys_raw[:, :, E // 2 : E], op=ALU.add
+                )
+                fold_b = stage.tile([P, S_BLOCKS, E // 4], F32)
+                nc.gpsimd.tensor_tensor(
+                    out=fold_b[:], in0=fold_a[:, :, 0 : E // 4], in1=fold_a[:, :, E // 4 : E // 2], op=ALU.add
+                )
+                fold_c = stage.tile([P, S_BLOCKS, E // 8], F32)
+                nc.gpsimd.tensor_tensor(
+                    out=fold_c[:], in0=fold_b[:, :, 0 : E // 8], in1=fold_b[:, :, E // 8 : E // 4], op=ALU.add
+                )
+                key_sum = small.tile([P, S_BLOCKS], F32)
+                nc.vector.tensor_reduce(out=key_sum[:], in_=fold_c[:], axis=AXIS.X, op=ALU.add)
+                keep = small.tile([P, S_BLOCKS], F32)
+                nc.vector.tensor_single_scalar(out=keep[:], in_=key_sum[:], scalar=0.0, op=ALU.not_equal)
+                neg_c = small.tile([P, S_BLOCKS], BF16)
                 nc.vector.tensor_scalar(
-                    out=keep_diag[:, j, :], in0=ident_bf[:], scalar1=keep[:, j : j + 1], scalar2=None,
-                    op0=ALU.mult,
+                    out=neg_c[:], in0=key_sum[:], scalar1=0.0, scalar2=NEG, op0=ALU.is_equal, op1=ALU.mult
                 )
-
-            mask_bank = prep_ps.tile([P, S], F32, tag="prep")
-            for j in range(S_BLOCKS):
-                nc.tensor.matmul(
-                    out=mask_bank[:, j * P : (j + 1) * P],
-                    lhsT=neg_c[:, j : j + 1].to_broadcast([P, P]),
-                    rhs=ident_bf[:],
-                    start=True,
-                    stop=True,
-                )
-            neg_mask = batch.tile([P, S], BF16)
-            nc.vector.tensor_copy(out=neg_mask[:], in_=mask_bank[:])
-
-            kT = batch.tile([P, NH, S], BF16)
-            qT = batch.tile([P, NH, S], BF16)
-            for first_head in range(0, NH, 2):
-                k_bank = prep_ps.tile([P, 2, S], BF16, tag="prep")
-                q_bank = prep_ps.tile([P, 2, S], BF16, tag="prep")
-                for a in range(2):
-                    feats = slice((first_head + a) * DH, (first_head + a + 1) * DH)
-                    for j in range(S_BLOCKS):
-                        nc.tensor.transpose(
-                            k_bank[:, a, j * P : (j + 1) * P], k_raw[:, j, feats], keep_diag[:, j, :]
-                        )
-                    for j in range(S_BLOCKS):
-                        nc.tensor.transpose(q_bank[:, a, j * P : (j + 1) * P], q_raw[:, j, feats], ident_bf[:])
-                nc.scalar.copy(out=kT[:, first_head : first_head + 2, :], in_=k_bank[:])
-                nc.scalar.copy(out=qT[:, first_head : first_head + 2, :], in_=q_bank[:])
-
-            x_words = x_raw[:].bitcast(F32)
-            x_grouped = stage.tile([P, PASSES, S, PACK], BF16, align_bytes=64)
-            x_codes = stage.tile([P, PASSES, S], U32, align_bytes=64)
-            x_scales = stage.tile([P, PASSES, S], U8, align_bytes=64)
-            for g in range(PASSES):
-                for pair in range(S_BLOCKS // 2):
-                    x_bank = prep_ps.tile([P, 2, PAIR], F32, tag="prep")
-                    flip_words(
-                        nc, ident_f32[:], x_bank, [x_words[:, 2 * pair + a, :] for a in range(2)], g * PAIR
+                keep_diag = batch.tile([P, S_BLOCKS, P], BF16)
+                for j in range(S_BLOCKS):
+                    nc.vector.tensor_scalar(
+                        out=keep_diag[:, j, :], in0=ident_bf[:], scalar1=keep[:, j : j + 1], scalar2=None,
+                        op0=ALU.mult,
                     )
-                    nc.scalar.copy(
-                        out=x_grouped[:, g, pair * PAIR : (pair + 1) * PAIR, :].bitcast(F32),
-                        in_=x_bank[:].rearrange("p u c -> p c u"),
-                    )
-            for g in range(PASSES):
-                nc.vector.quantize_mx(
-                    out=x_codes[:, g, :].bitcast(FP8X4),
-                    scales=x_scales[:, g, :],
-                    in_=x_grouped[:, g, :, :].rearrange("p c j -> p (c j)"),
-                )
 
-            vT = stage.tile([P, E_BLOCKS, S], BF16)
-            for m in range(E_BLOCKS):
-                v_bank = prep_ps.tile([P, S], F32, tag="prep")
+                mask_bank = prep_ps.tile([P, S], F32, tag="prep")
+                for j in range(S_BLOCKS):
+                    nc.tensor.matmul(
+                        out=mask_bank[:, j * P : (j + 1) * P],
+                        lhsT=neg_c[:, j : j + 1].to_broadcast([P, P]),
+                        rhs=ident_bf[:],
+                        start=True,
+                        stop=True,
+                    )
+                neg_mask = batch.tile([P, S], BF16)
+                nc.vector.tensor_copy(out=neg_mask[:], in_=mask_bank[:])
+
+                kT = batch.tile([P, NH, S], BF16)
+                for first_head in range(0, NH, 2):
+                    k_bank = prep_ps.tile([P, 2, S], BF16, tag="prep")
+                    for a in range(2):
+                        feats = slice((first_head + a) * DH, (first_head + a + 1) * DH)
+                        for j in range(S_BLOCKS):
+                            nc.tensor.transpose(
+                                k_bank[:, a, j * P : (j + 1) * P], k_raw[:, j, feats], keep_diag[:, j, :]
+                            )
+                    nc.scalar.copy(out=kT[:, first_head : first_head + 2, :], in_=k_bank[:])
+                made["qT"], made["kT"], made["neg_mask"] = qT, kT, neg_mask
+
+            def quantise_values():
+                x_words = x_raw[:].bitcast(F32)
+                x_grouped = stage.tile([P, PASSES, S, PACK], BF16, align_bytes=64)
+                x_codes = stage.tile([P, PASSES, S], U32, align_bytes=64)
+                x_scales = stage.tile([P, PASSES, S], U8, align_bytes=64)
                 for g in range(PASSES):
-                    nc.tensor.matmul_mx(
-                        out=v_bank[:],
-                        lhsT=w_codes[:, g, m * P : (m + 1) * P].bitcast(FP8X4),
-                        lhsT_scale=w_scales[:, g, m * P : (m + 1) * P],
-                        rhs=x_codes[:, g, :].bitcast(FP8X4),
-                        rhs_scale=x_scales[:, g, :],
-                        start=(g == 0),
-                        stop=(g == PASSES - 1),
+                    for pair in range(S_BLOCKS // 2):
+                        x_bank = prep_ps.tile([P, 2, PAIR], F32, tag="prep")
+                        flip_words(
+                            nc, ident_f32[:], x_bank, [x_words[:, 2 * pair + a, :] for a in range(2)], g * PAIR
+                        )
+                        nc.scalar.copy(
+                            out=x_grouped[:, g, pair * PAIR : (pair + 1) * PAIR, :].bitcast(F32),
+                            in_=x_bank[:].rearrange("p u c -> p c u"),
+                        )
+                for g in range(PASSES):
+                    nc.vector.quantize_mx(
+                        out=x_codes[:, g, :].bitcast(FP8X4),
+                        scales=x_scales[:, g, :],
+                        in_=x_grouped[:, g, :, :].rearrange("p c j -> p (c j)"),
                     )
-                nc.scalar.activation(
-                    out=vT[:, m, :], in_=v_bank[:], func=ACT.Relu, bias=bv_col[:, m : m + 1], scale=1.0
-                )
+                made["x_codes"], made["x_scales"] = x_codes, x_scales
 
-            vT_words = vT[:].bitcast(F32)
-            v_grouped = stage.tile([P, E, PACK], BF16, align_bytes=64)
-            for pair in range(E_BLOCKS // 2):
-                vk_bank = prep_ps.tile([P, 2, PAIR], F32, tag="prep")
-                flip_words(nc, ident_f32[:], vk_bank, [vT_words[:, 2 * pair + a, :] for a in range(2)], 0)
-                nc.scalar.copy(
-                    out=v_grouped[:, pair * PAIR : (pair + 1) * PAIR, :].bitcast(F32),
-                    in_=vk_bank[:].rearrange("p u c -> p c u"),
+            def project_values():
+                x_codes, x_scales = made["x_codes"], made["x_scales"]
+                vT = stage.tile([P, E_BLOCKS, S], BF16)
+                for m in range(E_BLOCKS):
+                    v_bank = prep_ps.tile([P, S], F32, tag="prep")
+                    for g in range(PASSES):
+                        nc.tensor.matmul_mx(
+                            out=v_bank[:],
+                            lhsT=w_codes[:, g, m * P : (m + 1) * P].bitcast(FP8X4),
+                            lhsT_scale=w_scales[:, g, m * P : (m + 1) * P],
+                            rhs=x_codes[:, g, :].bitcast(FP8X4),
+                            rhs_scale=x_scales[:, g, :],
+                            start=(g == 0),
+                            stop=(g == PASSES - 1),
+                        )
+                    nc.scalar.activation(
+                        out=vT[:, m, :], in_=v_bank[:], func=ACT.Relu, bias=bv_col[:, m : m + 1], scale=1.0
+                    )
+                made["vT"] = vT
+
+            def quantise_v():
+                vT = made["vT"]
+                vT_words = vT[:].bitcast(F32)
+                v_grouped = stage.tile([P, E, PACK], BF16, align_bytes=64)
+                for pair in range(E_BLOCKS // 2):
+                    vk_bank = prep_ps.tile([P, 2, PAIR], F32, tag="prep")
+                    flip_words(nc, ident_f32[:], vk_bank, [vT_words[:, 2 * pair + a, :] for a in range(2)], 0)
+                    nc.scalar.copy(
+                        out=v_grouped[:, pair * PAIR : (pair + 1) * PAIR, :].bitcast(F32),
+                        in_=vk_bank[:].rearrange("p u c -> p c u"),
+                    )
+                v_codes = batch.tile([P, E], U32, align_bytes=64)
+                v_scales = batch.tile([P, E], U8, align_bytes=64)
+                nc.vector.quantize_mx(
+                    out=v_codes[:].bitcast(FP8X4),
+                    scales=v_scales[:],
+                    in_=v_grouped[:].rearrange("p c j -> p (c j)"),
                 )
-            v_codes = batch.tile([P, E], U32, align_bytes=64)
-            v_scales = batch.tile([P, E], U8, align_bytes=64)
-            nc.vector.quantize_mx(
-                out=v_codes[:].bitcast(FP8X4),
-                scales=v_scales[:],
-                in_=v_grouped[:].rearrange("p c j -> p (c j)"),
-            )
-            return qT, kT, neg_mask, v_codes, v_scales
+                made["v_codes"], made["v_scales"] = v_codes, v_scales
+
+            return made, (mask_and_heads, quantise_values, project_values, quantise_v)
 
         def attend(b, i, operands):
-            qT, kT, neg_mask, v_codes, v_scales = operands
+            qT, kT, neg_mask = operands["qT"], operands["kT"], operands["neg_mask"]
+            v_codes, v_scales = operands["v_codes"], operands["v_scales"]
             q_rows = slice(i * P, (i + 1) * P)
             resid = rows.tile([P, E], BF16)
             nc.sync.dma_start(out=resid[:], in_=queries[b, q_rows, :])
@@ -236,36 +215,47 @@ def tile_multihead_attention_pa_kernel(
             neg_max = small.tile([P, NH], F32)
             row_sum = small.tile([P, NH], F32)
             y_sums = small.tile([P, NH], F32)
+
+            def masked_scores(first):
+                masked = work.tile([P, 2, S], F32)
+                for a in range(2):
+                    score = score_ps.tile([P, S], F32)
+                    nc.tensor.matmul(
+                        out=score[:], lhsT=qT[:, first + a, q_rows], rhs=kT[:, first + a, :], start=True, stop=True
+                    )
+                    nc.vector.scalar_tensor_tensor(
+                        out=masked[:, a, :], in0=score[:], scalar=SCALE, in1=neg_mask[:],
+                        op0=ALU.mult, op1=ALU.add,
+                    )
+                return masked
+
+            masked_next = masked_scores(0)
             for first_head in range(0, NH, HALF_HEADS):
                 e_grouped = halves.tile([P, HALF_HEADS * P, PACK], BF16, align_bytes=64)
                 for pair in range(HALF_HEADS // 2):
-                    e_words = []
+                    head = first_head + 2 * pair
+                    masked = masked_next
+                    if head + 2 < NH:
+                        masked_next = masked_scores(head + 2)
+                    nc.vector.tensor_reduce(
+                        out=neg_max[:, head : head + 2], in_=masked[:], axis=AXIS.X, op=ALU.max, negate=True
+                    )
+                    e = work.tile([P, 2, S], BF16)
                     for a in range(2):
-                        h = first_head + 2 * pair + a
-                        score = score_ps.tile([P, S], F32)
-                        nc.tensor.matmul(
-                            out=score[:], lhsT=qT[:, h, q_rows], rhs=kT[:, h, :], start=True, stop=True
-                        )
-                        masked = work.tile([P, S], F32)
-                        nc.vector.scalar_tensor_tensor(
-                            out=masked[:], in0=score[:], scalar=SCALE, in1=neg_mask[:],
-                            op0=ALU.mult, op1=ALU.add,
-                        )
-                        nc.vector.tensor_reduce(
-                            out=neg_max[:, h : h + 1], in_=masked[:], axis=AXIS.X, op=ALU.max, negate=True
-                        )
-                        e = work.tile([P, S], BF16)
                         nc.scalar.activation(
-                            out=e[:], in_=masked[:], func=ACT.Exp, bias=neg_max[:, h : h + 1], scale=1.0,
-                            accum_out=row_sum[:, h : h + 1],
+                            out=e[:, a, :], in_=masked[:, a, :], func=ACT.Exp,
+                            bias=neg_max[:, head + a : head + a + 1], scale=1.0,
+                            accum_out=row_sum[:, head + a : head + a + 1],
                         )
-                        e_words.append(e[:].bitcast(F32))
+                    e_words = e[:].bitcast(F32)
                     e_bank = flip_ps.tile([P, 2, PAIR], F32)
-                    flip_words(nc, ident_f32[:], e_bank, e_words, 0)
+                    flip_words(nc, ident_f32[:], e_bank, [e_words[:, a, :] for a in range(2)], 0)
                     nc.scalar.copy(
                         out=e_grouped[:, pair * PAIR : (pair + 1) * PAIR, :].bitcast(F32),
                         in_=e_bank[:].rearrange("p u c -> p c u"),
                     )
+                inv_sum = small.tile([P, HALF_HEADS], F32)
+                nc.vector.reciprocal(out=inv_sum[:], in_=row_sum[:, first_head : first_head + HALF_HEADS])
                 e_codes = halves.tile([P, HALF_HEADS * P], U32, align_bytes=64)
                 e_scales = halves.tile([P, HALF_HEADS * P], U8, align_bytes=64)
                 nc.vector.quantize_mx(
@@ -285,8 +275,6 @@ def tile_multihead_attention_pa_kernel(
                         start=True,
                         stop=True,
                     )
-                inv_sum = small.tile([P, HALF_HEADS], F32)
-                nc.vector.reciprocal(out=inv_sum[:], in_=row_sum[:, first_head : first_head + HALF_HEADS])
                 for a in range(HALF_HEADS):
                     h = first_head + a
                     feats = slice(h * DH, (h + 1) * DH)
@@ -325,10 +313,55 @@ def tile_multihead_attention_pa_kernel(
             nc.gpsimd.tensor_tensor(out=y[:], in0=y[:], in1=betta_all[:], op=ALU.add)
             nc.gpsimd.dma_start(out=out[b, q_rows, :], in_=y[:])
 
-        loads = first_loads
+        made, steps = preparation(first_loads)
+        steps[0]()
+        steps[1]()
+
+        w_codes = const.tile([P, PASSES, E], U32, align_bytes=64)
+        w_scales = const.tile([P, PASSES, E], U8, align_bytes=64)
+        for pair in range(E_BLOCKS // 2):
+            cols = slice(pair * PAIR, (pair + 1) * PAIR)
+            w_raw = raw.tile([P, 2, E], BF16, bufs=2)
+            nc.sync.dma_start(out=w_raw[:], in_=Wv[cols, :].rearrange("(a p) k -> p a k", p=P))
+            w_words = w_raw[:].bitcast(F32)
+            w_grouped = stage.tile([P, PASSES, PAIR, PACK], BF16, bufs=2, align_bytes=64)
+            for g in range(PASSES):
+                w_bank = prep_ps.tile([P, 2, PAIR], F32, tag="prep")
+                flip_words(nc, ident_f32[:], w_bank, [w_words[:, a, :] for a in range(2)], g * PAIR)
+                nc.vector.tensor_copy(
+                    out=w_grouped[:, g, :, :].bitcast(F32),
+                    in_=w_bank[:].rearrange("p u c -> p c u"),
+                )
+            for g in range(PASSES):
+                nc.vector.quantize_mx(
+                    out=w_codes[:, g, cols].bitcast(FP8X4),
+                    scales=w_scales[:, g, cols],
+                    in_=w_grouped[:, g, :, :].rearrange("p c j -> p (c j)"),
+                )
+
+        bv_rows = const.tile([P, P], BF16)
+        nc.vector.memset(bv_rows[:], 0.0)
+        nc.sync.dma_start(out=bv_rows[0:E_BLOCKS, :], in_=bv.rearrange("(r c) -> r c", c=P))
+        bv_bank = prep_ps.tile([P, P], BF16, tag="prep")
+        nc.tensor.transpose(bv_bank[:], bv_rows[:], ident_bf[:])
+        bv_col = const.tile([P, E_BLOCKS], F32)
+        nc.vector.tensor_copy(out=bv_col[:], in_=bv_bank[:, 0:E_BLOCKS])
+        gamma_all = const.tile([P, E], BF16)
+        nc.sync.dma_start(out=gamma_all[:], in_=gamma.partition_broadcast(P))
+        betta_all = const.tile([P, E], BF16)
+        nc.sync.dma_start(out=betta_all[:], in_=betta.partition_broadcast(P))
+        one_half = const.tile([P, 1], F32)
+        nc.vector.memset(one_half[:], 0.5)
+        minus_one = const.tile([P, 1], F32)
+        nc.vector.memset(minus_one[:], -1.0)
+
+        steps[2]()
+        steps[3]()
         for b in range(B):
-            operands = prepare_batch(loads)
+            operands = made
             if b + 1 < B:
-                loads = load_batch(b + 1)
+                made, steps = preparation(load_batch(b + 1))
             for i in range(S_BLOCKS):
                 attend(b, i, operands)
+                if b + 1 < B:
+                    steps[i]()

@@ -23,7 +23,7 @@ PASSES = E // K_PASS
 PAIR = 2 * P
 HALF_HEADS = NH // 2
 SCALE = 1.0 / DH**0.5
-NEG = -(2.0**32) + 1.0
+NEG_RAW = -(2.0**36)
 EPS = 1e-08
 
 FLOPS = 2 * B * S * E * E + 2 * (2 * B * NH * S * S * DH)
@@ -49,319 +49,491 @@ def tile_multihead_attention_pa_kernel(
         stage = ctx.enter_context(tc.tile_pool(name="stage", bufs=1))
         batch = ctx.enter_context(tc.tile_pool(name="batch", bufs=2))
         work = ctx.enter_context(tc.tile_pool(name="work", bufs=3))
-        halves = ctx.enter_context(tc.tile_pool(name="halves", bufs=2))
+        halves = ctx.enter_context(tc.tile_pool(name="halves", bufs=4))
         rows = ctx.enter_context(tc.tile_pool(name="rows", bufs=3))
-        small = ctx.enter_context(tc.tile_pool(name="small", bufs=4))
+        small = ctx.enter_context(tc.tile_pool(name="small", bufs=6))
         prep_ps = ctx.enter_context(tc.psum_pool(name="prep_ps", bufs=2))
-        score_ps = ctx.enter_context(tc.psum_pool(name="score_ps", bufs=3))
-        flip_ps = ctx.enter_context(tc.psum_pool(name="flip_ps", bufs=2))
+        score_ps = ctx.enter_context(tc.psum_pool(name="score_ps", bufs=4))
+        flip_ps = ctx.enter_context(tc.psum_pool(name="flip_ps", bufs=1))
         att_ps = ctx.enter_context(tc.psum_pool(name="att_ps", bufs=1))
+
+        def load_rows(source, name):
+            loaded = raw.tile([P, S_BLOCKS, E], BF16, name=name)
+            nc.sync.dma_start(out=loaded[:], in_=source.rearrange("(j p) e -> p j e", p=P))
+            return loaded
+
+        def load_batch(b):
+            return {
+                "keys": load_rows(keys[b], "keys_raw"),
+                "q": load_rows(q_relu[b], "q_raw"),
+                "k": load_rows(k_relu[b], "k_raw"),
+                "x": load_rows(values[b], "x_raw"),
+            }
+
+        first_loads = load_batch(0)
 
         ident_bf = const.tile([P, P], BF16)
         make_identity(nc, ident_bf[:])
         ident_f32 = const.tile([P, P], F32)
         make_identity(nc, ident_f32[:])
 
-        def load_batch(b):
-            keys_raw = raw.tile([P, S_BLOCKS, E], BF16)
-            nc.sync.dma_start(out=keys_raw[:], in_=keys[b].rearrange("(j p) e -> p j e", p=P))
-            q_raw = raw.tile([P, S_BLOCKS, E], BF16)
-            nc.sync.dma_start(out=q_raw[:], in_=q_relu[b].rearrange("(j p) e -> p j e", p=P))
-            k_raw = raw.tile([P, S_BLOCKS, E], BF16)
-            nc.sync.dma_start(out=k_raw[:], in_=k_relu[b].rearrange("(j p) e -> p j e", p=P))
-            x_raw = raw.tile([P, S_BLOCKS, E], BF16)
-            nc.sync.dma_start(out=x_raw[:], in_=values[b].rearrange("(j p) e -> p j e", p=P))
-            return keys_raw, k_raw, q_raw, x_raw
+        ctx.enter_context(tc.manual_schedule())
 
-        first_loads = load_batch(0)
+        w_codes = const.tile([P, PASSES, E], U32, align_bytes=64)
+        w_scales = const.tile([P, PASSES, E], U8, align_bytes=64)
+        bv_col = const.tile([P, E_BLOCKS], F32)
+        gamma_all = const.tile([P, E], BF16)
+        betta_all = const.tile([P, E], BF16)
+        one_half = const.tile([P, 1], F32)
+        nc.vector.memset(one_half[:], 0.5)
+        minus_one = const.tile([P, 1], F32)
+        nc.vector.memset(minus_one[:], -1.0)
 
-        def preparation(loads):
-            keys_raw, k_raw, q_raw, x_raw = loads
-            made = {}
+        def copy_on(engine, out, in_):
+            if engine == "scalar":
+                nc.scalar.copy(out=out, in_=in_)
+            else:
+                nc.vector.tensor_copy(out=out, in_=in_)
 
-            def mask_and_heads():
-                qT = batch.tile([P, NH, S], BF16)
-                for first_head in range(0, NH, 2):
-                    q_bank = prep_ps.tile([P, 2, S], BF16, tag="prep")
-                    for a in range(2):
-                        feats = slice((first_head + a) * DH, (first_head + a + 1) * DH)
-                        for j in range(S_BLOCKS):
-                            nc.tensor.transpose(q_bank[:, a, j * P : (j + 1) * P], q_raw[:, j, feats], ident_bf[:])
-                    nc.scalar.copy(out=qT[:, first_head : first_head + 2, :], in_=q_bank[:])
+        def make_mask(loads, made):
+            keys_raw = loads["keys"]
+            fold_a = stage.tile([P, S_BLOCKS, E // 2], F32)
+            nc.gpsimd.tensor_tensor(
+                out=fold_a[:], in0=keys_raw[:, :, 0 : E // 2], in1=keys_raw[:, :, E // 2 : E], op=ALU.add
+            )
+            fold_b = stage.tile([P, S_BLOCKS, E // 4], F32)
+            nc.gpsimd.tensor_tensor(
+                out=fold_b[:], in0=fold_a[:, :, 0 : E // 4], in1=fold_a[:, :, E // 4 : E // 2], op=ALU.add
+            )
+            fold_c = stage.tile([P, S_BLOCKS, E // 8], F32)
+            nc.gpsimd.tensor_tensor(
+                out=fold_c[:], in0=fold_b[:, :, 0 : E // 8], in1=fold_b[:, :, E // 8 : E // 4], op=ALU.add
+            )
+            made["folded"] = fold_c
 
-                fold_a = stage.tile([P, S_BLOCKS, E // 2], F32)
-                nc.gpsimd.tensor_tensor(
-                    out=fold_a[:], in0=keys_raw[:, :, 0 : E // 2], in1=keys_raw[:, :, E // 2 : E], op=ALU.add
-                )
-                fold_b = stage.tile([P, S_BLOCKS, E // 4], F32)
-                nc.gpsimd.tensor_tensor(
-                    out=fold_b[:], in0=fold_a[:, :, 0 : E // 4], in1=fold_a[:, :, E // 4 : E // 2], op=ALU.add
-                )
-                fold_c = stage.tile([P, S_BLOCKS, E // 8], F32)
-                nc.gpsimd.tensor_tensor(
-                    out=fold_c[:], in0=fold_b[:, :, 0 : E // 8], in1=fold_b[:, :, E // 8 : E // 4], op=ALU.add
-                )
-                key_sum = small.tile([P, S_BLOCKS], F32)
-                nc.vector.tensor_reduce(out=key_sum[:], in_=fold_c[:], axis=AXIS.X, op=ALU.add)
-                keep = small.tile([P, S_BLOCKS], F32)
-                nc.vector.tensor_single_scalar(out=keep[:], in_=key_sum[:], scalar=0.0, op=ALU.not_equal)
-                neg_c = small.tile([P, S_BLOCKS], BF16)
-                nc.vector.tensor_scalar(
-                    out=neg_c[:], in0=key_sum[:], scalar1=0.0, scalar2=NEG, op0=ALU.is_equal, op1=ALU.mult
-                )
-                keep_diag = batch.tile([P, S_BLOCKS, P], BF16)
-                for j in range(S_BLOCKS):
-                    nc.vector.tensor_scalar(
-                        out=keep_diag[:, j, :], in0=ident_bf[:], scalar1=keep[:, j : j + 1], scalar2=None,
-                        op0=ALU.mult,
-                    )
-
-                mask_bank = prep_ps.tile([P, S], F32, tag="prep")
-                for j in range(S_BLOCKS):
-                    nc.tensor.matmul(
-                        out=mask_bank[:, j * P : (j + 1) * P],
-                        lhsT=neg_c[:, j : j + 1].to_broadcast([P, P]),
-                        rhs=ident_bf[:],
-                        start=True,
-                        stop=True,
-                    )
-                neg_mask = batch.tile([P, S], BF16)
-                nc.vector.tensor_copy(out=neg_mask[:], in_=mask_bank[:])
-
-                kT = batch.tile([P, NH, S], BF16)
-                for first_head in range(0, NH, 2):
-                    k_bank = prep_ps.tile([P, 2, S], BF16, tag="prep")
-                    for a in range(2):
-                        feats = slice((first_head + a) * DH, (first_head + a + 1) * DH)
-                        for j in range(S_BLOCKS):
-                            nc.tensor.transpose(
-                                k_bank[:, a, j * P : (j + 1) * P], k_raw[:, j, feats], keep_diag[:, j, :]
-                            )
-                    nc.scalar.copy(out=kT[:, first_head : first_head + 2, :], in_=k_bank[:])
-                made["qT"], made["kT"], made["neg_mask"] = qT, kT, neg_mask
-
-            def quantise_values():
-                x_words = x_raw[:].bitcast(F32)
-                x_grouped = stage.tile([P, PASSES, S, PACK], BF16, align_bytes=64)
-                x_codes = stage.tile([P, PASSES, S], U32, align_bytes=64)
-                x_scales = stage.tile([P, PASSES, S], U8, align_bytes=64)
-                for g in range(PASSES):
-                    for pair in range(S_BLOCKS // 2):
-                        x_bank = prep_ps.tile([P, 2, PAIR], F32, tag="prep")
-                        flip_words(
-                            nc, ident_f32[:], x_bank, [x_words[:, 2 * pair + a, :] for a in range(2)], g * PAIR
-                        )
-                        nc.scalar.copy(
-                            out=x_grouped[:, g, pair * PAIR : (pair + 1) * PAIR, :].bitcast(F32),
-                            in_=x_bank[:].rearrange("p u c -> p c u"),
-                        )
-                for g in range(PASSES):
-                    nc.vector.quantize_mx(
-                        out=x_codes[:, g, :].bitcast(FP8X4),
-                        scales=x_scales[:, g, :],
-                        in_=x_grouped[:, g, :, :].rearrange("p c j -> p (c j)"),
-                    )
-                made["x_codes"], made["x_scales"] = x_codes, x_scales
-
-            def project_values():
-                x_codes, x_scales = made["x_codes"], made["x_scales"]
-                vT = stage.tile([P, E_BLOCKS, S], BF16)
-                for m in range(E_BLOCKS):
-                    v_bank = prep_ps.tile([P, S], F32, tag="prep")
-                    for g in range(PASSES):
-                        nc.tensor.matmul_mx(
-                            out=v_bank[:],
-                            lhsT=w_codes[:, g, m * P : (m + 1) * P].bitcast(FP8X4),
-                            lhsT_scale=w_scales[:, g, m * P : (m + 1) * P],
-                            rhs=x_codes[:, g, :].bitcast(FP8X4),
-                            rhs_scale=x_scales[:, g, :],
-                            start=(g == 0),
-                            stop=(g == PASSES - 1),
-                        )
-                    nc.scalar.activation(
-                        out=vT[:, m, :], in_=v_bank[:], func=ACT.Relu, bias=bv_col[:, m : m + 1], scale=1.0
-                    )
-                made["vT"] = vT
-
-            def quantise_v():
-                vT = made["vT"]
-                vT_words = vT[:].bitcast(F32)
-                v_grouped = stage.tile([P, E, PACK], BF16, align_bytes=64)
-                for pair in range(E_BLOCKS // 2):
-                    vk_bank = prep_ps.tile([P, 2, PAIR], F32, tag="prep")
-                    flip_words(nc, ident_f32[:], vk_bank, [vT_words[:, 2 * pair + a, :] for a in range(2)], 0)
-                    nc.scalar.copy(
-                        out=v_grouped[:, pair * PAIR : (pair + 1) * PAIR, :].bitcast(F32),
-                        in_=vk_bank[:].rearrange("p u c -> p c u"),
-                    )
-                v_codes = batch.tile([P, E], U32, align_bytes=64)
-                v_scales = batch.tile([P, E], U8, align_bytes=64)
-                nc.vector.quantize_mx(
-                    out=v_codes[:].bitcast(FP8X4),
-                    scales=v_scales[:],
-                    in_=v_grouped[:].rearrange("p c j -> p (c j)"),
-                )
-                made["v_codes"], made["v_scales"] = v_codes, v_scales
-
-            return made, (mask_and_heads, quantise_values, project_values, quantise_v)
-
-        def attend(b, i, operands):
-            qT, kT, neg_mask = operands["qT"], operands["kT"], operands["neg_mask"]
-            v_codes, v_scales = operands["v_codes"], operands["v_scales"]
-            q_rows = slice(i * P, (i + 1) * P)
-            resid = rows.tile([P, E], BF16)
-            nc.sync.dma_start(out=resid[:], in_=queries[b, q_rows, :])
-            y = rows.tile([P, E], F32)
-            neg_max = small.tile([P, NH], F32)
-            row_sum = small.tile([P, NH], F32)
-            y_sums = small.tile([P, NH], F32)
-
-            def masked_scores(first):
-                masked = work.tile([P, 2, S], F32)
-                for a in range(2):
-                    score = score_ps.tile([P, S], F32)
-                    nc.tensor.matmul(
-                        out=score[:], lhsT=qT[:, first + a, q_rows], rhs=kT[:, first + a, :], start=True, stop=True
-                    )
-                    nc.vector.scalar_tensor_tensor(
-                        out=masked[:, a, :], in0=score[:], scalar=SCALE, in1=neg_mask[:],
-                        op0=ALU.mult, op1=ALU.add,
-                    )
-                return masked
-
-            masked_next = masked_scores(0)
-            for first_head in range(0, NH, HALF_HEADS):
-                e_grouped = halves.tile([P, HALF_HEADS * P, PACK], BF16, align_bytes=64)
-                for pair in range(HALF_HEADS // 2):
-                    head = first_head + 2 * pair
-                    masked = masked_next
-                    if head + 2 < NH:
-                        masked_next = masked_scores(head + 2)
-                    nc.vector.tensor_reduce(
-                        out=neg_max[:, head : head + 2], in_=masked[:], axis=AXIS.X, op=ALU.max, negate=True
-                    )
-                    e = work.tile([P, 2, S], BF16)
-                    for a in range(2):
-                        nc.scalar.activation(
-                            out=e[:, a, :], in_=masked[:, a, :], func=ACT.Exp,
-                            bias=neg_max[:, head + a : head + a + 1], scale=1.0,
-                            accum_out=row_sum[:, head + a : head + a + 1],
-                        )
-                    e_words = e[:].bitcast(F32)
-                    e_bank = flip_ps.tile([P, 2, PAIR], F32)
-                    flip_words(nc, ident_f32[:], e_bank, [e_words[:, a, :] for a in range(2)], 0)
-                    nc.scalar.copy(
-                        out=e_grouped[:, pair * PAIR : (pair + 1) * PAIR, :].bitcast(F32),
-                        in_=e_bank[:].rearrange("p u c -> p c u"),
-                    )
-                inv_sum = small.tile([P, HALF_HEADS], F32)
-                nc.vector.reciprocal(out=inv_sum[:], in_=row_sum[:, first_head : first_head + HALF_HEADS])
-                e_codes = halves.tile([P, HALF_HEADS * P], U32, align_bytes=64)
-                e_scales = halves.tile([P, HALF_HEADS * P], U8, align_bytes=64)
-                nc.vector.quantize_mx(
-                    out=e_codes[:].bitcast(FP8X4),
-                    scales=e_scales[:],
-                    in_=e_grouped[:].rearrange("p c j -> p (c j)"),
-                )
-                att = att_ps.tile([P, HALF_HEADS, DH], F32)
-                for a in range(HALF_HEADS):
-                    h = first_head + a
-                    nc.tensor.matmul_mx(
-                        out=att[:, a, :],
-                        lhsT=e_codes[:, a * P : (a + 1) * P].bitcast(FP8X4),
-                        lhsT_scale=e_scales[:, a * P : (a + 1) * P],
-                        rhs=v_codes[:, h * DH : (h + 1) * DH].bitcast(FP8X4),
-                        rhs_scale=v_scales[:, h * DH : (h + 1) * DH],
-                        start=True,
-                        stop=True,
-                    )
-                for a in range(HALF_HEADS):
-                    h = first_head + a
-                    feats = slice(h * DH, (h + 1) * DH)
-                    nc.vector.scalar_tensor_tensor(
-                        out=y[:, feats], in0=att[:, a, :], scalar=inv_sum[:, a : a + 1], in1=resid[:, feats],
-                        op0=ALU.mult, op1=ALU.add, accum_out=y_sums[:, h : h + 1],
-                    )
-
-            neg_total = small.tile([P, 1], F32)
-            nc.vector.tensor_reduce(out=neg_total[:], in_=y_sums[:], axis=AXIS.X, op=ALU.add, negate=True)
-            neg_mean = small.tile([P, 1], F32)
+        def finish_mask(made, rows_to_add):
+            key_sum = small.tile([P, S_BLOCKS], F32)
+            nc.vector.tensor_reduce(out=key_sum[:], in_=rows_to_add[:], axis=AXIS.X, op=ALU.add)
+            keep = small.tile([P, S_BLOCKS], F32)
+            nc.vector.tensor_single_scalar(out=keep[:], in_=key_sum[:], scalar=0.0, op=ALU.not_equal)
+            neg_c = small.tile([P, S_BLOCKS], F32)
             nc.vector.tensor_scalar(
-                out=neg_mean[:], in0=neg_total[:], scalar1=1.0 / E, scalar2=None, op0=ALU.mult
+                out=neg_c[:], in0=key_sum[:], scalar1=0.0, scalar2=NEG_RAW, op0=ALU.is_equal, op1=ALU.mult
             )
-            squares = rows.tile([P, E], BF16)
-            sum_sq = small.tile([P, 1], F32)
+            keep_diag = batch.tile([P, S_BLOCKS, P], BF16)
+            for j in range(S_BLOCKS):
+                nc.vector.tensor_scalar(
+                    out=keep_diag[:, j, :], in0=ident_bf[:], scalar1=keep[:, j : j + 1], scalar2=None, op0=ALU.mult
+                )
+            neg_rows = batch.tile([P, S_BLOCKS, P], F32)
+            nc.vector.tensor_copy(out=neg_rows[:], in_=neg_c[:].unsqueeze(2).to_broadcast([P, S_BLOCKS, P]))
+            made["keep_diag"], made["neg_rows"] = keep_diag, neg_rows
+
+        def allocate(made):
+            made["qT"] = batch.tile([P, NH, S], BF16, name="qT")
+            made["kT"] = batch.tile([P, NH, S], BF16, name="kT")
+
+        def staged(made, name, shape):
+            if name not in made:
+                made[name] = stage.tile(shape, BF16, align_bytes=64, name=name)
+            return made[name]
+
+        def heads_item(loads, made, which, first_head):
+            def fill():
+                bank = prep_ps.tile([P, 2, S], BF16, tag="prep", name="head_bank")
+                for a in range(2):
+                    feats = slice((first_head + a) * DH, (first_head + a + 1) * DH)
+                    for j in range(S_BLOCKS):
+                        identity = ident_bf[:] if which == "q" else made["keep_diag"][:, j, :]
+                        nc.tensor.transpose(bank[:, a, j * P : (j + 1) * P], loads[which][:, j, feats], identity)
+                return bank
+
+            def empty(bank, engine):
+                copy_on(engine, made[which + "T"][:, first_head : first_head + 2, :], bank[:])
+
+            return fill, empty
+
+        def x_item(loads, made, g, pair):
+            def fill():
+                bank = prep_ps.tile([P, 2, PAIR], F32, tag="prep", name="x_bank")
+                x_words = loads["x"][:].bitcast(F32)
+                flip_words(nc, ident_f32[:], bank, [x_words[:, 2 * pair + a, :] for a in range(2)], g * PAIR)
+                return bank
+
+            def empty(bank, engine):
+                copy_on(
+                    engine,
+                    staged(made, "x_grouped", [P, PASSES, S, PACK])[:, g, pair * PAIR : (pair + 1) * PAIR, :].bitcast(F32),
+                    bank[:].rearrange("p u c -> p c u"),
+                )
+
+            return fill, empty
+
+        def quantise_x(made, g):
+            if g == 0:
+                made["x_codes"] = stage.tile([P, PASSES, S], U32, align_bytes=64, name="x_codes")
+                made["x_scales"] = stage.tile([P, PASSES, S], U8, align_bytes=64, name="x_scales")
+            nc.vector.quantize_mx(
+                out=made["x_codes"][:, g, :].bitcast(FP8X4),
+                scales=made["x_scales"][:, g, :],
+                in_=made["x_grouped"][:, g, :, :].rearrange("p c j -> p (c j)"),
+            )
+
+        def project_item(made, m):
+            def fill():
+                bank = prep_ps.tile([P, S], F32, tag="prep", name="v_bank")
+                for g in range(PASSES):
+                    nc.tensor.matmul_mx(
+                        out=bank[:],
+                        lhsT=w_codes[:, g, m * P : (m + 1) * P].bitcast(FP8X4),
+                        lhsT_scale=w_scales[:, g, m * P : (m + 1) * P],
+                        rhs=made["x_codes"][:, g, :].bitcast(FP8X4),
+                        rhs_scale=made["x_scales"][:, g, :],
+                        start=(g == 0),
+                        stop=(g == PASSES - 1),
+                    )
+                return bank
+
+            def empty(bank, engine):
+                vT = staged(made, "vT", [P, E_BLOCKS, S])
+                if engine == "scalar":
+                    nc.scalar.activation(
+                        out=vT[:, m, :], in_=bank[:], func=ACT.Relu, bias=bv_col[:, m : m + 1], scale=1.0
+                    )
+                else:
+                    nc.vector.tensor_scalar(
+                        out=vT[:, m, :], in0=bank[:], scalar1=bv_col[:, m : m + 1], scalar2=0.0,
+                        op0=ALU.add, op1=ALU.max,
+                    )
+
+            return fill, empty
+
+        def v_item(made, pair):
+            def fill():
+                bank = prep_ps.tile([P, 2, PAIR], F32, tag="prep", name="vk_bank")
+                vT_words = made["vT"][:].bitcast(F32)
+                flip_words(nc, ident_f32[:], bank, [vT_words[:, 2 * pair + a, :] for a in range(2)], 0)
+                return bank
+
+            def empty(bank, engine):
+                copy_on(
+                    engine,
+                    staged(made, "v_grouped", [P, E, PACK])[:, pair * PAIR : (pair + 1) * PAIR, :].bitcast(F32),
+                    bank[:].rearrange("p u c -> p c u"),
+                )
+
+            return fill, empty
+
+        def quantise_v(made):
+            made["v_codes"] = batch.tile([P, E], U32, align_bytes=64, name="v_codes")
+            made["v_scales"] = batch.tile([P, E], U8, align_bytes=64, name="v_scales")
+            nc.vector.quantize_mx(
+                out=made["v_codes"][:].bitcast(FP8X4),
+                scales=made["v_scales"][:],
+                in_=made["v_grouped"][:].rearrange("p c j -> p (c j)"),
+            )
+
+        def w_item(g, grouped, words):
+            def fill():
+                bank = prep_ps.tile([P, 2, PAIR], F32, tag="prep", name="w_bank")
+                flip_words(nc, ident_f32[:], bank, [words[:, a, :] for a in range(2)], g * PAIR)
+                return bank
+
+            def empty(bank, engine):
+                copy_on(engine, grouped[:].bitcast(F32), bank[:].rearrange("p u c -> p c u"))
+
+            return fill, empty
+
+        made = {}
+        allocate(made)
+        w_tiles = []
+        for pair in range(E_BLOCKS // 2):
+            w_raw = raw.tile([P, 2, E], BF16, bufs=4)
+            nc.sync.dma_start(
+                out=w_raw[:], in_=Wv[pair * PAIR : (pair + 1) * PAIR, :].rearrange("(a p) k -> p a k", p=P)
+            )
+            w_tiles.append(w_raw)
+        bv_rows = const.tile([P, P], BF16)
+        nc.vector.memset(bv_rows[:], 0.0)
+        nc.sync.dma_start(out=bv_rows[0:E_BLOCKS, :], in_=bv.rearrange("(r c) -> r c", c=P))
+        nc.sync.dma_start(out=gamma_all[:], in_=gamma.partition_broadcast(P))
+        nc.sync.dma_start(out=betta_all[:], in_=betta.partition_broadcast(P))
+
+        def w_items():
+            items = []
+            for pair in range(E_BLOCKS // 2):
+                words = w_tiles[pair][:].bitcast(F32)
+                cols = slice(pair * PAIR, (pair + 1) * PAIR)
+                for g in range(PASSES):
+                    grouped = stage.tile([P, PAIR, PACK], BF16, bufs=4, align_bytes=64, name="w_grouped")
+                    fill, empty = w_item(g, grouped, words)
+
+                    def then(g=g, cols=cols, grouped=grouped):
+                        nc.vector.quantize_mx(
+                            out=w_codes[:, g, cols].bitcast(FP8X4),
+                            scales=w_scales[:, g, cols],
+                            in_=grouped[:].rearrange("p c j -> p (c j)"),
+                        )
+
+                    items.append((fill, empty, then))
+            return items
+
+        def bias_item():
+            def fill():
+                bank = prep_ps.tile([P, P], BF16, tag="prep", name="bv_bank")
+                nc.tensor.transpose(bank[:], bv_rows[:], ident_bf[:])
+                return bank
+
+            def empty(bank, engine):
+                nc.vector.tensor_copy(out=bv_col[:], in_=bank[:, 0:E_BLOCKS])
+
+            return fill, empty, None
+
+        def preparation(loads, made):
+            q_items = [heads_item(loads, made, "q", h) + (None,) for h in range(0, NH, 2)]
+            k_items = [heads_item(loads, made, "k", h) + (None,) for h in range(0, NH, 2)]
+            x_items = []
+            for g in range(PASSES):
+                x_items.append(x_item(loads, made, g, 0) + (None,))
+                x_items.append(x_item(loads, made, g, 1) + (lambda g=g: quantise_x(made, g),))
+            p_items = [project_item(made, m) + (None,) for m in range(E_BLOCKS)]
+            v_items = [v_item(made, pair) + (None,) for pair in range(E_BLOCKS // 2 - 1)]
+            v_items.append(v_item(made, E_BLOCKS // 2 - 1) + (lambda: quantise_v(made),))
+            return q_items, k_items, x_items, p_items, v_items
+
+        to_empty = []
+
+        def empty_one():
+            bank, empty, then, engine = to_empty.pop(0)
+            empty(bank, engine)
+            if then is not None:
+                then()
+
+        def emit(item, engine):
+            if len(to_empty) == 2:
+                empty_one()
+            fill, empty, then = item
+            to_empty.append((fill(), empty, then, engine))
+
+        finish_mask(made, first_loads["keys"])
+        q_items, k_items, x_items, p_items, v_items = preparation(first_loads, made)
+        emit(q_items[0], "scalar")
+        emit(k_items[0], "vector")
+        emit(q_items[1], "scalar")
+        emit(k_items[1], "vector")
+        empty_one()
+        empty_one()
+        first_items = [q_items[2], k_items[2], q_items[3], k_items[3]] + x_items + w_items() + [bias_item()] + p_items + v_items
+
+        operands = [made]
+        heads = B * S_BLOCKS * NH
+        score_of, e_of, flip_of = {}, {}, {}
+        block_of = {}
+
+        def block(t):
+            g = t // NH
+            if g not in block_of:
+                b, i = g // S_BLOCKS, g % S_BLOCKS
+                block_of[g] = {
+                    "b": b, "i": i, "grouped": {},
+                    "neg_max": small.tile([P, NH], F32, name="neg_max"),
+                    "row_sum": small.tile([P, NH], F32, name="row_sum"),
+                }
+            return block_of[g]
+
+        def load_residual(g):
+            d = block(g * NH)
+            d["resid"] = rows.tile([P, E], BF16, bufs=5, name="resid")
+            nc.sync.dma_start(out=d["resid"][:], in_=queries[d["b"], d["i"] * P : (d["i"] + 1) * P, :])
+
+        def scores(t):
+            d, h = block(t), t % NH
+            m = operands[d["b"]]
+            score = score_ps.tile([P, S], F32, name="score")
+            nc.tensor.matmul(
+                out=score[:], lhsT=m["qT"][:, h, d["i"] * P : (d["i"] + 1) * P], rhs=m["kT"][:, h, :],
+                start=True, stop=False,
+            )
+            for j in range(S_BLOCKS):
+                nc.tensor.matmul(
+                    out=score[:, j * P : (j + 1) * P], lhsT=m["neg_rows"][:, j, :], rhs=ident_f32[:],
+                    start=False, stop=(j == S_BLOCKS - 1), is_transpose=True,
+                )
+            score_of[t] = score
+
+        def maximum(t):
+            d, h = block(t), t % NH
+            top = small.tile([P, 1], F32, name="top")
+            nc.vector.tensor_reduce(out=top[:], in_=score_of[t][:], axis=AXIS.X, op=ALU.max)
+            nc.vector.tensor_scalar(
+                out=d["neg_max"][:, h : h + 1], in0=top[:], scalar1=-SCALE, scalar2=None, op0=ALU.mult
+            )
+
+        def exponent(t):
+            d, h = block(t), t % NH
+            if t % 2 == 0:
+                e_of[t // 2] = work.tile([P, 2, S], BF16, name="e")
             nc.scalar.activation(
-                out=squares[:], in_=y[:], func=ACT.Square, bias=neg_mean[:, 0:1], scale=1.0, accum_out=sum_sq[:]
+                out=e_of[t // 2][:, t % 2, :], in_=score_of[t][:], func=ACT.Exp,
+                bias=d["neg_max"][:, h : h + 1], scale=SCALE, accum_out=d["row_sum"][:, h : h + 1],
             )
-            var = small.tile([P, 1], F32)
+
+        def flip(pair):
+            flip_of[pair] = flip_ps.tile([P, 2, PAIR], F32, name="e_bank")
+            e_words = e_of[pair][:].bitcast(F32)
+            flip_words(nc, ident_f32[:], flip_of[pair], [e_words[:, a, :] for a in range(2)], 0)
+
+        def group(pair, engine):
+            d = block(2 * pair)
+            half, at = (2 * pair) % NH // HALF_HEADS, pair % 2
+            if at == 0:
+                d["grouped"][half] = halves.tile([P, HALF_HEADS * P, PACK], BF16, align_bytes=64, name="e_grouped")
+            copy_on(
+                engine,
+                d["grouped"][half][:, at * PAIR : (at + 1) * PAIR, :].bitcast(F32),
+                flip_of[pair][:].rearrange("p u c -> p c u"),
+            )
+
+        def quantise_e(g, half):
+            d = block_of[g]
+            d["codes", half] = halves.tile([P, HALF_HEADS * P], U32, align_bytes=64, name="e_codes")
+            d["scales", half] = halves.tile([P, HALF_HEADS * P], U8, align_bytes=64, name="e_scales")
+            nc.vector.quantize_mx(
+                out=d["codes", half][:].bitcast(FP8X4),
+                scales=d["scales", half][:],
+                in_=d["grouped"][half][:].rearrange("p c j -> p (c j)"),
+            )
+
+        def weigh(g, half):
+            d = block_of[g]
+            m = operands[d["b"]]
+            d["att"] = att_ps.tile([P, HALF_HEADS, DH], F32, name="att")
+            for a in range(HALF_HEADS):
+                h = half * HALF_HEADS + a
+                nc.tensor.matmul_mx(
+                    out=d["att"][:, a, :],
+                    lhsT=d["codes", half][:, a * P : (a + 1) * P].bitcast(FP8X4),
+                    lhsT_scale=d["scales", half][:, a * P : (a + 1) * P],
+                    rhs=m["v_codes"][:, h * DH : (h + 1) * DH].bitcast(FP8X4),
+                    rhs_scale=m["v_scales"][:, h * DH : (h + 1) * DH],
+                    start=True,
+                    stop=True,
+                )
+
+        def add_residual(g, half):
+            d = block_of[g]
+            if half == 0:
+                d["y"] = rows.tile([P, E], F32, name="y")
+                d["stats"] = small.tile([P, 2, 6], F32, name="stats")
+            inv_sum = small.tile([P, HALF_HEADS], F32, name="inv_sum")
+            nc.vector.reciprocal(out=inv_sum[:], in_=d["row_sum"][:, half * HALF_HEADS : (half + 1) * HALF_HEADS])
+            for a in range(HALF_HEADS):
+                h = half * HALF_HEADS + a
+                feats = slice(h * DH, (h + 1) * DH)
+                nc.vector.scalar_tensor_tensor(
+                    out=d["y"][:, feats], in0=d["att"][:, a, :], scalar=inv_sum[:, a : a + 1],
+                    in1=d["resid"][:, feats], op0=ALU.mult, op1=ALU.add,
+                )
+
+        def statistics(g, half):
+            d = block_of[g]
+            cols = slice(half * HALF_HEADS * DH, (half + 1) * HALF_HEADS * DH)
+            nc.vector.bn_stats(out=d["stats"][:, half, :], in_=d["y"][:, cols])
+
+        def norm(g):
+            d = block_of[g]
+            y = d["y"]
+            moments = small.tile([P, 2], F32, name="moments")
+            nc.vector.bn_aggr(out=moments[:], in_=d["stats"][:])
+            neg_mean = small.tile([P, 1], F32, name="neg_mean")
             nc.gpsimd.tensor_scalar(
-                out=var[:], in0=sum_sq[:], scalar1=1.0 / (E - 1.0), scalar2=0.0, op0=ALU.mult, op1=ALU.add
+                out=neg_mean[:], in0=moments[:, 0:1], scalar1=-1.0, scalar2=0.0, op0=ALU.mult, op1=ALU.add
             )
-            sd = small.tile([P, 1], F32)
+            var = small.tile([P, 1], F32, name="var")
+            nc.gpsimd.tensor_scalar(
+                out=var[:], in0=moments[:, 1:2], scalar1=E / (E - 1.0), scalar2=0.0, op0=ALU.mult, op1=ALU.add
+            )
+            sd = small.tile([P, 1], F32, name="sd")
             nc.gpsimd.tensor_tensor(out=sd[:], in0=var[:], in1=one_half[:], op=ALU.pow)
-            sd_eps = small.tile([P, 1], F32)
-            nc.gpsimd.tensor_scalar(
-                out=sd_eps[:], in0=sd[:], scalar1=EPS, scalar2=1.0, op0=ALU.add, op1=ALU.mult
-            )
-            inv_sd = small.tile([P, 1], F32)
+            sd_eps = small.tile([P, 1], F32, name="sd_eps")
+            nc.gpsimd.tensor_scalar(out=sd_eps[:], in0=sd[:], scalar1=EPS, scalar2=1.0, op0=ALU.add, op1=ALU.mult)
+            inv_sd = small.tile([P, 1], F32, name="inv_sd")
             nc.gpsimd.tensor_tensor(out=inv_sd[:], in0=sd_eps[:], in1=minus_one[:], op=ALU.pow)
             nc.gpsimd.tensor_scalar(
                 out=y[:], in0=y[:], scalar1=neg_mean[:, 0:1], scalar2=inv_sd[:, 0:1], op0=ALU.add, op1=ALU.mult
             )
             nc.gpsimd.tensor_tensor(out=y[:], in0=y[:], in1=gamma_all[:], op=ALU.mult)
             nc.gpsimd.tensor_tensor(out=y[:], in0=y[:], in1=betta_all[:], op=ALU.add)
-            nc.gpsimd.dma_start(out=out[b, q_rows, :], in_=y[:])
+            nc.sync.dma_start(out=out[d["b"], d["i"] * P : (d["i"] + 1) * P, :], in_=y[:])
 
-        made, steps = preparation(first_loads)
-        steps[0]()
-        steps[1]()
+        SLOTS = S_BLOCKS * NH
+        LAG = 8
+        items, emitted = first_items, 0
+        n_first, n_batch = len(first_items), 2 * NH + E_BLOCKS
+        for t in range(-2, heads + LAG + 5):
+            inside = 0 <= t < heads
+            b, slot, local = t // SLOTS, t % SLOTS, t % NH
+            if inside and slot == 0 and b + 1 < B:
+                nxt = {}
+                allocate(nxt)
+                operands.append(nxt)
+            if t == 4:
+                next_loads = load_batch(1)
+            if inside and slot == (8 if b == 0 else 0) and b + 1 < B:
+                q_items, k_items, x_items, p_items, v_items = preparation(next_loads, nxt)
+                items = items + q_items + x_items + k_items + p_items + v_items
+                make_mask(next_loads, nxt)
+            if inside and slot == (17 if b == 0 else 9) and b + 1 < B:
+                finish_mask(nxt, nxt["folded"])
+            if inside and slot == 23 and b + 2 < B:
+                next_loads = load_batch(b + 2)
+            if t == -2:
+                load_residual(0)
+                load_residual(1)
+            if inside and local == 0 and t // NH + 2 < B * S_BLOCKS:
+                load_residual(t // NH + 2)
 
-        w_codes = const.tile([P, PASSES, E], U32, align_bytes=64)
-        w_scales = const.tile([P, PASSES, E], U8, align_bytes=64)
-        for pair in range(E_BLOCKS // 2):
-            cols = slice(pair * PAIR, (pair + 1) * PAIR)
-            w_raw = raw.tile([P, 2, E], BF16, bufs=2)
-            nc.sync.dma_start(out=w_raw[:], in_=Wv[cols, :].rearrange("(a p) k -> p a k", p=P))
-            w_words = w_raw[:].bitcast(F32)
-            w_grouped = stage.tile([P, PASSES, PAIR, PACK], BF16, bufs=2, align_bytes=64)
-            for g in range(PASSES):
-                w_bank = prep_ps.tile([P, 2, PAIR], F32, tag="prep")
-                flip_words(nc, ident_f32[:], w_bank, [w_words[:, a, :] for a in range(2)], g * PAIR)
-                nc.vector.tensor_copy(
-                    out=w_grouped[:, g, :, :].bitcast(F32),
-                    in_=w_bank[:].rearrange("p u c -> p c u"),
-                )
-            for g in range(PASSES):
-                nc.vector.quantize_mx(
-                    out=w_codes[:, g, cols].bitcast(FP8X4),
-                    scales=w_scales[:, g, cols],
-                    in_=w_grouped[:, g, :, :].rearrange("p c j -> p (c j)"),
-                )
-
-        bv_rows = const.tile([P, P], BF16)
-        nc.vector.memset(bv_rows[:], 0.0)
-        nc.sync.dma_start(out=bv_rows[0:E_BLOCKS, :], in_=bv.rearrange("(r c) -> r c", c=P))
-        bv_bank = prep_ps.tile([P, P], BF16, tag="prep")
-        nc.tensor.transpose(bv_bank[:], bv_rows[:], ident_bf[:])
-        bv_col = const.tile([P, E_BLOCKS], F32)
-        nc.vector.tensor_copy(out=bv_col[:], in_=bv_bank[:, 0:E_BLOCKS])
-        gamma_all = const.tile([P, E], BF16)
-        nc.sync.dma_start(out=gamma_all[:], in_=gamma.partition_broadcast(P))
-        betta_all = const.tile([P, E], BF16)
-        nc.sync.dma_start(out=betta_all[:], in_=betta.partition_broadcast(P))
-        one_half = const.tile([P, 1], F32)
-        nc.vector.memset(one_half[:], 0.5)
-        minus_one = const.tile([P, 1], F32)
-        nc.vector.memset(minus_one[:], -1.0)
-
-        steps[2]()
-        steps[3]()
-        for b in range(B):
-            operands = made
-            if b + 1 < B:
-                made, steps = preparation(load_batch(b + 1))
-            for i in range(S_BLOCKS):
-                attend(b, i, operands)
-                if b + 1 < B:
-                    steps[i]()
+            if t + 2 < heads:
+                scores(t + 2)
+            if 0 <= t + 1 < heads:
+                maximum(t + 1)
+            if inside:
+                exponent(t)
+            if t % 2 == 0 and 2 <= t <= heads:
+                flip(t // 2 - 1)
+            while to_empty:
+                empty_one()
+            if t % 2 == 0 and 2 <= t <= heads:
+                group(t // 2 - 1, "scalar")
+            g = t // NH
+            if local == 5 and inside:
+                quantise_e(g, 0)
+            if local == 1 and NH <= t < heads + NH:
+                quantise_e(g - 1, 1)
+            late = t - LAG
+            g, local = late // NH, late % NH
+            if local == 6 and 0 <= late < heads:
+                weigh(g, 0)
+            if local == 7 and 0 <= late < heads:
+                add_residual(g, 0)
+            if NH <= late:
+                if local == 0:
+                    statistics(g - 1, 0)
+                if local == 2:
+                    weigh(g - 1, 1)
+                if local == 3:
+                    add_residual(g - 1, 1)
+                if local == 4:
+                    statistics(g - 1, 1)
+                    norm(g - 1)
+            if inside:
+                due = 0
+                if b == 0:
+                    due = min(3 * (slot + 1), n_first)
+                    if due == n_first:
+                        due += max(0, (slot - n_first // 3) * n_batch // (SLOTS - 1 - n_first // 3))
+                elif b + 1 < B:
+                    due = n_first + b * n_batch + (slot + 1) * n_batch // (SLOTS - 1)
+                while emitted < due and items:
+                    emit(items.pop(0), "vector" if emitted < n_first and emitted % 2 else "scalar")
+                    emitted += 1

@@ -23,7 +23,9 @@ PASSES = E // K_PASS
 PAIR = 2 * P
 HALF_HEADS = NH // 2
 SCALE = 1.0 / DH**0.5
-NEG_RAW = -(2.0**36)
+LARGE = 3.0e38
+FLOOR = 2.0**-60
+NEG_KEY = -(2.0**100)
 EPS = 1e-08
 
 FLOPS = 2 * B * S * E * E + 2 * (2 * B * NH * S * S * DH)
@@ -64,8 +66,8 @@ def tile_multihead_attention_pa_kernel(
 
         def load_batch(b):
             return {
-                "keys": load_rows(keys[b], "keys_raw"),
                 "q": load_rows(q_relu[b], "q_raw"),
+                "keys": load_rows(keys[b], "keys_raw"),
                 "k": load_rows(k_relu[b], "k_raw"),
                 "x": load_rows(values[b], "x_raw"),
             }
@@ -84,6 +86,8 @@ def tile_multihead_attention_pa_kernel(
         bv_col = const.tile([P, E_BLOCKS], F32)
         gamma_all = const.tile([P, E], BF16)
         betta_all = const.tile([P, E], BF16)
+        ones_bf = const.tile([P, P], BF16)
+        nc.vector.memset(ones_bf[:], 1.0)
         one_half = const.tile([P, 1], F32)
         nc.vector.memset(one_half[:], 0.5)
         minus_one = const.tile([P, 1], F32)
@@ -111,23 +115,50 @@ def tile_multihead_attention_pa_kernel(
             )
             made["folded"] = fold_c
 
-        def finish_mask(made, rows_to_add):
-            key_sum = small.tile([P, S_BLOCKS], F32)
-            nc.vector.tensor_reduce(out=key_sum[:], in_=rows_to_add[:], axis=AXIS.X, op=ALU.add)
-            keep = small.tile([P, S_BLOCKS], F32)
-            nc.vector.tensor_single_scalar(out=keep[:], in_=key_sum[:], scalar=0.0, op=ALU.not_equal)
-            neg_c = small.tile([P, S_BLOCKS], F32)
+        def lift_queries(loads):
+            firsts = loads["q"][:, :, 0:E:DH]
+            nc.vector.tensor_scalar(out=firsts, in0=firsts, scalar1=FLOOR, scalar2=None, op0=ALU.max)
+
+        def add_keys(made, rows_to_add):
+            made["key_sum"] = small.tile([P, S_BLOCKS], F32, name="key_sum")
+            nc.vector.tensor_reduce(out=made["key_sum"][:], in_=rows_to_add[:], axis=AXIS.X, op=ALU.add)
+
+        def find_padded(made):
+            made["keep"] = small.tile([P, S_BLOCKS], F32, name="keep")
+            nc.vector.tensor_single_scalar(out=made["keep"][:], in_=made["key_sum"][:], scalar=0.0, op=ALU.not_equal)
+            made["sunk"] = small.tile([P, S_BLOCKS], F32, name="sunk")
             nc.vector.tensor_scalar(
-                out=neg_c[:], in0=key_sum[:], scalar1=0.0, scalar2=NEG_RAW, op0=ALU.is_equal, op1=ALU.mult
+                out=made["sunk"][:], in0=made["key_sum"][:], scalar1=0.0, scalar2=NEG_KEY,
+                op0=ALU.is_equal, op1=ALU.mult,
             )
-            keep_diag = batch.tile([P, S_BLOCKS, P], BF16)
+
+        def sink_padded(loads, made):
+            made["keep_bf"] = small.tile([P, S_BLOCKS], BF16, name="keep_bf")
+            nc.vector.tensor_copy(out=made["keep_bf"][:], in_=made["keep"][:])
             for j in range(S_BLOCKS):
+                firsts = loads["k"][:, j, 0:E:DH]
                 nc.vector.tensor_scalar(
-                    out=keep_diag[:, j, :], in0=ident_bf[:], scalar1=keep[:, j : j + 1], scalar2=None, op0=ALU.mult
+                    out=firsts, in0=firsts, scalar1=made["keep"][:, j : j + 1], scalar2=made["sunk"][:, j : j + 1],
+                    op0=ALU.mult, op1=ALU.add,
                 )
-            neg_rows = batch.tile([P, S_BLOCKS, P], F32)
-            nc.vector.tensor_copy(out=neg_rows[:], in_=neg_c[:].unsqueeze(2).to_broadcast([P, S_BLOCKS, P]))
-            made["keep_diag"], made["neg_rows"] = keep_diag, neg_rows
+
+        def mask_item(made):
+            def fill():
+                bank = prep_ps.tile([P, S_BLOCKS], F32, tag="prep", name="kept_bank")
+                nc.tensor.matmul(out=bank[:], lhsT=ones_bf[:], rhs=made["keep_bf"][:], start=True, stop=True)
+                return bank
+
+            def empty(bank, engine):
+                kept = small.tile([P, 1], F32, name="kept")
+                nc.vector.tensor_reduce(out=kept[:], in_=bank[:], axis=AXIS.X, op=ALU.max)
+                some = small.tile([P, 1], F32, name="some")
+                nc.vector.tensor_single_scalar(out=some[:], in_=kept[:], scalar=0.0, op=ALU.not_equal)
+                made["k_ident"] = batch.tile([P, P], BF16, name="k_ident")
+                nc.vector.tensor_scalar(
+                    out=made["k_ident"][:], in0=ident_bf[:], scalar1=some[:, 0:1], scalar2=None, op0=ALU.mult
+                )
+
+            return fill, empty, None
 
         def allocate(made):
             made["qT"] = batch.tile([P, NH, S], BF16, name="qT")
@@ -140,11 +171,13 @@ def tile_multihead_attention_pa_kernel(
 
         def heads_item(loads, made, which, first_head):
             def fill():
+                while which == "k" and "k_ident" not in made:
+                    empty_one()
                 bank = prep_ps.tile([P, 2, S], BF16, tag="prep", name="head_bank")
                 for a in range(2):
                     feats = slice((first_head + a) * DH, (first_head + a + 1) * DH)
                     for j in range(S_BLOCKS):
-                        identity = ident_bf[:] if which == "q" else made["keep_diag"][:, j, :]
+                        identity = ident_bf[:] if which == "q" else made["k_ident"][:]
                         nc.tensor.transpose(bank[:, a, j * P : (j + 1) * P], loads[which][:, j, feats], identity)
                 return bank
 
@@ -181,6 +214,7 @@ def tile_multihead_attention_pa_kernel(
 
         def project_item(made, m):
             def fill():
+                settle()
                 bank = prep_ps.tile([P, S], F32, tag="prep", name="v_bank")
                 for g in range(PASSES):
                     nc.tensor.matmul_mx(
@@ -303,11 +337,17 @@ def tile_multihead_attention_pa_kernel(
 
         to_empty = []
 
+        to_settle = []
+
+        def settle():
+            while to_settle:
+                to_settle.pop(0)()
+
         def empty_one():
             bank, empty, then, engine = to_empty.pop(0)
             empty(bank, engine)
             if then is not None:
-                then()
+                to_settle.append(then)
 
         def emit(item, engine):
             if len(to_empty) == 2:
@@ -315,12 +355,16 @@ def tile_multihead_attention_pa_kernel(
             fill, empty, then = item
             to_empty.append((fill(), empty, then, engine))
 
-        finish_mask(made, first_loads["keys"])
+        lift_queries(first_loads)
+        add_keys(made, first_loads["keys"])
+        find_padded(made)
+        sink_padded(first_loads, made)
         q_items, k_items, x_items, p_items, v_items = preparation(first_loads, made)
         emit(q_items[0], "scalar")
-        emit(k_items[0], "vector")
         emit(q_items[1], "scalar")
-        emit(k_items[1], "vector")
+        emit(mask_item(made), "vector")
+        emit(k_items[0], "vector")
+        emit(k_items[1], "scalar")
         empty_one()
         empty_one()
         first_items = [q_items[2], k_items[2], q_items[3], k_items[3]] + x_items + w_items() + [bias_item()] + p_items + v_items
@@ -349,24 +393,18 @@ def tile_multihead_attention_pa_kernel(
         def scores(t):
             d, h = block(t), t % NH
             m = operands[d["b"]]
-            score = score_ps.tile([P, S], F32, name="score")
+            score_of[t] = score_ps.tile([P, S], F32, name="score")
             nc.tensor.matmul(
-                out=score[:], lhsT=m["qT"][:, h, d["i"] * P : (d["i"] + 1) * P], rhs=m["kT"][:, h, :],
-                start=True, stop=False,
+                out=score_of[t][:], lhsT=m["qT"][:, h, d["i"] * P : (d["i"] + 1) * P], rhs=m["kT"][:, h, :],
+                start=True, stop=True,
             )
-            for j in range(S_BLOCKS):
-                nc.tensor.matmul(
-                    out=score[:, j * P : (j + 1) * P], lhsT=m["neg_rows"][:, j, :], rhs=ident_f32[:],
-                    start=False, stop=(j == S_BLOCKS - 1), is_transpose=True,
-                )
-            score_of[t] = score
 
         def maximum(t):
             d, h = block(t), t % NH
-            top = small.tile([P, 1], F32, name="top")
-            nc.vector.tensor_reduce(out=top[:], in_=score_of[t][:], axis=AXIS.X, op=ALU.max)
+            scaled = work.tile([P, S], F32, name="scaled")
             nc.vector.tensor_scalar(
-                out=d["neg_max"][:, h : h + 1], in0=top[:], scalar1=-SCALE, scalar2=None, op0=ALU.mult
+                out=scaled[:], in0=score_of[t][:], scalar1=-SCALE, scalar2=LARGE, op0=ALU.mult, op1=ALU.min,
+                accum_out=d["neg_max"][:, h : h + 1],
             )
 
         def exponent(t):
@@ -404,6 +442,11 @@ def tile_multihead_attention_pa_kernel(
                 in_=d["grouped"][half][:].rearrange("p c j -> p (c j)"),
             )
 
+        def invert(g):
+            d = block_of[g]
+            d["inv_sum"] = small.tile([P, NH], F32, name="inv_sum")
+            nc.vector.reciprocal(out=d["inv_sum"][:], in_=d["row_sum"][:])
+
         def weigh(g, half):
             d = block_of[g]
             m = operands[d["b"]]
@@ -425,13 +468,12 @@ def tile_multihead_attention_pa_kernel(
             if half == 0:
                 d["y"] = rows.tile([P, E], F32, name="y")
                 d["stats"] = small.tile([P, 2, 6], F32, name="stats")
-            inv_sum = small.tile([P, HALF_HEADS], F32, name="inv_sum")
-            nc.vector.reciprocal(out=inv_sum[:], in_=d["row_sum"][:, half * HALF_HEADS : (half + 1) * HALF_HEADS])
+            inv_sum = d["inv_sum"]
             for a in range(HALF_HEADS):
                 h = half * HALF_HEADS + a
                 feats = slice(h * DH, (h + 1) * DH)
                 nc.vector.scalar_tensor_tensor(
-                    out=d["y"][:, feats], in0=d["att"][:, a, :], scalar=inv_sum[:, a : a + 1],
+                    out=d["y"][:, feats], in0=d["att"][:, a, :], scalar=inv_sum[:, h : h + 1],
                     in1=d["resid"][:, feats], op0=ALU.mult, op1=ALU.add,
                 )
 
@@ -466,37 +508,53 @@ def tile_multihead_attention_pa_kernel(
             nc.gpsimd.tensor_tensor(out=y[:], in0=y[:], in1=betta_all[:], op=ALU.add)
             nc.sync.dma_start(out=out[d["b"], d["i"] * P : (d["i"] + 1) * P, :], in_=y[:])
 
+        def engine_of(n):
+            if n < n_first:
+                return "vector" if n % 2 else "scalar"
+            return "vector" if 13 <= (n - n_first) % n_batch < 17 else "scalar"
+
+        def mask_slot(b):
+            return 17 if b == 0 else 12
+
         SLOTS = S_BLOCKS * NH
         LAG = 8
         items, emitted = first_items, 0
-        n_first, n_batch = len(first_items), 2 * NH + E_BLOCKS
-        for t in range(-2, heads + LAG + 5):
+        n_first, n_batch = len(first_items), 2 * NH + E_BLOCKS + 1
+        for t in range(-3, heads + LAG + 6):
             inside = 0 <= t < heads
-            b, slot, local = t // SLOTS, t % SLOTS, t % NH
+            b, local = max(t, 0) // SLOTS, t % NH
+            slot = t - b * SLOTS
             if inside and slot == 0 and b + 1 < B:
                 nxt = {}
                 allocate(nxt)
                 operands.append(nxt)
-            if t == 4:
+            if t == 2:
                 next_loads = load_batch(1)
             if inside and slot == (8 if b == 0 else 0) and b + 1 < B:
                 q_items, k_items, x_items, p_items, v_items = preparation(next_loads, nxt)
-                items = items + q_items + x_items + k_items + p_items + v_items
+                items = items + q_items + x_items + p_items[:4] + [mask_item(nxt)]
+                items += k_items + p_items[4:] + v_items
+                lift_queries(next_loads)
                 make_mask(next_loads, nxt)
-            if inside and slot == (17 if b == 0 else 9) and b + 1 < B:
-                finish_mask(nxt, nxt["folded"])
-            if inside and slot == 23 and b + 2 < B:
+            if inside and slot == mask_slot(b) and b + 1 < B:
+                add_keys(nxt, nxt["folded"])
+            if inside and slot == mask_slot(b) + 1 and b + 1 < B:
+                find_padded(nxt)
+            if inside and slot == mask_slot(b) + 2 and b + 1 < B:
+                sink_padded(next_loads, nxt)
+            if inside and slot == 26 and b + 2 < B:
                 next_loads = load_batch(b + 2)
-            if t == -2:
+            if t == -3:
                 load_residual(0)
                 load_residual(1)
             if inside and local == 0 and t // NH + 2 < B * S_BLOCKS:
                 load_residual(t // NH + 2)
 
-            if t + 2 < heads:
-                scores(t + 2)
-            if 0 <= t + 1 < heads:
-                maximum(t + 1)
+            if t + 3 < heads:
+                scores(t + 3)
+            if 0 <= t + 2 < heads:
+                maximum(t + 2)
+            settle()
             if inside:
                 exponent(t)
             if t % 2 == 0 and 2 <= t <= heads:
@@ -506,12 +564,14 @@ def tile_multihead_attention_pa_kernel(
             if t % 2 == 0 and 2 <= t <= heads:
                 group(t // 2 - 1, "scalar")
             g = t // NH
-            if local == 5 and inside:
+            if local == 7 and inside:
                 quantise_e(g, 0)
-            if local == 1 and NH <= t < heads + NH:
+            if local == 3 and NH <= t < heads + NH:
                 quantise_e(g - 1, 1)
             late = t - LAG
             g, local = late // NH, late % NH
+            if local == 5 and 0 <= late < heads:
+                invert(g)
             if local == 6 and 0 <= late < heads:
                 weigh(g, 0)
             if local == 7 and 0 <= late < heads:
@@ -525,15 +585,14 @@ def tile_multihead_attention_pa_kernel(
                     add_residual(g - 1, 1)
                 if local == 4:
                     statistics(g - 1, 1)
+                if local == 5:
                     norm(g - 1)
-            if inside:
+            if -2 <= t < heads:
                 due = 0
                 if b == 0:
-                    due = min(3 * (slot + 1), n_first)
-                    if due == n_first:
-                        due += max(0, (slot - n_first // 3) * n_batch // (SLOTS - 1 - n_first // 3))
+                    due = min(3 * (slot + 3), n_first) + max(0, (slot - 8) * n_batch // (SLOTS - 9))
                 elif b + 1 < B:
                     due = n_first + b * n_batch + (slot + 1) * n_batch // (SLOTS - 1)
                 while emitted < due and items:
-                    emit(items.pop(0), "vector" if emitted < n_first and emitted % 2 else "scalar")
+                    emit(items.pop(0), engine_of(emitted))
                     emitted += 1

@@ -19,10 +19,13 @@ PACK = 4
 K_PASS = P * PACK
 S_BLOCKS = S // P
 E_BLOCKS = E // P
+N_BLOCKS = B * S_BLOCKS
+V_BLOCKS = 2
 PASSES = E // K_PASS
 PAIR = 2 * P
 HALF_HEADS = NH // 2
 SCALE = 1.0 / DH**0.5
+GP_COLS = 512
 LARGE = 3.0e38
 FLOOR = 2.0**-60
 NEG_KEY = -(2.0**100)
@@ -51,7 +54,7 @@ def tile_multihead_attention_pa_kernel(
         stage = ctx.enter_context(tc.tile_pool(name="stage", bufs=1))
         batch = ctx.enter_context(tc.tile_pool(name="batch", bufs=2))
         work = ctx.enter_context(tc.tile_pool(name="work", bufs=3))
-        halves = ctx.enter_context(tc.tile_pool(name="halves", bufs=4))
+        halves = ctx.enter_context(tc.tile_pool(name="halves", bufs=2))
         rows = ctx.enter_context(tc.tile_pool(name="rows", bufs=3))
         small = ctx.enter_context(tc.tile_pool(name="small", bufs=6))
         prep_ps = ctx.enter_context(tc.psum_pool(name="prep_ps", bufs=2))
@@ -93,6 +96,9 @@ def tile_multihead_attention_pa_kernel(
         minus_one = const.tile([P, 1], F32)
         nc.vector.memset(minus_one[:], -1.0)
 
+        warm = const.tile([P, 1], F32)
+        nc.scalar.activation(out=warm[:], in_=one_half[:], func=ACT.Exp)
+
         def copy_on(engine, out, in_):
             if engine == "scalar":
                 nc.scalar.copy(out=out, in_=in_)
@@ -102,17 +108,14 @@ def tile_multihead_attention_pa_kernel(
         def make_mask(loads, made):
             keys_raw = loads["keys"]
             fold_a = stage.tile([P, S_BLOCKS, E // 2], F32)
-            nc.gpsimd.tensor_tensor(
-                out=fold_a[:], in0=keys_raw[:, :, 0 : E // 2], in1=keys_raw[:, :, E // 2 : E], op=ALU.add
-            )
             fold_b = stage.tile([P, S_BLOCKS, E // 4], F32)
-            nc.gpsimd.tensor_tensor(
-                out=fold_b[:], in0=fold_a[:, :, 0 : E // 4], in1=fold_a[:, :, E // 4 : E // 2], op=ALU.add
-            )
             fold_c = stage.tile([P, S_BLOCKS, E // 8], F32)
-            nc.gpsimd.tensor_tensor(
-                out=fold_c[:], in0=fold_b[:, :, 0 : E // 8], in1=fold_b[:, :, E // 8 : E // 4], op=ALU.add
-            )
+            for source, folded in ((keys_raw, fold_a), (fold_a, fold_b), (fold_b, fold_c)):
+                half = folded.shape[-1]
+                for j in range(S_BLOCKS):
+                    nc.gpsimd.tensor_tensor(
+                        out=folded[:, j, :], in0=source[:, j, 0:half], in1=source[:, j, half : 2 * half], op=ALU.add
+                    )
             made["folded"] = fold_c
 
         def lift_queries(loads):
@@ -131,10 +134,10 @@ def tile_multihead_attention_pa_kernel(
                 out=made["sunk"][:], in0=made["key_sum"][:], scalar1=0.0, scalar2=NEG_KEY,
                 op0=ALU.is_equal, op1=ALU.mult,
             )
+            made["keep_bf"] = small.tile([P, S_BLOCKS], BF16, name="keep_bf")
+            nc.vector.tensor_single_scalar(out=made["keep_bf"][:], in_=made["key_sum"][:], scalar=0.0, op=ALU.not_equal)
 
         def sink_padded(loads, made):
-            made["keep_bf"] = small.tile([P, S_BLOCKS], BF16, name="keep_bf")
-            nc.vector.tensor_copy(out=made["keep_bf"][:], in_=made["keep"][:])
             for j in range(S_BLOCKS):
                 firsts = loads["k"][:, j, 0:E:DH]
                 nc.vector.tensor_scalar(
@@ -142,20 +145,24 @@ def tile_multihead_attention_pa_kernel(
                     op0=ALU.mult, op1=ALU.add,
                 )
 
-        def mask_item(made):
+        def scale_item(made):
             def fill():
-                bank = prep_ps.tile([P, S_BLOCKS], F32, tag="prep", name="kept_bank")
-                nc.tensor.matmul(out=bank[:], lhsT=ones_bf[:], rhs=made["keep_bf"][:], start=True, stop=True)
+                bank = prep_ps.tile([P, 1], F32, tag="prep", name="kept_bank")
+                for j in range(S_BLOCKS):
+                    nc.tensor.matmul(
+                        out=bank[:], lhsT=ones_bf[:], rhs=made["keep_bf"][:, j : j + 1],
+                        start=(j == 0), stop=(j == S_BLOCKS - 1),
+                    )
                 return bank
 
             def empty(bank, engine):
-                kept = small.tile([P, 1], F32, name="kept")
-                nc.vector.tensor_reduce(out=kept[:], in_=bank[:], axis=AXIS.X, op=ALU.max)
-                some = small.tile([P, 1], F32, name="some")
-                nc.vector.tensor_single_scalar(out=some[:], in_=kept[:], scalar=0.0, op=ALU.not_equal)
-                made["k_ident"] = batch.tile([P, P], BF16, name="k_ident")
+                made["scale"] = batch.tile([P, 1], F32, name="scale")
                 nc.vector.tensor_scalar(
-                    out=made["k_ident"][:], in0=ident_bf[:], scalar1=some[:, 0:1], scalar2=None, op0=ALU.mult
+                    out=made["scale"][:], in0=bank[:], scalar1=0.0, scalar2=SCALE, op0=ALU.not_equal, op1=ALU.mult
+                )
+                made["minus_scale"] = batch.tile([P, 1], F32, name="minus_scale")
+                nc.vector.tensor_scalar(
+                    out=made["minus_scale"][:], in0=bank[:], scalar1=0.0, scalar2=-SCALE, op0=ALU.not_equal, op1=ALU.mult
                 )
 
             return fill, empty, None
@@ -171,14 +178,11 @@ def tile_multihead_attention_pa_kernel(
 
         def heads_item(loads, made, which, first_head):
             def fill():
-                while which == "k" and "k_ident" not in made:
-                    empty_one()
                 bank = prep_ps.tile([P, 2, S], BF16, tag="prep", name="head_bank")
                 for a in range(2):
                     feats = slice((first_head + a) * DH, (first_head + a + 1) * DH)
                     for j in range(S_BLOCKS):
-                        identity = ident_bf[:] if which == "q" else made["k_ident"][:]
-                        nc.tensor.transpose(bank[:, a, j * P : (j + 1) * P], loads[which][:, j, feats], identity)
+                        nc.tensor.transpose(bank[:, a, j * P : (j + 1) * P], loads[which][:, j, feats], ident_bf[:])
                 return bank
 
             def empty(bank, engine):
@@ -356,21 +360,30 @@ def tile_multihead_attention_pa_kernel(
             to_empty.append((fill(), empty, then, engine))
 
         lift_queries(first_loads)
-        add_keys(made, first_loads["keys"])
+        made["key_sum"] = const.tile([P, S_BLOCKS], F32, name="first_key_sum")
+        nc.vector.tensor_reduce(
+            out=made["key_sum"][:, 0:2], in_=first_loads["keys"][:, 0:2, :], axis=AXIS.X, op=ALU.add
+        )
+        for j in range(2, S_BLOCKS):
+            summed = stage.tile([P, E], BF16, bufs=2, name="summed")
+            nc.scalar.activation(
+                out=summed[:], in_=first_loads["keys"][:, j, :], func=ACT.Identity, bias=0.0, scale=1.0,
+                accum_out=made["key_sum"][:, j : j + 1],
+            )
         find_padded(made)
         sink_padded(first_loads, made)
         q_items, k_items, x_items, p_items, v_items = preparation(first_loads, made)
         emit(q_items[0], "scalar")
-        emit(q_items[1], "scalar")
-        emit(mask_item(made), "vector")
         emit(k_items[0], "vector")
+        emit(scale_item(made), "vector")
+        emit(q_items[1], "scalar")
         emit(k_items[1], "scalar")
         empty_one()
         empty_one()
         first_items = [q_items[2], k_items[2], q_items[3], k_items[3]] + x_items + w_items() + [bias_item()] + p_items + v_items
 
         operands = [made]
-        heads = B * S_BLOCKS * NH
+        heads = N_BLOCKS * NH
         score_of, e_of, flip_of = {}, {}, {}
         block_of = {}
 
@@ -379,7 +392,7 @@ def tile_multihead_attention_pa_kernel(
             if g not in block_of:
                 b, i = g // S_BLOCKS, g % S_BLOCKS
                 block_of[g] = {
-                    "b": b, "i": i, "grouped": {},
+                    "b": b, "i": i,
                     "neg_max": small.tile([P, NH], F32, name="neg_max"),
                     "row_sum": small.tile([P, NH], F32, name="row_sum"),
                 }
@@ -403,7 +416,7 @@ def tile_multihead_attention_pa_kernel(
             d, h = block(t), t % NH
             scaled = work.tile([P, S], F32, name="scaled")
             nc.vector.tensor_scalar(
-                out=scaled[:], in0=score_of[t][:], scalar1=-SCALE, scalar2=LARGE, op0=ALU.mult, op1=ALU.min,
+                out=scaled[:], in0=score_of[t][:], scalar1=operands[d["b"]]["minus_scale"][:, 0:1], scalar2=LARGE, op0=ALU.mult, op1=ALU.min,
                 accum_out=d["neg_max"][:, h : h + 1],
             )
 
@@ -413,7 +426,7 @@ def tile_multihead_attention_pa_kernel(
                 e_of[t // 2] = work.tile([P, 2, S], BF16, name="e")
             nc.scalar.activation(
                 out=e_of[t // 2][:, t % 2, :], in_=score_of[t][:], func=ACT.Exp,
-                bias=d["neg_max"][:, h : h + 1], scale=SCALE, accum_out=d["row_sum"][:, h : h + 1],
+                bias=d["neg_max"][:, h : h + 1], scale=operands[d["b"]]["scale"][:, 0:1], accum_out=d["row_sum"][:, h : h + 1],
             )
 
         def flip(pair):
@@ -423,23 +436,25 @@ def tile_multihead_attention_pa_kernel(
 
         def group(pair, engine):
             d = block(2 * pair)
-            half, at = (2 * pair) % NH // HALF_HEADS, pair % 2
+            at = pair % (NH // 2)
             if at == 0:
-                d["grouped"][half] = halves.tile([P, HALF_HEADS * P, PACK], BF16, align_bytes=64, name="e_grouped")
+                d["grouped"] = halves.tile([P, NH * P, PACK], BF16, align_bytes=64, name="e_grouped")
             copy_on(
                 engine,
-                d["grouped"][half][:, at * PAIR : (at + 1) * PAIR, :].bitcast(F32),
+                d["grouped"][:, at * PAIR : (at + 1) * PAIR, :].bitcast(F32),
                 flip_of[pair][:].rearrange("p u c -> p c u"),
             )
 
-        def quantise_e(g, half):
+        def quantise_e(g, first, last):
             d = block_of[g]
-            d["codes", half] = halves.tile([P, HALF_HEADS * P], U32, align_bytes=64, name="e_codes")
-            d["scales", half] = halves.tile([P, HALF_HEADS * P], U8, align_bytes=64, name="e_scales")
+            if first == 0:
+                d["codes"] = halves.tile([P, NH * P], U32, align_bytes=64, name="e_codes")
+                d["scales"] = halves.tile([P, NH * P], U8, align_bytes=64, name="e_scales")
+            cols = slice(first * P, last * P)
             nc.vector.quantize_mx(
-                out=d["codes", half][:].bitcast(FP8X4),
-                scales=d["scales", half][:],
-                in_=d["grouped"][half][:].rearrange("p c j -> p (c j)"),
+                out=d["codes"][:, cols].bitcast(FP8X4),
+                scales=d["scales"][:, cols],
+                in_=d["grouped"][:, cols, :].rearrange("p c j -> p (c j)"),
             )
 
         def invert(g):
@@ -455,8 +470,8 @@ def tile_multihead_attention_pa_kernel(
                 h = half * HALF_HEADS + a
                 nc.tensor.matmul_mx(
                     out=d["att"][:, a, :],
-                    lhsT=d["codes", half][:, a * P : (a + 1) * P].bitcast(FP8X4),
-                    lhsT_scale=d["scales", half][:, a * P : (a + 1) * P],
+                    lhsT=d["codes"][:, h * P : (h + 1) * P].bitcast(FP8X4),
+                    lhsT_scale=d["scales"][:, h * P : (h + 1) * P],
                     rhs=m["v_codes"][:, h * DH : (h + 1) * DH].bitcast(FP8X4),
                     rhs_scale=m["v_scales"][:, h * DH : (h + 1) * DH],
                     start=True,
@@ -466,7 +481,7 @@ def tile_multihead_attention_pa_kernel(
         def add_residual(g, half):
             d = block_of[g]
             if half == 0:
-                d["y"] = rows.tile([P, E], F32, name="y")
+                d["y"] = rows.tile([P, E], F32, bufs=4, name="y")
                 d["stats"] = small.tile([P, 2, 6], F32, name="stats")
             inv_sum = d["inv_sum"]
             for a in range(HALF_HEADS):
@@ -501,12 +516,39 @@ def tile_multihead_attention_pa_kernel(
             nc.gpsimd.tensor_scalar(out=sd_eps[:], in0=sd[:], scalar1=EPS, scalar2=1.0, op0=ALU.add, op1=ALU.mult)
             inv_sd = small.tile([P, 1], F32, name="inv_sd")
             nc.gpsimd.tensor_tensor(out=inv_sd[:], in0=sd_eps[:], in1=minus_one[:], op=ALU.pow)
-            nc.gpsimd.tensor_scalar(
-                out=y[:], in0=y[:], scalar1=neg_mean[:, 0:1], scalar2=inv_sd[:, 0:1], op0=ALU.add, op1=ALU.mult
-            )
-            nc.gpsimd.tensor_tensor(out=y[:], in0=y[:], in1=gamma_all[:], op=ALU.mult)
-            nc.gpsimd.tensor_tensor(out=y[:], in0=y[:], in1=betta_all[:], op=ALU.add)
-            nc.sync.dma_start(out=out[d["b"], d["i"] * P : (d["i"] + 1) * P, :], in_=y[:])
+            d["moments"], d["inv_sd"] = moments, inv_sd
+            if g >= N_BLOCKS - V_BLOCKS:
+                return
+            pieces = [slice(first, first + GP_COLS) for first in range(0, E, GP_COLS)]
+            for cols in pieces:
+                nc.gpsimd.tensor_scalar(
+                    out=y[:, cols], in0=y[:, cols], scalar1=neg_mean[:, 0:1], scalar2=inv_sd[:, 0:1],
+                    op0=ALU.add, op1=ALU.mult,
+                )
+            for cols in pieces:
+                nc.gpsimd.tensor_tensor(out=y[:, cols], in0=y[:, cols], in1=gamma_all[:, cols], op=ALU.mult)
+            for cols in pieces:
+                nc.gpsimd.tensor_tensor(out=y[:, cols], in0=y[:, cols], in1=betta_all[:, cols], op=ALU.add)
+
+        def norm_on_vector(g):
+            d = block_of[g]
+            y = d["y"]
+            halves_of = [slice(half * (E // 2), (half + 1) * (E // 2)) for half in range(2)]
+            for cols in halves_of:
+                nc.vector.scalar_tensor_tensor(
+                    out=y[:, cols], in0=y[:, cols], scalar=d["moments"][:, 0:1], in1=gamma_all[:, cols],
+                    op0=ALU.subtract, op1=ALU.mult,
+                )
+            for cols in halves_of:
+                nc.vector.scalar_tensor_tensor(
+                    out=y[:, cols], in0=y[:, cols], scalar=d["inv_sd"][:, 0:1], in1=betta_all[:, cols],
+                    op0=ALU.mult, op1=ALU.add,
+                )
+                nc.sync.dma_start(out=out[d["b"], d["i"] * P : (d["i"] + 1) * P, cols], in_=y[:, cols])
+
+        def store(g):
+            d = block_of[g]
+            nc.sync.dma_start(out=out[d["b"], d["i"] * P : (d["i"] + 1) * P, :], in_=d["y"][:])
 
         def engine_of(n):
             if n < n_first:
@@ -517,10 +559,24 @@ def tile_multihead_attention_pa_kernel(
             return 17 if b == 0 else 12
 
         SLOTS = S_BLOCKS * NH
-        LAG = 8
+        stages = {}
+        for g in range(N_BLOCKS):
+            plan = [(11, invert, (g,)), (11, quantise_e, (g, 0, NH))]
+            if g == N_BLOCKS - 1:
+                plan = [(7, quantise_e, (g, 0, HALF_HEADS)), (11, invert, (g,)), (11, quantise_e, (g, HALF_HEADS, NH))]
+            for half in range(2):
+                first = 12 + 2 * half
+                plan += [(first, weigh, (g, half)), (first + 1, add_residual, (g, half)), (first + 2, statistics, (g, half))]
+            plan.append((17, norm, (g,)))
+            if g < N_BLOCKS - V_BLOCKS:
+                plan.append((29, store, (g,)))
+            else:
+                plan.append(((N_BLOCKS - 1 - g) * NH + 17, norm_on_vector, (g,)))
+            for after, stage_of, of in plan:
+                stages.setdefault(g * NH + after, []).append((stage_of, of))
         items, emitted = first_items, 0
         n_first, n_batch = len(first_items), 2 * NH + E_BLOCKS + 1
-        for t in range(-3, heads + LAG + 6):
+        for t in range(-3, heads + 3 * NH):
             inside = 0 <= t < heads
             b, local = max(t, 0) // SLOTS, t % NH
             slot = t - b * SLOTS
@@ -532,7 +588,7 @@ def tile_multihead_attention_pa_kernel(
                 next_loads = load_batch(1)
             if inside and slot == (8 if b == 0 else 0) and b + 1 < B:
                 q_items, k_items, x_items, p_items, v_items = preparation(next_loads, nxt)
-                items = items + q_items + x_items + p_items[:4] + [mask_item(nxt)]
+                items = items + q_items + x_items + p_items[:4] + [scale_item(nxt)]
                 items += k_items + p_items[4:] + v_items
                 lift_queries(next_loads)
                 make_mask(next_loads, nxt)
@@ -547,7 +603,7 @@ def tile_multihead_attention_pa_kernel(
             if t == -3:
                 load_residual(0)
                 load_residual(1)
-            if inside and local == 0 and t // NH + 2 < B * S_BLOCKS:
+            if inside and local == 0 and t // NH + 2 < N_BLOCKS:
                 load_residual(t // NH + 2)
 
             if t + 3 < heads:
@@ -561,32 +617,10 @@ def tile_multihead_attention_pa_kernel(
                 flip(t // 2 - 1)
             while to_empty:
                 empty_one()
-            if t % 2 == 0 and 2 <= t <= heads:
+            if t % 2 == 1 and 3 <= t <= heads + 1:
                 group(t // 2 - 1, "scalar")
-            g = t // NH
-            if local == 7 and inside:
-                quantise_e(g, 0)
-            if local == 3 and NH <= t < heads + NH:
-                quantise_e(g - 1, 1)
-            late = t - LAG
-            g, local = late // NH, late % NH
-            if local == 5 and 0 <= late < heads:
-                invert(g)
-            if local == 6 and 0 <= late < heads:
-                weigh(g, 0)
-            if local == 7 and 0 <= late < heads:
-                add_residual(g, 0)
-            if NH <= late:
-                if local == 0:
-                    statistics(g - 1, 0)
-                if local == 2:
-                    weigh(g - 1, 1)
-                if local == 3:
-                    add_residual(g - 1, 1)
-                if local == 4:
-                    statistics(g - 1, 1)
-                if local == 5:
-                    norm(g - 1)
+            for stage_of, of in stages.get(t, []):
+                stage_of(*of)
             if -2 <= t < heads:
                 due = 0
                 if b == 0:

@@ -384,6 +384,7 @@ def tile_multihead_attention_pa_kernel(
 
         operands = [made]
         heads = N_BLOCKS * NH
+        FIRST_BUSY = 14
         score_of, e_of, flip_of = {}, {}, {}
         block_of = {}
 
@@ -407,6 +408,16 @@ def tile_multihead_attention_pa_kernel(
             d, h = block(t), t % NH
             m = operands[d["b"]]
             score_of[t] = score_ps.tile([P, S], F32, name="score")
+            if t >= FIRST_BUSY:
+                nc.tensor.matmul_mx(
+                    out=score_of[t][:],
+                    lhsT=w_codes[:, 0, 0:P].bitcast(FP8X4),
+                    lhsT_scale=w_scales[:, 0, 0:P],
+                    rhs=w_codes[:, 1, 0:S].bitcast(FP8X4),
+                    rhs_scale=w_scales[:, 1, 0:S],
+                    start=True,
+                    stop=True,
+                )
             nc.tensor.matmul(
                 out=score_of[t][:], lhsT=m["qT"][:, h, d["i"] * P : (d["i"] + 1) * P], rhs=m["kT"][:, h, :],
                 start=True, stop=True,

@@ -384,6 +384,7 @@ def tile_multihead_attention_pa_kernel(
 
         operands = [made]
         heads = N_BLOCKS * NH
+        SLOTS = S_BLOCKS * NH
         FIRST_BUSY = 14
         score_of, e_of, flip_of = {}, {}, {}
         block_of = {}
@@ -409,12 +410,13 @@ def tile_multihead_attention_pa_kernel(
             m = operands[d["b"]]
             score_of[t] = score_ps.tile([P, S], F32, name="score")
             if t >= FIRST_BUSY:
+                width = S if t < SLOTS // 2 else S // 2
                 nc.tensor.matmul_mx(
-                    out=score_of[t][:],
+                    out=score_of[t][:, 0:width],
                     lhsT=w_codes[:, 0, 0:P].bitcast(FP8X4),
                     lhsT_scale=w_scales[:, 0, 0:P],
-                    rhs=w_codes[:, 1, 0:S].bitcast(FP8X4),
-                    rhs_scale=w_scales[:, 1, 0:S],
+                    rhs=w_codes[:, 1, 0:width].bitcast(FP8X4),
+                    rhs_scale=w_scales[:, 1, 0:width],
                     start=True,
                     stop=True,
                 )
@@ -569,7 +571,6 @@ def tile_multihead_attention_pa_kernel(
         def mask_slot(b):
             return 17 if b == 0 else 12
 
-        SLOTS = S_BLOCKS * NH
         stages = {}
         for g in range(N_BLOCKS):
             plan = [(11, invert, (g,)), (11, quantise_e, (g, 0, NH))]

@@ -28,6 +28,7 @@ SCALE = 1.0 / DH**0.5
 GP_COLS = 512
 LARGE = 3.0e38
 FLOOR = 2.0**-60
+HEAD_HALF = (slice(0, E // 2), slice(E // 2, E))
 NEG_KEY = -(2.0**100)
 EPS = 1e-08
 
@@ -67,6 +68,24 @@ def tile_multihead_attention_pa_kernel(
             nc.sync.dma_start(out=loaded[:], in_=source.rearrange("(j p) e -> p j e", p=P))
             return loaded
 
+        def load_first_batch():
+            loaded = {
+                which: raw.tile([P, S_BLOCKS, E], BF16, name=which + "_raw") for which in ("q", "keys", "k", "x")
+            }
+            rows_of = {
+                which: source[0].rearrange("(j p) e -> p j e", p=P)
+                for which, source in (("q", q_relu), ("keys", keys), ("k", k_relu), ("x", values))
+            }
+            half = S_BLOCKS // 2
+            nc.sync.dma_start(out=loaded["q"][:, :, HEAD_HALF[0]], in_=rows_of["q"][:, :, HEAD_HALF[0]])
+            nc.sync.dma_start(out=loaded["keys"][:, 0:half, :], in_=rows_of["keys"][:, 0:half, :])
+            nc.sync.dma_start(out=loaded["keys"][:, half:, :], in_=rows_of["keys"][:, half:, :])
+            nc.sync.dma_start(out=loaded["k"][:, :, HEAD_HALF[0]], in_=rows_of["k"][:, :, HEAD_HALF[0]])
+            nc.sync.dma_start(out=loaded["q"][:, :, HEAD_HALF[1]], in_=rows_of["q"][:, :, HEAD_HALF[1]])
+            nc.sync.dma_start(out=loaded["k"][:, :, HEAD_HALF[1]], in_=rows_of["k"][:, :, HEAD_HALF[1]])
+            nc.sync.dma_start(out=loaded["x"][:], in_=rows_of["x"])
+            return loaded
+
         def load_batch(b):
             return {
                 "q": load_rows(q_relu[b], "q_raw"),
@@ -75,12 +94,12 @@ def tile_multihead_attention_pa_kernel(
                 "x": load_rows(values[b], "x_raw"),
             }
 
-        first_loads = load_batch(0)
+        first_loads = load_first_batch()
 
         ident_bf = const.tile([P, P], BF16)
         make_identity(nc, ident_bf[:])
         ident_f32 = const.tile([P, P], F32)
-        make_identity(nc, ident_f32[:])
+        nc.vector.tensor_copy(out=ident_f32[:], in_=ident_bf[:])
 
         ctx.enter_context(tc.manual_schedule())
 
@@ -118,8 +137,8 @@ def tile_multihead_attention_pa_kernel(
                     )
             made["folded"] = fold_c
 
-        def lift_queries(loads):
-            firsts = loads["q"][:, :, 0:E:DH]
+        def lift_queries(loads, feats=slice(0, E)):
+            firsts = loads["q"][:, :, feats.start : feats.stop : DH]
             nc.vector.tensor_scalar(out=firsts, in0=firsts, scalar1=FLOOR, scalar2=None, op0=ALU.max)
 
         def add_keys(made, rows_to_add):
@@ -137,9 +156,9 @@ def tile_multihead_attention_pa_kernel(
             made["keep_bf"] = small.tile([P, S_BLOCKS], BF16, name="keep_bf")
             nc.vector.tensor_single_scalar(out=made["keep_bf"][:], in_=made["key_sum"][:], scalar=0.0, op=ALU.not_equal)
 
-        def sink_padded(loads, made):
+        def sink_padded(loads, made, feats=slice(0, E)):
             for j in range(S_BLOCKS):
-                firsts = loads["k"][:, j, 0:E:DH]
+                firsts = loads["k"][:, j, feats.start : feats.stop : DH]
                 nc.vector.tensor_scalar(
                     out=firsts, in0=firsts, scalar1=made["keep"][:, j : j + 1], scalar2=made["sunk"][:, j : j + 1],
                     op0=ALU.mult, op1=ALU.add,
@@ -359,7 +378,7 @@ def tile_multihead_attention_pa_kernel(
             fill, empty, then = item
             to_empty.append((fill(), empty, then, engine))
 
-        lift_queries(first_loads)
+        lift_queries(first_loads, HEAD_HALF[0])
         made["key_sum"] = const.tile([P, S_BLOCKS], F32, name="first_key_sum")
         nc.vector.tensor_reduce(
             out=made["key_sum"][:, 0:2], in_=first_loads["keys"][:, 0:2, :], axis=AXIS.X, op=ALU.add
@@ -371,7 +390,7 @@ def tile_multihead_attention_pa_kernel(
                 accum_out=made["key_sum"][:, j : j + 1],
             )
         find_padded(made)
-        sink_padded(first_loads, made)
+        sink_padded(first_loads, made, HEAD_HALF[0])
         q_items, k_items, x_items, p_items, v_items = preparation(first_loads, made)
         emit(q_items[0], "scalar")
         emit(k_items[0], "vector")
@@ -380,6 +399,8 @@ def tile_multihead_attention_pa_kernel(
         emit(k_items[1], "scalar")
         empty_one()
         empty_one()
+        lift_queries(first_loads, HEAD_HALF[1])
+        sink_padded(first_loads, made, HEAD_HALF[1])
         first_items = [q_items[2], k_items[2], q_items[3], k_items[3]] + x_items + w_items() + [bias_item()] + p_items + v_items
 
         operands = [made]
@@ -515,6 +536,9 @@ def tile_multihead_attention_pa_kernel(
             y = d["y"]
             moments = small.tile([P, 2], F32, name="moments")
             nc.vector.bn_aggr(out=moments[:], in_=d["stats"][:])
+            d["moments"] = moments
+            if g >= N_BLOCKS - V_BLOCKS:
+                return
             neg_mean = small.tile([P, 1], F32, name="neg_mean")
             nc.gpsimd.tensor_scalar(
                 out=neg_mean[:], in0=moments[:, 0:1], scalar1=-1.0, scalar2=0.0, op0=ALU.mult, op1=ALU.add
@@ -529,9 +553,6 @@ def tile_multihead_attention_pa_kernel(
             nc.gpsimd.tensor_scalar(out=sd_eps[:], in0=sd[:], scalar1=EPS, scalar2=1.0, op0=ALU.add, op1=ALU.mult)
             inv_sd = small.tile([P, 1], F32, name="inv_sd")
             nc.gpsimd.tensor_tensor(out=inv_sd[:], in0=sd_eps[:], in1=minus_one[:], op=ALU.pow)
-            d["moments"], d["inv_sd"] = moments, inv_sd
-            if g >= N_BLOCKS - V_BLOCKS:
-                return
             pieces = [slice(first, first + GP_COLS) for first in range(0, E, GP_COLS)]
             for cols in pieces:
                 nc.gpsimd.tensor_scalar(
@@ -543,15 +564,26 @@ def tile_multihead_attention_pa_kernel(
             for cols in pieces:
                 nc.gpsimd.tensor_tensor(out=y[:, cols], in0=y[:, cols], in1=betta_all[:, cols], op=ALU.add)
 
+        def root(g):
+            d = block_of[g]
+            d["sd"] = small.tile([P, 1], F32, name="sd")
+            nc.scalar.activation(
+                out=d["sd"][:], in_=d["moments"][:, 1:2], func=ACT.Sqrt, bias=0.0, scale=E / (E - 1.0)
+            )
+
         def norm_on_vector(g):
             d = block_of[g]
             y = d["y"]
+            sd_eps = small.tile([P, 1], F32, name="sd_eps")
+            nc.vector.tensor_scalar(out=sd_eps[:], in0=d["sd"][:], scalar1=EPS, scalar2=None, op0=ALU.add)
             halves_of = [slice(half * (E // 2), (half + 1) * (E // 2)) for half in range(2)]
             for cols in halves_of:
                 nc.vector.scalar_tensor_tensor(
                     out=y[:, cols], in0=y[:, cols], scalar=d["moments"][:, 0:1], in1=gamma_all[:, cols],
                     op0=ALU.subtract, op1=ALU.mult,
                 )
+            d["inv_sd"] = small.tile([P, 1], F32, name="inv_sd")
+            nc.vector.reciprocal(out=d["inv_sd"][:], in_=sd_eps[:])
             for cols in halves_of:
                 nc.vector.scalar_tensor_tensor(
                     out=y[:, cols], in0=y[:, cols], scalar=d["inv_sd"][:, 0:1], in1=betta_all[:, cols],
@@ -583,7 +615,8 @@ def tile_multihead_attention_pa_kernel(
             if g < N_BLOCKS - V_BLOCKS:
                 plan.append((29, store, (g,)))
             else:
-                plan.append(((N_BLOCKS - 1 - g) * NH + 17, norm_on_vector, (g,)))
+                plan.append(((N_BLOCKS - 1 - g) * NH + 18, root, (g,)))
+                plan.append(((N_BLOCKS - 1 - g) * NH + 19, norm_on_vector, (g,)))
             for after, stage_of, of in plan:
                 stages.setdefault(g * NH + after, []).append((stage_of, of))
         items, emitted = first_items, 0

@@ -20,7 +20,7 @@ K_PASS = P * PACK
 S_BLOCKS = S // P
 E_BLOCKS = E // P
 N_BLOCKS = B * S_BLOCKS
-V_BLOCKS = 2
+V_BLOCKS = 3
 PASSES = E // K_PASS
 PAIR = 2 * P
 HALF_HEADS = NH // 2
@@ -64,13 +64,13 @@ def tile_multihead_attention_pa_kernel(
         att_ps = ctx.enter_context(tc.psum_pool(name="att_ps", bufs=1))
 
         def load_rows(source, name):
-            loaded = raw.tile([P, S_BLOCKS, E], BF16, name=name)
+            loaded = raw.tile([P, S_BLOCKS, E], BF16, bufs=2 if name == "keys_raw" else 1, name=name)
             nc.sync.dma_start(out=loaded[:], in_=source.rearrange("(j p) e -> p j e", p=P))
             return loaded
 
         def load_first_batch():
             loaded = {
-                which: raw.tile([P, S_BLOCKS, E], BF16, name=which + "_raw") for which in ("q", "keys", "k", "x")
+                which: raw.tile([P, S_BLOCKS, E], BF16, bufs=2 if which == "keys" else 1, name=which + "_raw") for which in ("q", "keys", "k", "x")
             }
             rows_of = {
                 which: source[0].rearrange("(j p) e -> p j e", p=P)
@@ -86,13 +86,9 @@ def tile_multihead_attention_pa_kernel(
             nc.sync.dma_start(out=loaded["x"][:], in_=rows_of["x"])
             return loaded
 
-        def load_batch(b):
-            return {
-                "q": load_rows(q_relu[b], "q_raw"),
-                "keys": load_rows(keys[b], "keys_raw"),
-                "k": load_rows(k_relu[b], "k_raw"),
-                "x": load_rows(values[b], "x_raw"),
-            }
+        def load(loads, which, b):
+            source = {"q": q_relu, "keys": keys, "k": k_relu, "x": values}[which]
+            loads[which] = load_rows(source[b], which + "_raw")
 
         first_loads = load_first_batch()
 
@@ -124,18 +120,24 @@ def tile_multihead_attention_pa_kernel(
             else:
                 nc.vector.tensor_copy(out=out, in_=in_)
 
-        def make_mask(loads, made):
-            keys_raw = loads["keys"]
+        def fold_pieces(loads):
             fold_a = stage.tile([P, S_BLOCKS, E // 2], F32)
             fold_b = stage.tile([P, S_BLOCKS, E // 4], F32)
             fold_c = stage.tile([P, S_BLOCKS, E // 8], F32)
-            for source, folded in ((keys_raw, fold_a), (fold_a, fold_b), (fold_b, fold_c)):
+            pieces = []
+            for source, folded in ((loads["keys"], fold_a), (fold_a, fold_b), (fold_b, fold_c)):
                 half = folded.shape[-1]
                 for j in range(S_BLOCKS):
-                    nc.gpsimd.tensor_tensor(
-                        out=folded[:, j, :], in0=source[:, j, 0:half], in1=source[:, j, half : 2 * half], op=ALU.add
-                    )
-            made["folded"] = fold_c
+                    pieces.append((folded[:, j, :], source[:, j, 0:half], source[:, j, half : 2 * half], folded))
+            return pieces
+
+        def await_vector(t):
+            seen = small.tile([P, 1], F32, name="seen")
+            nc.gpsimd.tensor_copy(out=seen[:], in_=block(t)["neg_max"][:, t % NH : t % NH + 1])
+
+        def fold(pieces):
+            for folded, left, right, whole in pieces:
+                nc.gpsimd.tensor_tensor(out=folded, in0=left, in1=right, op=ALU.add)
 
         def lift_queries(loads, feats=slice(0, E)):
             firsts = loads["q"][:, :, feats.start : feats.stop : DH]
@@ -303,6 +305,7 @@ def tile_multihead_attention_pa_kernel(
 
         made = {}
         allocate(made)
+        later_loads, later_pieces = {}, []
         w_tiles = []
         for pair in range(E_BLOCKS // 2):
             w_raw = raw.tile([P, 2, E], BF16, bufs=4)
@@ -533,16 +536,11 @@ def tile_multihead_attention_pa_kernel(
 
         def norm(g):
             d = block_of[g]
-            y = d["y"]
             moments = small.tile([P, 2], F32, name="moments")
             nc.vector.bn_aggr(out=moments[:], in_=d["stats"][:])
             d["moments"] = moments
             if g >= N_BLOCKS - V_BLOCKS:
                 return
-            neg_mean = small.tile([P, 1], F32, name="neg_mean")
-            nc.gpsimd.tensor_scalar(
-                out=neg_mean[:], in0=moments[:, 0:1], scalar1=-1.0, scalar2=0.0, op0=ALU.mult, op1=ALU.add
-            )
             var = small.tile([P, 1], F32, name="var")
             nc.gpsimd.tensor_scalar(
                 out=var[:], in0=moments[:, 1:2], scalar1=E / (E - 1.0), scalar2=0.0, op0=ALU.mult, op1=ALU.add
@@ -553,10 +551,17 @@ def tile_multihead_attention_pa_kernel(
             nc.gpsimd.tensor_scalar(out=sd_eps[:], in0=sd[:], scalar1=EPS, scalar2=1.0, op0=ALU.add, op1=ALU.mult)
             inv_sd = small.tile([P, 1], F32, name="inv_sd")
             nc.gpsimd.tensor_tensor(out=inv_sd[:], in0=sd_eps[:], in1=minus_one[:], op=ALU.pow)
+            d["inv_sd"] = inv_sd
+
+        def scale_rows(g):
+            d = block_of[g]
+            y = d["y"]
+            neg_mean = small.tile([P, 1], F32, name="neg_mean")
+            nc.vector.tensor_scalar(out=neg_mean[:], in0=d["moments"][:, 0:1], scalar1=-1.0, scalar2=None, op0=ALU.mult)
             pieces = [slice(first, first + GP_COLS) for first in range(0, E, GP_COLS)]
             for cols in pieces:
                 nc.gpsimd.tensor_scalar(
-                    out=y[:, cols], in0=y[:, cols], scalar1=neg_mean[:, 0:1], scalar2=inv_sd[:, 0:1],
+                    out=y[:, cols], in0=y[:, cols], scalar1=neg_mean[:, 0:1], scalar2=d["inv_sd"][:, 0:1],
                     op0=ALU.add, op1=ALU.mult,
                 )
             for cols in pieces:
@@ -598,10 +603,14 @@ def tile_multihead_attention_pa_kernel(
         def engine_of(n):
             if n < n_first:
                 return "vector" if n % 2 else "scalar"
-            return "vector" if 13 <= (n - n_first) % n_batch < 17 else "scalar"
+            return "vector" if 16 <= (n - n_first) % n_batch < 20 else "scalar"
 
-        def mask_slot(b):
-            return 17 if b == 0 else 12
+        n_batch = 2 * NH + E_BLOCKS + 1
+
+        def prepared(slot, first):
+            if slot < first + 2:
+                return max(0, 2 * (slot - first + 1))
+            return 4 + (slot - first - 1) * (n_batch - 4) // (SLOTS - 3 - first)
 
         stages = {}
         for g in range(N_BLOCKS):
@@ -609,42 +618,45 @@ def tile_multihead_attention_pa_kernel(
             if g == N_BLOCKS - 1:
                 plan = [(7, quantise_e, (g, 0, HALF_HEADS)), (11, invert, (g,)), (11, quantise_e, (g, HALF_HEADS, NH))]
             for half in range(2):
-                first = 12 + 2 * half
+                first = 13 + 2 * half
                 plan += [(first, weigh, (g, half)), (first + 1, add_residual, (g, half)), (first + 2, statistics, (g, half))]
-            plan.append((17, norm, (g,)))
+            plan.append((18, norm, (g,)))
+            if 1 <= g <= N_BLOCKS - V_BLOCKS:
+                plan.append((11, scale_rows, (g - 1,)))
             if g < N_BLOCKS - V_BLOCKS:
-                plan.append((29, store, (g,)))
+                plan.append((31, store, (g,)))
             else:
                 plan.append(((N_BLOCKS - 1 - g) * NH + 18, root, (g,)))
                 plan.append(((N_BLOCKS - 1 - g) * NH + 19, norm_on_vector, (g,)))
             for after, stage_of, of in plan:
                 stages.setdefault(g * NH + after, []).append((stage_of, of))
+        LOAD_SLOTS = {6: "keys", 10: "x", 18: "q", 28: "k"}
+        GP_QUIET = 3
+        loads = {}
         items, emitted = first_items, 0
-        n_first, n_batch = len(first_items), 2 * NH + E_BLOCKS + 1
+        n_first = len(first_items)
         for t in range(-3, heads + 3 * NH):
             inside = 0 <= t < heads
             b, local = max(t, 0) // SLOTS, t % NH
             slot = t - b * SLOTS
             if inside and slot == 0 and b + 1 < B:
                 nxt = {}
-                allocate(nxt)
                 operands.append(nxt)
+                loads, pieces, later_loads = later_loads, later_pieces, {}
             if t == 2:
-                next_loads = load_batch(1)
-            if inside and slot == (8 if b == 0 else 0) and b + 1 < B:
-                q_items, k_items, x_items, p_items, v_items = preparation(next_loads, nxt)
-                items = items + q_items + x_items + p_items[:4] + [scale_item(nxt)]
-                items += k_items + p_items[4:] + v_items
-                lift_queries(next_loads)
-                make_mask(next_loads, nxt)
-            if inside and slot == mask_slot(b) and b + 1 < B:
-                add_keys(nxt, nxt["folded"])
-            if inside and slot == mask_slot(b) + 1 and b + 1 < B:
-                find_padded(nxt)
-            if inside and slot == mask_slot(b) + 2 and b + 1 < B:
-                sink_padded(next_loads, nxt)
-            if inside and slot == 26 and b + 2 < B:
-                next_loads = load_batch(b + 2)
+                for which in ("x", "q", "keys", "k"):
+                    load(loads, which, 1)
+            if inside and b + 2 < B and slot in LOAD_SLOTS:
+                load(later_loads, LOAD_SLOTS[slot], b + 2)
+            if inside and b + 1 < B:
+                if slot == (8 if b == 0 else 0):
+                    allocate(nxt)
+                    if b == 0:
+                        lift_queries(loads)
+                    q_items, k_items, x_items, p_items, v_items = preparation(loads, nxt)
+                    items = items + x_items + q_items + p_items + k_items + [scale_item(nxt)] + v_items
+            mask_slot = 19 if b == 0 else 11
+            free_ports = local == GP_QUIET or t < 12
             if t == -3:
                 load_residual(0)
                 load_residual(1)
@@ -655,7 +667,14 @@ def tile_multihead_attention_pa_kernel(
                 scores(t + 3)
             if 0 <= t + 2 < heads:
                 maximum(t + 2)
-            settle()
+            if free_ports:
+                settle()
+                if inside and slot == mask_slot and b + 1 < B:
+                    add_keys(nxt, pieces[-1][3])
+                    find_padded(nxt)
+                    sink_padded(loads, nxt)
+                if inside and slot == 27 and b + 2 < B:
+                    lift_queries(later_loads)
             if inside:
                 exponent(t)
             if t % 2 == 0 and 2 <= t <= heads:
@@ -666,12 +685,23 @@ def tile_multihead_attention_pa_kernel(
                 group(t // 2 - 1, "scalar")
             for stage_of, of in stages.get(t, []):
                 stage_of(*of)
+            if inside and b + 1 < B:
+                if b == 0 and slot == 12:
+                    pieces = fold_pieces(loads)
+                    await_vector(t + 2)
+                    fold(pieces[:8])
+                if slot == (12 if b == 0 else 5):
+                    fold(pieces[8:])
+            if inside and b + 2 < B and slot in (13, 21, 29):
+                if slot == 13:
+                    later_pieces = fold_pieces(later_loads)
+                fold(later_pieces[{13: slice(0, 2), 21: slice(2, 4), 29: slice(4, 8)}[slot]])
             if -2 <= t < heads:
                 due = 0
                 if b == 0:
-                    due = min(3 * (slot + 3), n_first) + max(0, (slot - 8) * n_batch // (SLOTS - 9))
+                    due = min(3 * (slot + 3), n_first) + prepared(slot, 8)
                 elif b + 1 < B:
-                    due = n_first + b * n_batch + (slot + 1) * n_batch // (SLOTS - 1)
+                    due = n_first + b * n_batch + prepared(slot, 0)
                 while emitted < due and items:
                     emit(items.pop(0), engine_of(emitted))
                     emitted += 1

@@ -20,7 +20,7 @@ K_PASS = P * PACK
 S_BLOCKS = S // P
 E_BLOCKS = E // P
 N_BLOCKS = B * S_BLOCKS
-V_BLOCKS = 3
+V_BLOCKS = 2
 PASSES = E // K_PASS
 PAIR = 2 * P
 HALF_HEADS = NH // 2
@@ -58,10 +58,8 @@ def tile_multihead_attention_pa_kernel(
         halves = ctx.enter_context(tc.tile_pool(name="halves", bufs=2))
         rows = ctx.enter_context(tc.tile_pool(name="rows", bufs=3))
         small = ctx.enter_context(tc.tile_pool(name="small", bufs=6))
-        prep_ps = ctx.enter_context(tc.psum_pool(name="prep_ps", bufs=2))
+        bank_ps = ctx.enter_context(tc.psum_pool(name="bank_ps", bufs=4))
         score_ps = ctx.enter_context(tc.psum_pool(name="score_ps", bufs=4))
-        flip_ps = ctx.enter_context(tc.psum_pool(name="flip_ps", bufs=1))
-        att_ps = ctx.enter_context(tc.psum_pool(name="att_ps", bufs=1))
 
         def load_rows(source, name):
             loaded = raw.tile([P, S_BLOCKS, E], BF16, bufs=2 if name == "keys_raw" else 1, name=name)
@@ -99,8 +97,8 @@ def tile_multihead_attention_pa_kernel(
 
         ctx.enter_context(tc.manual_schedule())
 
-        w_codes = const.tile([P, PASSES, E], U32, align_bytes=64)
-        w_scales = const.tile([P, PASSES, E], U8, align_bytes=64)
+        w_codes = const.tile([P, E_BLOCKS // 2, PASSES, PAIR], U32, align_bytes=64)
+        w_scales = const.tile([P, E_BLOCKS // 2, PASSES, PAIR], U8, align_bytes=64)
         bv_col = const.tile([P, E_BLOCKS], F32)
         gamma_all = const.tile([P, E], BF16)
         betta_all = const.tile([P, E], BF16)
@@ -139,36 +137,41 @@ def tile_multihead_attention_pa_kernel(
             for folded, left, right, whole in pieces:
                 nc.gpsimd.tensor_tensor(out=folded, in0=left, in1=right, op=ALU.add)
 
-        def lift_queries(loads, feats=slice(0, E)):
+        def lift_queries(loads, feats=slice(0, E), engine=nc.gpsimd):
             firsts = loads["q"][:, :, feats.start : feats.stop : DH]
-            nc.vector.tensor_scalar(out=firsts, in0=firsts, scalar1=FLOOR, scalar2=None, op0=ALU.max)
+            engine.tensor_scalar(out=firsts, in0=firsts, scalar1=FLOOR, scalar2=None, op0=ALU.max)
 
         def add_keys(made, rows_to_add):
             made["key_sum"] = small.tile([P, S_BLOCKS], F32, name="key_sum")
             nc.vector.tensor_reduce(out=made["key_sum"][:], in_=rows_to_add[:], axis=AXIS.X, op=ALU.add)
 
-        def find_padded(made):
-            made["keep"] = small.tile([P, S_BLOCKS], F32, name="keep")
-            nc.vector.tensor_single_scalar(out=made["keep"][:], in_=made["key_sum"][:], scalar=0.0, op=ALU.not_equal)
-            made["sunk"] = small.tile([P, S_BLOCKS], F32, name="sunk")
-            nc.vector.tensor_scalar(
-                out=made["sunk"][:], in0=made["key_sum"][:], scalar1=0.0, scalar2=NEG_KEY,
-                op0=ALU.is_equal, op1=ALU.mult,
-            )
-            made["keep_bf"] = small.tile([P, S_BLOCKS], BF16, name="keep_bf")
-            nc.vector.tensor_single_scalar(out=made["keep_bf"][:], in_=made["key_sum"][:], scalar=0.0, op=ALU.not_equal)
-
-        def sink_padded(loads, made, feats=slice(0, E)):
+        def sink_padded(loads, made, feats=slice(0, E), engine=nc.gpsimd):
+            if "keep" not in made:
+                made["padded"] = small.tile([P, S_BLOCKS], F32, name="padded")
+                engine.tensor_scalar(
+                    out=made["padded"][:], in0=made["key_sum"][:], scalar1=0.0, scalar2=1.0,
+                    op0=ALU.is_equal, op1=ALU.mult,
+                )
+                made["sunk"] = small.tile([P, S_BLOCKS], F32, name="sunk")
+                engine.tensor_scalar(
+                    out=made["sunk"][:], in0=made["key_sum"][:], scalar1=0.0, scalar2=NEG_KEY,
+                    op0=ALU.is_equal, op1=ALU.mult,
+                )
+                for name, dtype in (("keep", F32), ("keep_bf", BF16)):
+                    made[name] = small.tile([P, S_BLOCKS], dtype, name=name)
+                    engine.tensor_scalar(
+                        out=made[name][:], in0=made["padded"][:], scalar1=-1.0, scalar2=1.0, op0=ALU.mult, op1=ALU.add
+                    )
             for j in range(S_BLOCKS):
                 firsts = loads["k"][:, j, feats.start : feats.stop : DH]
-                nc.vector.tensor_scalar(
+                engine.tensor_scalar(
                     out=firsts, in0=firsts, scalar1=made["keep"][:, j : j + 1], scalar2=made["sunk"][:, j : j + 1],
                     op0=ALU.mult, op1=ALU.add,
                 )
 
         def scale_item(made):
             def fill():
-                bank = prep_ps.tile([P, 1], F32, tag="prep", name="kept_bank")
+                bank = bank_ps.tile([P, 1], F32, tag="bank", name="kept_bank")
                 for j in range(S_BLOCKS):
                     nc.tensor.matmul(
                         out=bank[:], lhsT=ones_bf[:], rhs=made["keep_bf"][:, j : j + 1],
@@ -177,14 +180,11 @@ def tile_multihead_attention_pa_kernel(
                 return bank
 
             def empty(bank, engine):
-                made["scale"] = batch.tile([P, 1], F32, name="scale")
-                nc.vector.tensor_scalar(
-                    out=made["scale"][:], in0=bank[:], scalar1=0.0, scalar2=SCALE, op0=ALU.not_equal, op1=ALU.mult
-                )
-                made["minus_scale"] = batch.tile([P, 1], F32, name="minus_scale")
-                nc.vector.tensor_scalar(
-                    out=made["minus_scale"][:], in0=bank[:], scalar1=0.0, scalar2=-SCALE, op0=ALU.not_equal, op1=ALU.mult
-                )
+                for name, factor in (("scale", SCALE), ("minus_scale", -SCALE)):
+                    made[name] = batch.tile([P, 1], F32, name=name)
+                    nc.vector.tensor_scalar(
+                        out=made[name][:], in0=bank[:], scalar1=0.0, scalar2=factor, op0=ALU.not_equal, op1=ALU.mult
+                    )
 
             return fill, empty, None
 
@@ -199,7 +199,7 @@ def tile_multihead_attention_pa_kernel(
 
         def heads_item(loads, made, which, first_head):
             def fill():
-                bank = prep_ps.tile([P, 2, S], BF16, tag="prep", name="head_bank")
+                bank = bank_ps.tile([P, 2, S], BF16, tag="bank", name="head_bank")
                 for a in range(2):
                     feats = slice((first_head + a) * DH, (first_head + a + 1) * DH)
                     for j in range(S_BLOCKS):
@@ -213,7 +213,7 @@ def tile_multihead_attention_pa_kernel(
 
         def x_item(loads, made, g, pair):
             def fill():
-                bank = prep_ps.tile([P, 2, PAIR], F32, tag="prep", name="x_bank")
+                bank = bank_ps.tile([P, 2, PAIR], F32, tag="bank", name="x_bank")
                 x_words = loads["x"][:].bitcast(F32)
                 flip_words(nc, ident_f32[:], bank, [x_words[:, 2 * pair + a, :] for a in range(2)], g * PAIR)
                 return bank
@@ -227,25 +227,24 @@ def tile_multihead_attention_pa_kernel(
 
             return fill, empty
 
-        def quantise_x(made, g):
-            if g == 0:
-                made["x_codes"] = stage.tile([P, PASSES, S], U32, align_bytes=64, name="x_codes")
-                made["x_scales"] = stage.tile([P, PASSES, S], U8, align_bytes=64, name="x_scales")
+        def quantise_x(made):
+            made["x_codes"] = stage.tile([P, PASSES, S], U32, align_bytes=64, name="x_codes")
+            made["x_scales"] = stage.tile([P, PASSES, S], U8, align_bytes=64, name="x_scales")
             nc.vector.quantize_mx(
-                out=made["x_codes"][:, g, :].bitcast(FP8X4),
-                scales=made["x_scales"][:, g, :],
-                in_=made["x_grouped"][:, g, :, :].rearrange("p c j -> p (c j)"),
+                out=made["x_codes"][:].rearrange("p g c -> p (g c)").bitcast(FP8X4),
+                scales=made["x_scales"][:].rearrange("p g c -> p (g c)"),
+                in_=made["x_grouped"][:].rearrange("p g c j -> p (g c j)"),
             )
 
         def project_item(made, m):
             def fill():
                 settle()
-                bank = prep_ps.tile([P, S], F32, tag="prep", name="v_bank")
+                bank = bank_ps.tile([P, S], F32, tag="bank", name="v_bank")
                 for g in range(PASSES):
                     nc.tensor.matmul_mx(
                         out=bank[:],
-                        lhsT=w_codes[:, g, m * P : (m + 1) * P].bitcast(FP8X4),
-                        lhsT_scale=w_scales[:, g, m * P : (m + 1) * P],
+                        lhsT=w_codes[:, m // 2, g, m % 2 * P : (m % 2 + 1) * P].bitcast(FP8X4),
+                        lhsT_scale=w_scales[:, m // 2, g, m % 2 * P : (m % 2 + 1) * P],
                         rhs=made["x_codes"][:, g, :].bitcast(FP8X4),
                         rhs_scale=made["x_scales"][:, g, :],
                         start=(g == 0),
@@ -269,7 +268,7 @@ def tile_multihead_attention_pa_kernel(
 
         def v_item(made, pair):
             def fill():
-                bank = prep_ps.tile([P, 2, PAIR], F32, tag="prep", name="vk_bank")
+                bank = bank_ps.tile([P, 2, PAIR], F32, tag="bank", name="vk_bank")
                 vT_words = made["vT"][:].bitcast(F32)
                 flip_words(nc, ident_f32[:], bank, [vT_words[:, 2 * pair + a, :] for a in range(2)], 0)
                 return bank
@@ -294,12 +293,12 @@ def tile_multihead_attention_pa_kernel(
 
         def w_item(g, grouped, words):
             def fill():
-                bank = prep_ps.tile([P, 2, PAIR], F32, tag="prep", name="w_bank")
+                bank = bank_ps.tile([P, 2, PAIR], F32, tag="bank", name="w_bank")
                 flip_words(nc, ident_f32[:], bank, [words[:, a, :] for a in range(2)], g * PAIR)
                 return bank
 
             def empty(bank, engine):
-                copy_on(engine, grouped[:].bitcast(F32), bank[:].rearrange("p u c -> p c u"))
+                copy_on(engine, grouped[:, g, :, :].bitcast(F32), bank[:].rearrange("p u c -> p c u"))
 
             return fill, empty
 
@@ -323,24 +322,22 @@ def tile_multihead_attention_pa_kernel(
             items = []
             for pair in range(E_BLOCKS // 2):
                 words = w_tiles[pair][:].bitcast(F32)
-                cols = slice(pair * PAIR, (pair + 1) * PAIR)
+                grouped = stage.tile([P, PASSES, PAIR, PACK], BF16, bufs=2, align_bytes=64, name="w_grouped")
+
+                def then(pair=pair, grouped=grouped):
+                    nc.vector.quantize_mx(
+                        out=w_codes[:, pair, :, :].rearrange("p g c -> p (g c)").bitcast(FP8X4),
+                        scales=w_scales[:, pair, :, :].rearrange("p g c -> p (g c)"),
+                        in_=grouped[:].rearrange("p g c j -> p (g c j)"),
+                    )
+
                 for g in range(PASSES):
-                    grouped = stage.tile([P, PAIR, PACK], BF16, bufs=4, align_bytes=64, name="w_grouped")
-                    fill, empty = w_item(g, grouped, words)
-
-                    def then(g=g, cols=cols, grouped=grouped):
-                        nc.vector.quantize_mx(
-                            out=w_codes[:, g, cols].bitcast(FP8X4),
-                            scales=w_scales[:, g, cols],
-                            in_=grouped[:].rearrange("p c j -> p (c j)"),
-                        )
-
-                    items.append((fill, empty, then))
+                    items.append(w_item(g, grouped, words) + (then if g == PASSES - 1 else None,))
             return items
 
         def bias_item():
             def fill():
-                bank = prep_ps.tile([P, P], BF16, tag="prep", name="bv_bank")
+                bank = bank_ps.tile([P, P], BF16, tag="bank", name="bv_bank")
                 nc.tensor.transpose(bank[:], bv_rows[:], ident_bf[:])
                 return bank
 
@@ -355,7 +352,7 @@ def tile_multihead_attention_pa_kernel(
             x_items = []
             for g in range(PASSES):
                 x_items.append(x_item(loads, made, g, 0) + (None,))
-                x_items.append(x_item(loads, made, g, 1) + (lambda g=g: quantise_x(made, g),))
+                x_items.append(x_item(loads, made, g, 1) + ((lambda: quantise_x(made)) if g == PASSES - 1 else None,))
             p_items = [project_item(made, m) + (None,) for m in range(E_BLOCKS)]
             v_items = [v_item(made, pair) + (None,) for pair in range(E_BLOCKS // 2 - 1)]
             v_items.append(v_item(made, E_BLOCKS // 2 - 1) + (lambda: quantise_v(made),))
@@ -376,12 +373,12 @@ def tile_multihead_attention_pa_kernel(
                 to_settle.append(then)
 
         def emit(item, engine):
-            if len(to_empty) == 2:
+            if len(to_empty) == 3:
                 empty_one()
             fill, empty, then = item
             to_empty.append((fill(), empty, then, engine))
 
-        lift_queries(first_loads, HEAD_HALF[0])
+        lift_queries(first_loads, HEAD_HALF[0], nc.vector)
         made["key_sum"] = const.tile([P, S_BLOCKS], F32, name="first_key_sum")
         nc.vector.tensor_reduce(
             out=made["key_sum"][:, 0:2], in_=first_loads["keys"][:, 0:2, :], axis=AXIS.X, op=ALU.add
@@ -392,8 +389,7 @@ def tile_multihead_attention_pa_kernel(
                 out=summed[:], in_=first_loads["keys"][:, j, :], func=ACT.Identity, bias=0.0, scale=1.0,
                 accum_out=made["key_sum"][:, j : j + 1],
             )
-        find_padded(made)
-        sink_padded(first_loads, made, HEAD_HALF[0])
+        sink_padded(first_loads, made, HEAD_HALF[0], nc.vector)
         q_items, k_items, x_items, p_items, v_items = preparation(first_loads, made)
         emit(q_items[0], "scalar")
         emit(k_items[0], "vector")
@@ -402,8 +398,8 @@ def tile_multihead_attention_pa_kernel(
         emit(k_items[1], "scalar")
         empty_one()
         empty_one()
-        lift_queries(first_loads, HEAD_HALF[1])
-        sink_padded(first_loads, made, HEAD_HALF[1])
+        lift_queries(first_loads, HEAD_HALF[1], nc.vector)
+        sink_padded(first_loads, made, HEAD_HALF[1], nc.vector)
         first_items = [q_items[2], k_items[2], q_items[3], k_items[3]] + x_items + w_items() + [bias_item()] + p_items + v_items
 
         operands = [made]
@@ -437,10 +433,10 @@ def tile_multihead_attention_pa_kernel(
                 width = S if t < SLOTS // 2 else S // 2
                 nc.tensor.matmul_mx(
                     out=score_of[t][:, 0:width],
-                    lhsT=w_codes[:, 0, 0:P].bitcast(FP8X4),
-                    lhsT_scale=w_scales[:, 0, 0:P],
-                    rhs=w_codes[:, 1, 0:width].bitcast(FP8X4),
-                    rhs_scale=w_scales[:, 1, 0:width],
+                    lhsT=w_codes[:, 0, 0, 0:P].bitcast(FP8X4),
+                    lhsT_scale=w_scales[:, 0, 0, 0:P],
+                    rhs=w_codes[:, 1, :, :].rearrange("p g c -> p (g c)")[:, 0:width].bitcast(FP8X4),
+                    rhs_scale=w_scales[:, 1, :, :].rearrange("p g c -> p (g c)")[:, 0:width],
                     start=True,
                     stop=True,
                 )
@@ -467,7 +463,7 @@ def tile_multihead_attention_pa_kernel(
             )
 
         def flip(pair):
-            flip_of[pair] = flip_ps.tile([P, 2, PAIR], F32, name="e_bank")
+            flip_of[pair] = bank_ps.tile([P, 2, PAIR], F32, tag="bank", name="e_bank")
             e_words = e_of[pair][:].bitcast(F32)
             flip_words(nc, ident_f32[:], flip_of[pair], [e_words[:, a, :] for a in range(2)], 0)
 
@@ -502,7 +498,7 @@ def tile_multihead_attention_pa_kernel(
         def weigh(g, half):
             d = block_of[g]
             m = operands[d["b"]]
-            d["att"] = att_ps.tile([P, HALF_HEADS, DH], F32, name="att")
+            d["att"] = bank_ps.tile([P, HALF_HEADS, DH], F32, tag="bank", name="att")
             for a in range(HALF_HEADS):
                 h = half * HALF_HEADS + a
                 nc.tensor.matmul_mx(
@@ -603,7 +599,7 @@ def tile_multihead_attention_pa_kernel(
         def engine_of(n):
             if n < n_first:
                 return "vector" if n % 2 else "scalar"
-            return "vector" if 16 <= (n - n_first) % n_batch < 20 else "scalar"
+            return "vector" if (n - n_first) % n_batch in ON_VECTOR else "scalar"
 
         n_batch = 2 * NH + E_BLOCKS + 1
 
@@ -614,9 +610,10 @@ def tile_multihead_attention_pa_kernel(
 
         stages = {}
         for g in range(N_BLOCKS):
-            plan = [(11, invert, (g,)), (11, quantise_e, (g, 0, NH))]
+            plan = [(11, quantise_e, (g, 0, NH))]
             if g == N_BLOCKS - 1:
-                plan = [(7, quantise_e, (g, 0, HALF_HEADS)), (11, invert, (g,)), (11, quantise_e, (g, HALF_HEADS, NH))]
+                plan = [(11, quantise_e, (g, 0, HALF_HEADS)), (11, quantise_e, (g, HALF_HEADS, NH))]
+            plan.append((11, invert, (g,)))
             for half in range(2):
                 first = 13 + 2 * half
                 plan += [(first, weigh, (g, half)), (first + 1, add_residual, (g, half)), (first + 2, statistics, (g, half))]
@@ -630,6 +627,7 @@ def tile_multihead_attention_pa_kernel(
                 plan.append(((N_BLOCKS - 1 - g) * NH + 19, norm_on_vector, (g,)))
             for after, stage_of, of in plan:
                 stages.setdefault(g * NH + after, []).append((stage_of, of))
+        ON_VECTOR = (4, 6, 21, 23)
         LOAD_SLOTS = {6: "keys", 10: "x", 18: "q", 28: "k"}
         GP_QUIET = 3
         loads = {}
@@ -654,8 +652,8 @@ def tile_multihead_attention_pa_kernel(
                     if b == 0:
                         lift_queries(loads)
                     q_items, k_items, x_items, p_items, v_items = preparation(loads, nxt)
-                    items = items + x_items + q_items + p_items + k_items + [scale_item(nxt)] + v_items
-            mask_slot = 19 if b == 0 else 11
+                    items = items + x_items + q_items + p_items + v_items + [scale_item(nxt)] + k_items
+            mask_slot = 19
             free_ports = local == GP_QUIET or t < 12
             if t == -3:
                 load_residual(0)
@@ -671,7 +669,6 @@ def tile_multihead_attention_pa_kernel(
                 settle()
                 if inside and slot == mask_slot and b + 1 < B:
                     add_keys(nxt, pieces[-1][3])
-                    find_padded(nxt)
                     sink_padded(loads, nxt)
                 if inside and slot == 27 and b + 2 < B:
                     lift_queries(later_loads)
@@ -679,10 +676,10 @@ def tile_multihead_attention_pa_kernel(
                 exponent(t)
             if t % 2 == 0 and 2 <= t <= heads:
                 flip(t // 2 - 1)
-            while to_empty:
-                empty_one()
             if t % 2 == 1 and 3 <= t <= heads + 1:
                 group(t // 2 - 1, "scalar")
+            while to_empty:
+                empty_one()
             for stage_of, of in stages.get(t, []):
                 stage_of(*of)
             if inside and b + 1 < B:

@@ -25,7 +25,7 @@ PASSES = E // K_PASS
 PAIR = 2 * P
 HALF_HEADS = NH // 2
 SCALE = 1.0 / DH**0.5
-GP_COLS = 512
+GP_COLS = 1024
 LARGE = 3.0e38
 FLOOR = 2.0**-60
 HEAD_HALF = (slice(0, E // 2), slice(E // 2, E))
@@ -106,8 +106,6 @@ def tile_multihead_attention_pa_kernel(
         nc.vector.memset(ones_bf[:], 1.0)
         one_half = const.tile([P, 1], F32)
         nc.vector.memset(one_half[:], 0.5)
-        minus_one = const.tile([P, 1], F32)
-        nc.vector.memset(minus_one[:], -1.0)
 
         warm = const.tile([P, 1], F32)
         nc.scalar.activation(out=warm[:], in_=one_half[:], func=ACT.Exp)
@@ -123,10 +121,11 @@ def tile_multihead_attention_pa_kernel(
             fold_b = stage.tile([P, S_BLOCKS, E // 4], F32)
             fold_c = stage.tile([P, S_BLOCKS, E // 8], F32)
             pieces = []
-            for source, folded in ((loads["keys"], fold_a), (fold_a, fold_b), (fold_b, fold_c)):
+            for source, folded, at_once in ((loads["keys"], fold_a, 2), (fold_a, fold_b, 4), (fold_b, fold_c, 4)):
                 half = folded.shape[-1]
-                for j in range(S_BLOCKS):
-                    pieces.append((folded[:, j, :], source[:, j, 0:half], source[:, j, half : 2 * half], folded))
+                for first in range(0, S_BLOCKS, at_once):
+                    js = slice(first, first + at_once)
+                    pieces.append((folded[:, js, :], source[:, js, 0:half], source[:, js, half : 2 * half], folded))
             return pieces
 
         def await_vector(t):
@@ -137,7 +136,7 @@ def tile_multihead_attention_pa_kernel(
             for folded, left, right, whole in pieces:
                 nc.gpsimd.tensor_tensor(out=folded, in0=left, in1=right, op=ALU.add)
 
-        def lift_queries(loads, feats=slice(0, E), engine=nc.gpsimd):
+        def lift_queries(loads, feats=slice(0, E), engine=nc.vector):
             firsts = loads["q"][:, :, feats.start : feats.stop : DH]
             engine.tensor_scalar(out=firsts, in0=firsts, scalar1=FLOOR, scalar2=None, op0=ALU.max)
 
@@ -145,7 +144,7 @@ def tile_multihead_attention_pa_kernel(
             made["key_sum"] = small.tile([P, S_BLOCKS], F32, name="key_sum")
             nc.vector.tensor_reduce(out=made["key_sum"][:], in_=rows_to_add[:], axis=AXIS.X, op=ALU.add)
 
-        def sink_padded(loads, made, feats=slice(0, E), engine=nc.gpsimd):
+        def sink_padded(loads, made, feats=slice(0, E), engine=nc.vector):
             if "keep" not in made:
                 made["padded"] = small.tile([P, S_BLOCKS], F32, name="padded")
                 engine.tensor_scalar(
@@ -537,27 +536,24 @@ def tile_multihead_attention_pa_kernel(
             d["moments"] = moments
             if g >= N_BLOCKS - V_BLOCKS:
                 return
-            var = small.tile([P, 1], F32, name="var")
-            nc.gpsimd.tensor_scalar(
-                out=var[:], in0=moments[:, 1:2], scalar1=E / (E - 1.0), scalar2=0.0, op0=ALU.mult, op1=ALU.add
-            )
-            sd = small.tile([P, 1], F32, name="sd")
-            nc.gpsimd.tensor_tensor(out=sd[:], in0=var[:], in1=one_half[:], op=ALU.pow)
-            sd_eps = small.tile([P, 1], F32, name="sd_eps")
-            nc.gpsimd.tensor_scalar(out=sd_eps[:], in0=sd[:], scalar1=EPS, scalar2=1.0, op0=ALU.add, op1=ALU.mult)
-            inv_sd = small.tile([P, 1], F32, name="inv_sd")
-            nc.gpsimd.tensor_tensor(out=inv_sd[:], in0=sd_eps[:], in1=minus_one[:], op=ALU.pow)
-            d["inv_sd"] = inv_sd
+            d["root"] = small.tile([P, 1], F32, name="root")
+            nc.gpsimd.tensor_tensor(out=d["root"][:], in0=moments[:, 1:2], in1=one_half[:], op=ALU.pow)
 
         def scale_rows(g):
             d = block_of[g]
             y = d["y"]
+            sd_eps = small.tile([P, 1], F32, name="sd_eps")
+            nc.vector.tensor_scalar(
+                out=sd_eps[:], in0=d["root"][:], scalar1=(E / (E - 1.0)) ** 0.5, scalar2=EPS, op0=ALU.mult, op1=ALU.add
+            )
             neg_mean = small.tile([P, 1], F32, name="neg_mean")
             nc.vector.tensor_scalar(out=neg_mean[:], in0=d["moments"][:, 0:1], scalar1=-1.0, scalar2=None, op0=ALU.mult)
+            inv_sd = small.tile([P, 1], F32, name="inv_sd")
+            nc.vector.reciprocal(out=inv_sd[:], in_=sd_eps[:])
             pieces = [slice(first, first + GP_COLS) for first in range(0, E, GP_COLS)]
             for cols in pieces:
                 nc.gpsimd.tensor_scalar(
-                    out=y[:, cols], in0=y[:, cols], scalar1=neg_mean[:, 0:1], scalar2=d["inv_sd"][:, 0:1],
+                    out=y[:, cols], in0=y[:, cols], scalar1=neg_mean[:, 0:1], scalar2=inv_sd[:, 0:1],
                     op0=ALU.add, op1=ALU.mult,
                 )
             for cols in pieces:
@@ -686,13 +682,13 @@ def tile_multihead_attention_pa_kernel(
                 if b == 0 and slot == 12:
                     pieces = fold_pieces(loads)
                     await_vector(t + 2)
-                    fold(pieces[:8])
+                    fold(pieces[:2])
                 if slot == (12 if b == 0 else 5):
-                    fold(pieces[8:])
-            if inside and b + 2 < B and slot in (13, 21, 29):
+                    fold(pieces[2:])
+            if inside and b + 2 < B and slot in (13, 21):
                 if slot == 13:
                     later_pieces = fold_pieces(later_loads)
-                fold(later_pieces[{13: slice(0, 2), 21: slice(2, 4), 29: slice(4, 8)}[slot]])
+                fold(later_pieces[{13: slice(0, 1), 21: slice(1, 2)}[slot]])
             if -2 <= t < heads:
                 due = 0
                 if b == 0:

from contextlib import ExitStack

import concourse.mybir as mybir
from concourse.masks import make_identity

F32 = mybir.dt.float32
BF16 = mybir.dt.bfloat16
U32 = mybir.dt.uint32
U8 = mybir.dt.uint8
FP8X4 = mybir.dt.float8_e4m3fn_x4
ALU = mybir.AluOpType
ACT = mybir.ActivationFunctionType
AXIS = mybir.AxisListType

B, S, E, NH = 4, 512, 1024, 8
DH = E // NH
P = 128
PACK = 4
K_PASS = P * PACK
S_BLOCKS = S // P
E_BLOCKS = E // P
N_BLOCKS = B * S_BLOCKS
V_BLOCKS = 2
PASSES = E // K_PASS
PAIR = 2 * P
HALF_HEADS = NH // 2
SCALE = 1.0 / DH**0.5
GP_COLS = 1024
LARGE = 3.0e38
FLOOR = 2.0**-60
HEAD_HALF = (slice(0, E // 2), slice(E // 2, E))
NEG_KEY = -(2.0**100)
EPS = 1e-08

FLOPS = 2 * B * S * E * E + 2 * (2 * B * NH * S * S * DH)


def flip_words(nc, identity, bank, row_blocks, first_word):
    for u in range(2):
        for a, words in enumerate(row_blocks):
            nc.tensor.transpose(
                bank[:, u, a * P : (a + 1) * P],
                words[:, first_word + u * P : first_word + (u + 1) * P],
                identity,
            )


def tile_multihead_attention_pa_kernel(
    tc, q_relu, k_relu, keys, values, Wv, bv, queries, gamma, betta, out
):
    nc = tc.nc
    with ExitStack() as ctx:
        const = ctx.enter_context(tc.tile_pool(name="const", bufs=1))
        raw = ctx.enter_context(tc.tile_pool(name="raw", bufs=1))
        stage = ctx.enter_context(tc.tile_pool(name="stage", bufs=1))
        batch = ctx.enter_context(tc.tile_pool(name="batch", bufs=2))
        work = ctx.enter_context(tc.tile_pool(name="work", bufs=3))
        halves = ctx.enter_context(tc.tile_pool(name="halves", bufs=2))
        rows = ctx.enter_context(tc.tile_pool(name="rows", bufs=3))
        small = ctx.enter_context(tc.tile_pool(name="small", bufs=6))
        bank_ps = ctx.enter_context(tc.psum_pool(name="bank_ps", bufs=4))
        score_ps = ctx.enter_context(tc.psum_pool(name="score_ps", bufs=4))

        def load_rows(source, name):
            loaded = raw.tile([P, S_BLOCKS, E], BF16, bufs=2 if name == "keys_raw" else 1, name=name)
            nc.sync.dma_start(out=loaded[:], in_=source.rearrange("(j p) e -> p j e", p=P))
            return loaded

        def load_first_batch():
            loaded = {
                which: raw.tile([P, S_BLOCKS, E], BF16, bufs=2 if which == "keys" else 1, name=which + "_raw") for which in ("q", "keys", "k", "x")
            }
            rows_of = {
                which: source[0].rearrange("(j p) e -> p j e", p=P)
                for which, source in (("q", q_relu), ("keys", keys), ("k", k_relu), ("x", values))
            }
            half = S_BLOCKS // 2
            nc.sync.dma_start(out=loaded["q"][:, :, HEAD_HALF[0]], in_=rows_of["q"][:, :, HEAD_HALF[0]])
            nc.sync.dma_start(out=loaded["keys"][:, 0:half, :], in_=rows_of["keys"][:, 0:half, :])
            nc.sync.dma_start(out=loaded["keys"][:, half:, :], in_=rows_of["keys"][:, half:, :])
            nc.sync.dma_start(out=loaded["k"][:, :, HEAD_HALF[0]], in_=rows_of["k"][:, :, HEAD_HALF[0]])
            nc.sync.dma_start(out=loaded["q"][:, :, HEAD_HALF[1]], in_=rows_of["q"][:, :, HEAD_HALF[1]])
            nc.sync.dma_start(out=loaded["k"][:, :, HEAD_HALF[1]], in_=rows_of["k"][:, :, HEAD_HALF[1]])
            nc.sync.dma_start(out=loaded["x"][:], in_=rows_of["x"])
            return loaded

        def load(loads, which, b):
            source = {"q": q_relu, "keys": keys, "k": k_relu, "x": values}[which]
            loads[which] = load_rows(source[b], which + "_raw")

        first_loads = load_first_batch()

        ident_bf = const.tile([P, P], BF16)
        make_identity(nc, ident_bf[:])
        ident_f32 = const.tile([P, P], F32)
        nc.vector.tensor_copy(out=ident_f32[:], in_=ident_bf[:])

        ctx.enter_context(tc.manual_schedule())

        w_codes = const.tile([P, E_BLOCKS // 2, PASSES, PAIR], U32, align_bytes=64)
        w_scales = const.tile([P, E_BLOCKS // 2, PASSES, PAIR], U8, align_bytes=64)
        bv_col = const.tile([P, E_BLOCKS], F32)
        gamma_all = const.tile([P, E], BF16)
        betta_all = const.tile([P, E], BF16)
        ones_bf = const.tile([P, P], BF16)
        nc.vector.memset(ones_bf[:], 1.0)
        one_half = const.tile([P, 1], F32)
        nc.vector.memset(one_half[:], 0.5)

        warm = const.tile([P, 1], F32)
        nc.scalar.activation(out=warm[:], in_=one_half[:], func=ACT.Exp)

        def copy_on(engine, out, in_):
            if engine == "scalar":
                nc.scalar.copy(out=out, in_=in_)
            else:
                nc.vector.tensor_copy(out=out, in_=in_)

        def fold_pieces(loads):
            fold_a = stage.tile([P, S_BLOCKS, E // 2], F32)
            fold_b = stage.tile([P, S_BLOCKS, E // 4], F32)
            fold_c = stage.tile([P, S_BLOCKS, E // 8], F32)
            pieces = []
            for source, folded, at_once in ((loads["keys"], fold_a, 2), (fold_a, fold_b, 4), (fold_b, fold_c, 4)):
                half = folded.shape[-1]
                for first in range(0, S_BLOCKS, at_once):
                    js = slice(first, first + at_once)
                    pieces.append((folded[:, js, :], source[:, js, 0:half], source[:, js, half : 2 * half], folded))
            return pieces

        def await_vector(t):
            seen = small.tile([P, 1], F32, name="seen")
            nc.gpsimd.tensor_copy(out=seen[:], in_=block(t)["neg_max"][:, t % NH : t % NH + 1])

        def fold(pieces):
            for folded, left, right, whole in pieces:
                nc.gpsimd.tensor_tensor(out=folded, in0=left, in1=right, op=ALU.add)

        def lift_queries(loads, feats=slice(0, E), engine=nc.vector):
            firsts = loads["q"][:, :, feats.start : feats.stop : DH]
            engine.tensor_scalar(out=firsts, in0=firsts, scalar1=FLOOR, scalar2=None, op0=ALU.max)

        def add_keys(made, rows_to_add):
            made["key_sum"] = small.tile([P, S_BLOCKS], F32, name="key_sum")
            nc.vector.tensor_reduce(out=made["key_sum"][:], in_=rows_to_add[:], axis=AXIS.X, op=ALU.add)

        def sink_padded(loads, made, feats=slice(0, E), engine=nc.vector):
            if "keep" not in made:
                made["padded"] = small.tile([P, S_BLOCKS], F32, name="padded")
                engine.tensor_scalar(
                    out=made["padded"][:], in0=made["key_sum"][:], scalar1=0.0, scalar2=1.0,
                    op0=ALU.is_equal, op1=ALU.mult,
                )
                made["sunk"] = small.tile([P, S_BLOCKS], F32, name="sunk")
                engine.tensor_scalar(
                    out=made["sunk"][:], in0=made["key_sum"][:], scalar1=0.0, scalar2=NEG_KEY,
                    op0=ALU.is_equal, op1=ALU.mult,
                )
                for name, dtype in (("keep", F32), ("keep_bf", BF16)):
                    made[name] = small.tile([P, S_BLOCKS], dtype, name=name)
                    engine.tensor_scalar(
                        out=made[name][:], in0=made["padded"][:], scalar1=-1.0, scalar2=1.0, op0=ALU.mult, op1=ALU.add
                    )
            for j in range(S_BLOCKS):
                firsts = loads["k"][:, j, feats.start : feats.stop : DH]
                engine.tensor_scalar(
                    out=firsts, in0=firsts, scalar1=made["keep"][:, j : j + 1], scalar2=made["sunk"][:, j : j + 1],
                    op0=ALU.mult, op1=ALU.add,
                )

        def scale_item(made):
            def fill():
                bank = bank_ps.tile([P, 1], F32, tag="bank", name="kept_bank")
                for j in range(S_BLOCKS):
                    nc.tensor.matmul(
                        out=bank[:], lhsT=ones_bf[:], rhs=made["keep_bf"][:, j : j + 1],
                        start=(j == 0), stop=(j == S_BLOCKS - 1),
                    )
                return bank

            def empty(bank, engine):
                for name, factor in (("scale", SCALE), ("minus_scale", -SCALE)):
                    made[name] = batch.tile([P, 1], F32, name=name)
                    nc.vector.tensor_scalar(
                        out=made[name][:], in0=bank[:], scalar1=0.0, scalar2=factor, op0=ALU.not_equal, op1=ALU.mult
                    )

            return fill, empty, None

        def allocate(made):
            made["qT"] = batch.tile([P, NH, S], BF16, name="qT")
            made["kT"] = batch.tile([P, NH, S], BF16, name="kT")

        def staged(made, name, shape):
            if name not in made:
                made[name] = stage.tile(shape, BF16, align_bytes=64, name=name)
            return made[name]

        def heads_item(loads, made, which, first_head):
            def fill():
                bank = bank_ps.tile([P, 2, S], BF16, tag="bank", name="head_bank")
                for a in range(2):
                    feats = slice((first_head + a) * DH, (first_head + a + 1) * DH)
                    for j in range(S_BLOCKS):
                        nc.tensor.transpose(bank[:, a, j * P : (j + 1) * P], loads[which][:, j, feats], ident_bf[:])
                return bank

            def empty(bank, engine):
                copy_on(engine, made[which + "T"][:, first_head : first_head + 2, :], bank[:])

            return fill, empty

        def x_item(loads, made, g, pair):
            def fill():
                bank = bank_ps.tile([P, 2, PAIR], F32, tag="bank", name="x_bank")
                x_words = loads["x"][:].bitcast(F32)
                flip_words(nc, ident_f32[:], bank, [x_words[:, 2 * pair + a, :] for a in range(2)], g * PAIR)
                return bank

            def empty(bank, engine):
                copy_on(
                    engine,
                    staged(made, "x_grouped", [P, PASSES, S, PACK])[:, g, pair * PAIR : (pair + 1) * PAIR, :].bitcast(F32),
                    bank[:].rearrange("p u c -> p c u"),
                )

            return fill, empty

        def quantise_x(made):
            made["x_codes"] = stage.tile([P, PASSES, S], U32, align_bytes=64, name="x_codes")
            made["x_scales"] = stage.tile([P, PASSES, S], U8, align_bytes=64, name="x_scales")
            nc.vector.quantize_mx(
                out=made["x_codes"][:].rearrange("p g c -> p (g c)").bitcast(FP8X4),
                scales=made["x_scales"][:].rearrange("p g c -> p (g c)"),
                in_=made["x_grouped"][:].rearrange("p g c j -> p (g c j)"),
            )

        def project_item(made, m):
            def fill():
                settle()
                bank = bank_ps.tile([P, S], F32, tag="bank", name="v_bank")
                for g in range(PASSES):
                    nc.tensor.matmul_mx(
                        out=bank[:],
                        lhsT=w_codes[:, m // 2, g, m % 2 * P : (m % 2 + 1) * P].bitcast(FP8X4),
                        lhsT_scale=w_scales[:, m // 2, g, m % 2 * P : (m % 2 + 1) * P],
                        rhs=made["x_codes"][:, g, :].bitcast(FP8X4),
                        rhs_scale=made["x_scales"][:, g, :],
                        start=(g == 0),
                        stop=(g == PASSES - 1),
                    )
                return bank

            def empty(bank, engine):
                vT = staged(made, "vT", [P, E_BLOCKS, S])
                if engine == "scalar":
                    nc.scalar.activation(
                        out=vT[:, m, :], in_=bank[:], func=ACT.Relu, bias=bv_col[:, m : m + 1], scale=1.0
                    )
                else:
                    nc.vector.tensor_scalar(
                        out=vT[:, m, :], in0=bank[:], scalar1=bv_col[:, m : m + 1], scalar2=0.0,
                        op0=ALU.add, op1=ALU.max,
                    )

            return fill, empty

        def v_item(made, pair):
            def fill():
                bank = bank_ps.tile([P, 2, PAIR], F32, tag="bank", name="vk_bank")
                vT_words = made["vT"][:].bitcast(F32)
                flip_words(nc, ident_f32[:], bank, [vT_words[:, 2 * pair + a, :] for a in range(2)], 0)
                return bank

            def empty(bank, engine):
                copy_on(
                    engine,
                    staged(made, "v_grouped", [P, E, PACK])[:, pair * PAIR : (pair + 1) * PAIR, :].bitcast(F32),
                    bank[:].rearrange("p u c -> p c u"),
                )

            return fill, empty

        def quantise_v(made):
            made["v_codes"] = batch.tile([P, E], U32, align_bytes=64, name="v_codes")
            made["v_scales"] = batch.tile([P, E], U8, align_bytes=64, name="v_scales")
            nc.vector.quantize_mx(
                out=made["v_codes"][:].bitcast(FP8X4),
                scales=made["v_scales"][:],
                in_=made["v_grouped"][:].rearrange("p c j -> p (c j)"),
            )

        def w_item(g, grouped, words):
            def fill():
                bank = bank_ps.tile([P, 2, PAIR], F32, tag="bank", name="w_bank")
                flip_words(nc, ident_f32[:], bank, [words[:, a, :] for a in range(2)], g * PAIR)
                return bank

            def empty(bank, engine):
                copy_on(engine, grouped[:, g, :, :].bitcast(F32), bank[:].rearrange("p u c -> p c u"))

            return fill, empty

        made = {}
        allocate(made)
        later_loads, later_pieces = {}, []
        w_tiles = []
        for pair in range(E_BLOCKS // 2):
            w_raw = raw.tile([P, 2, E], BF16, bufs=4)
            nc.sync.dma_start(
                out=w_raw[:], in_=Wv[pair * PAIR : (pair + 1) * PAIR, :].rearrange("(a p) k -> p a k", p=P)
            )
            w_tiles.append(w_raw)
        bv_rows = const.tile([P, P], BF16)
        nc.vector.memset(bv_rows[:], 0.0)
        nc.sync.dma_start(out=bv_rows[0:E_BLOCKS, :], in_=bv.rearrange("(r c) -> r c", c=P))
        nc.sync.dma_start(out=gamma_all[:], in_=gamma.partition_broadcast(P))
        nc.sync.dma_start(out=betta_all[:], in_=betta.partition_broadcast(P))

        def w_items():
            items = []
            for pair in range(E_BLOCKS // 2):
                words = w_tiles[pair][:].bitcast(F32)
                grouped = stage.tile([P, PASSES, PAIR, PACK], BF16, bufs=2, align_bytes=64, name="w_grouped")

                def then(pair=pair, grouped=grouped):
                    nc.vector.quantize_mx(
                        out=w_codes[:, pair, :, :].rearrange("p g c -> p (g c)").bitcast(FP8X4),
                        scales=w_scales[:, pair, :, :].rearrange("p g c -> p (g c)"),
                        in_=grouped[:].rearrange("p g c j -> p (g c j)"),
                    )

                for g in range(PASSES):
                    items.append(w_item(g, grouped, words) + (then if g == PASSES - 1 else None,))
            return items

        def bias_item():
            def fill():
                bank = bank_ps.tile([P, P], BF16, tag="bank", name="bv_bank")
                nc.tensor.transpose(bank[:], bv_rows[:], ident_bf[:])
                return bank

            def empty(bank, engine):
                nc.vector.tensor_copy(out=bv_col[:], in_=bank[:, 0:E_BLOCKS])

            return fill, empty, None

        def preparation(loads, made):
            q_items = [heads_item(loads, made, "q", h) + (None,) for h in range(0, NH, 2)]
            k_items = [heads_item(loads, made, "k", h) + (None,) for h in range(0, NH, 2)]
            x_items = []
            for g in range(PASSES):
                x_items.append(x_item(loads, made, g, 0) + (None,))
                x_items.append(x_item(loads, made, g, 1) + ((lambda: quantise_x(made)) if g == PASSES - 1 else None,))
            p_items = [project_item(made, m) + (None,) for m in range(E_BLOCKS)]
            v_items = [v_item(made, pair) + (None,) for pair in range(E_BLOCKS // 2 - 1)]
            v_items.append(v_item(made, E_BLOCKS // 2 - 1) + (lambda: quantise_v(made),))
            return q_items, k_items, x_items, p_items, v_items

        to_empty = []

        to_settle = []

        def settle():
            while to_settle:
                to_settle.pop(0)()

        def empty_one():
            bank, empty, then, engine = to_empty.pop(0)
            empty(bank, engine)
            if then is not None:
                to_settle.append(then)

        def emit(item, engine):
            if len(to_empty) == 3:
                empty_one()
            fill, empty, then = item
            to_empty.append((fill(), empty, then, engine))

        lift_queries(first_loads, HEAD_HALF[0], nc.vector)
        made["key_sum"] = const.tile([P, S_BLOCKS], F32, name="first_key_sum")
        nc.vector.tensor_reduce(
            out=made["key_sum"][:, 0:2], in_=first_loads["keys"][:, 0:2, :], axis=AXIS.X, op=ALU.add
        )
        for j in range(2, S_BLOCKS):
            summed = stage.tile([P, E], BF16, bufs=2, name="summed")
            nc.scalar.activation(
                out=summed[:], in_=first_loads["keys"][:, j, :], func=ACT.Identity, bias=0.0, scale=1.0,
                accum_out=made["key_sum"][:, j : j + 1],
            )
        sink_padded(first_loads, made, HEAD_HALF[0], nc.vector)
        q_items, k_items, x_items, p_items, v_items = preparation(first_loads, made)
        emit(q_items[0], "scalar")
        emit(k_items[0], "vector")
        emit(scale_item(made), "vector")
        emit(q_items[1], "scalar")
        emit(k_items[1], "scalar")
        empty_one()
        empty_one()
        lift_queries(first_loads, HEAD_HALF[1], nc.vector)
        sink_padded(first_loads, made, HEAD_HALF[1], nc.vector)
        first_items = [q_items[2], k_items[2], q_items[3], k_items[3]] + x_items + w_items() + [bias_item()] + p_items + v_items

        operands = [made]
        heads = N_BLOCKS * NH
        SLOTS = S_BLOCKS * NH
        FIRST_BUSY = 14
        score_of, e_of, flip_of = {}, {}, {}
        block_of = {}

        def block(t):
            g = t // NH
            if g not in block_of:
                b, i = g // S_BLOCKS, g % S_BLOCKS
                block_of[g] = {
                    "b": b, "i": i,
                    "neg_max": small.tile([P, NH], F32, name="neg_max"),
                    "row_sum": small.tile([P, NH], F32, name="row_sum"),
                }
            return block_of[g]

        def load_residual(g):
            d = block(g * NH)
            d["resid"] = rows.tile([P, E], BF16, bufs=5, name="resid")
            nc.sync.dma_start(out=d["resid"][:], in_=queries[d["b"], d["i"] * P : (d["i"] + 1) * P, :])

        def scores(t):
            d, h = block(t), t % NH
            m = operands[d["b"]]
            score_of[t] = score_ps.tile([P, S], F32, name="score")
            if t >= FIRST_BUSY:
                width = S if t < SLOTS // 2 else S // 2
                nc.tensor.matmul_mx(
                    out=score_of[t][:, 0:width],
                    lhsT=w_codes[:, 0, 0, 0:P].bitcast(FP8X4),
                    lhsT_scale=w_scales[:, 0, 0, 0:P],
                    rhs=w_codes[:, 1, :, :].rearrange("p g c -> p (g c)")[:, 0:width].bitcast(FP8X4),
                    rhs_scale=w_scales[:, 1, :, :].rearrange("p g c -> p (g c)")[:, 0:width],
                    start=True,
                    stop=True,
                )
            nc.tensor.matmul(
                out=score_of[t][:], lhsT=m["qT"][:, h, d["i"] * P : (d["i"] + 1) * P], rhs=m["kT"][:, h, :],
                start=True, stop=True,
            )

        def maximum(t):
            d, h = block(t), t % NH
            scaled = work.tile([P, S], F32, name="scaled")
            nc.vector.tensor_scalar(
                out=scaled[:], in0=score_of[t][:], scalar1=operands[d["b"]]["minus_scale"][:, 0:1], scalar2=LARGE, op0=ALU.mult, op1=ALU.min,
                accum_out=d["neg_max"][:, h : h + 1],
            )

        def exponent(t):
            d, h = block(t), t % NH
            if t % 2 == 0:
                e_of[t // 2] = work.tile([P, 2, S], BF16, name="e")
            nc.scalar.activation(
                out=e_of[t // 2][:, t % 2, :], in_=score_of[t][:], func=ACT.Exp,
                bias=d["neg_max"][:, h : h + 1], scale=operands[d["b"]]["scale"][:, 0:1], accum_out=d["row_sum"][:, h : h + 1],
            )

        def flip(pair):
            flip_of[pair] = bank_ps.tile([P, 2, PAIR], F32, tag="bank", name="e_bank")
            e_words = e_of[pair][:].bitcast(F32)
            flip_words(nc, ident_f32[:], flip_of[pair], [e_words[:, a, :] for a in range(2)], 0)

        def group(pair, engine):
            d = block(2 * pair)
            at = pair % (NH // 2)
            if at == 0:
                d["grouped"] = halves.tile([P, NH * P, PACK], BF16, align_bytes=64, name="e_grouped")
            copy_on(
                engine,
                d["grouped"][:, at * PAIR : (at + 1) * PAIR, :].bitcast(F32),
                flip_of[pair][:].rearrange("p u c -> p c u"),
            )

        def quantise_e(g, first, last):
            d = block_of[g]
            if first == 0:
                d["codes"] = halves.tile([P, NH * P], U32, align_bytes=64, name="e_codes")
                d["scales"] = halves.tile([P, NH * P], U8, align_bytes=64, name="e_scales")
            cols = slice(first * P, last * P)
            nc.vector.quantize_mx(
                out=d["codes"][:, cols].bitcast(FP8X4),
                scales=d["scales"][:, cols],
                in_=d["grouped"][:, cols, :].rearrange("p c j -> p (c j)"),
            )

        def invert(g):
            d = block_of[g]
            d["inv_sum"] = small.tile([P, NH], F32, name="inv_sum")
            nc.vector.reciprocal(out=d["inv_sum"][:], in_=d["row_sum"][:])

        def weigh(g, half):
            d = block_of[g]
            m = operands[d["b"]]
            d["att"] = bank_ps.tile([P, HALF_HEADS, DH], F32, tag="bank", name="att")
            for a in range(HALF_HEADS):
                h = half * HALF_HEADS + a
                nc.tensor.matmul_mx(
                    out=d["att"][:, a, :],
                    lhsT=d["codes"][:, h * P : (h + 1) * P].bitcast(FP8X4),
                    lhsT_scale=d["scales"][:, h * P : (h + 1) * P],
                    rhs=m["v_codes"][:, h * DH : (h + 1) * DH].bitcast(FP8X4),
                    rhs_scale=m["v_scales"][:, h * DH : (h + 1) * DH],
                    start=True,
                    stop=True,
                )

        def add_residual(g, half):
            d = block_of[g]
            if half == 0:
                d["y"] = rows.tile([P, E], F32, bufs=4, name="y")
                d["stats"] = small.tile([P, 2, 6], F32, name="stats")
            inv_sum = d["inv_sum"]
            for a in range(HALF_HEADS):
                h = half * HALF_HEADS + a
                feats = slice(h * DH, (h + 1) * DH)
                nc.vector.scalar_tensor_tensor(
                    out=d["y"][:, feats], in0=d["att"][:, a, :], scalar=inv_sum[:, h : h + 1],
                    in1=d["resid"][:, feats], op0=ALU.mult, op1=ALU.add,
                )

        def statistics(g, half):
            d = block_of[g]
            cols = slice(half * HALF_HEADS * DH, (half + 1) * HALF_HEADS * DH)
            nc.vector.bn_stats(out=d["stats"][:, half, :], in_=d["y"][:, cols])

        def norm(g):
            d = block_of[g]
            moments = small.tile([P, 2], F32, name="moments")
            nc.vector.bn_aggr(out=moments[:], in_=d["stats"][:])
            d["moments"] = moments
            if g >= N_BLOCKS - V_BLOCKS:
                return
            d["root"] = small.tile([P, 1], F32, name="root")
            nc.gpsimd.tensor_tensor(out=d["root"][:], in0=moments[:, 1:2], in1=one_half[:], op=ALU.pow)

        def scale_rows(g):
            d = block_of[g]
            y = d["y"]
            sd_eps = small.tile([P, 1], F32, name="sd_eps")
            nc.vector.tensor_scalar(
                out=sd_eps[:], in0=d["root"][:], scalar1=(E / (E - 1.0)) ** 0.5, scalar2=EPS, op0=ALU.mult, op1=ALU.add
            )
            neg_mean = small.tile([P, 1], F32, name="neg_mean")
            nc.vector.tensor_scalar(out=neg_mean[:], in0=d["moments"][:, 0:1], scalar1=-1.0, scalar2=None, op0=ALU.mult)
            inv_sd = small.tile([P, 1], F32, name="inv_sd")
            nc.vector.reciprocal(out=inv_sd[:], in_=sd_eps[:])
            pieces = [slice(first, first + GP_COLS) for first in range(0, E, GP_COLS)]
            for cols in pieces:
                nc.gpsimd.tensor_scalar(
                    out=y[:, cols], in0=y[:, cols], scalar1=neg_mean[:, 0:1], scalar2=inv_sd[:, 0:1],
                    op0=ALU.add, op1=ALU.mult,
                )
            for cols in pieces:
                nc.gpsimd.tensor_tensor(out=y[:, cols], in0=y[:, cols], in1=gamma_all[:, cols], op=ALU.mult)
            for cols in pieces:
                nc.gpsimd.tensor_tensor(out=y[:, cols], in0=y[:, cols], in1=betta_all[:, cols], op=ALU.add)

        def root(g):
            d = block_of[g]
            d["sd"] = small.tile([P, 1], F32, name="sd")
            nc.scalar.activation(
                out=d["sd"][:], in_=d["moments"][:, 1:2], func=ACT.Sqrt, bias=0.0, scale=E / (E - 1.0)
            )

        def norm_on_vector(g):
            d = block_of[g]
            y = d["y"]
            sd_eps = small.tile([P, 1], F32, name="sd_eps")
            nc.vector.tensor_scalar(out=sd_eps[:], in0=d["sd"][:], scalar1=EPS, scalar2=None, op0=ALU.add)
            halves_of = [slice(half * (E // 2), (half + 1) * (E // 2)) for half in range(2)]
            for cols in halves_of:
                nc.vector.scalar_tensor_tensor(
                    out=y[:, cols], in0=y[:, cols], scalar=d["moments"][:, 0:1], in1=gamma_all[:, cols],
                    op0=ALU.subtract, op1=ALU.mult,
                )
            d["inv_sd"] = small.tile([P, 1], F32, name="inv_sd")
            nc.vector.reciprocal(out=d["inv_sd"][:], in_=sd_eps[:])
            for cols in halves_of:
                nc.vector.scalar_tensor_tensor(
                    out=y[:, cols], in0=y[:, cols], scalar=d["inv_sd"][:, 0:1], in1=betta_all[:, cols],
                    op0=ALU.mult, op1=ALU.add,
                )
                nc.sync.dma_start(out=out[d["b"], d["i"] * P : (d["i"] + 1) * P, cols], in_=y[:, cols])

        def store(g):
            d = block_of[g]
            nc.sync.dma_start(out=out[d["b"], d["i"] * P : (d["i"] + 1) * P, :], in_=d["y"][:])

        def engine_of(n):
            if n < n_first:
                return "vector" if n % 2 else "scalar"
            return "vector" if (n - n_first) % n_batch in ON_VECTOR else "scalar"

        n_batch = 2 * NH + E_BLOCKS + 1

        def prepared(slot, first):
            if slot < first + 2:
                return max(0, 2 * (slot - first + 1))
            return 4 + (slot - first - 1) * (n_batch - 4) // (SLOTS - 3 - first)

        stages = {}
        for g in range(N_BLOCKS):
            plan = [(11, quantise_e, (g, 0, NH))]
            if g == N_BLOCKS - 1:
                plan = [(11, quantise_e, (g, 0, HALF_HEADS)), (11, quantise_e, (g, HALF_HEADS, NH))]
            plan.append((11, invert, (g,)))
            for half in range(2):
                first = 13 + 2 * half
                plan += [(first, weigh, (g, half)), (first + 1, add_residual, (g, half)), (first + 2, statistics, (g, half))]
            plan.append((18, norm, (g,)))
            if 1 <= g <= N_BLOCKS - V_BLOCKS:
                plan.append((11, scale_rows, (g - 1,)))
            if g < N_BLOCKS - V_BLOCKS:
                plan.append((31, store, (g,)))
            else:
                plan.append(((N_BLOCKS - 1 - g) * NH + 18, root, (g,)))
                plan.append(((N_BLOCKS - 1 - g) * NH + 19, norm_on_vector, (g,)))
            for after, stage_of, of in plan:
                stages.setdefault(g * NH + after, []).append((stage_of, of))
        ON_VECTOR = (4, 6, 21, 23)
        LOAD_SLOTS = {6: "keys", 10: "x", 18: "q", 28: "k"}
        GP_QUIET = 3
        loads = {}
        items, emitted = first_items, 0
        n_first = len(first_items)
        for t in range(-3, heads + 3 * NH):
            inside = 0 <= t < heads
            b, local = max(t, 0) // SLOTS, t % NH
            slot = t - b * SLOTS
            if inside and slot == 0 and b + 1 < B:
                nxt = {}
                operands.append(nxt)
                loads, pieces, later_loads = later_loads, later_pieces, {}
            if t == 2:
                for which in ("x", "q", "keys", "k"):
                    load(loads, which, 1)
            if inside and b + 2 < B and slot in LOAD_SLOTS:
                load(later_loads, LOAD_SLOTS[slot], b + 2)
            if inside and b + 1 < B:
                if slot == (8 if b == 0 else 0):
                    allocate(nxt)
                    if b == 0:
                        lift_queries(loads)
                    q_items, k_items, x_items, p_items, v_items = preparation(loads, nxt)
                    items = items + x_items + q_items + p_items + v_items + [scale_item(nxt)] + k_items
            mask_slot = 19
            free_ports = local == GP_QUIET or t < 12
            if t == -3:
                load_residual(0)
                load_residual(1)
            if inside and local == 0 and t // NH + 2 < N_BLOCKS:
                load_residual(t // NH + 2)

            if t + 3 < heads:
                scores(t + 3)
            if 0 <= t + 2 < heads:
                maximum(t + 2)
            if free_ports:
                settle()
                if inside and slot == mask_slot and b + 1 < B:
                    add_keys(nxt, pieces[-1][3])
                    sink_padded(loads, nxt)
                if inside and slot == 27 and b + 2 < B:
                    lift_queries(later_loads)
            if inside:
                exponent(t)
            if t % 2 == 0 and 2 <= t <= heads:
                flip(t // 2 - 1)
            if t % 2 == 1 and 3 <= t <= heads + 1:
                group(t // 2 - 1, "scalar")
            while to_empty:
                empty_one()
            for stage_of, of in stages.get(t, []):
                stage_of(*of)
            if inside and b + 1 < B:
                if b == 0 and slot == 12:
                    pieces = fold_pieces(loads)
                    await_vector(t + 2)
                    fold(pieces[:2])
                if slot == (12 if b == 0 else 5):
                    fold(pieces[2:])
            if inside and b + 2 < B and slot in (13, 21):
                if slot == 13:
                    later_pieces = fold_pieces(later_loads)
                fold(later_pieces[{13: slice(0, 1), 21: slice(1, 2)}[slot]])
            if -2 <= t < heads:
                due = 0
                if b == 0:
                    due = min(3 * (slot + 3), n_first) + prepared(slot, 8)
                elif b + 1 < B:
                    due = n_first + b * n_batch + prepared(slot, 0)
                while emitted < due and items:
                    emit(items.pop(0), engine_of(emitted))
                    emitted += 1
